import numpy as np
import ml_dtypes


def mxq(x, axis, fmt="e4m3"):
    dtype, down = {"e4m3": (ml_dtypes.float8_e4m3fn, 7), "e5m2": (ml_dtypes.float8_e5m2, 14)}[fmt]
    v = np.moveaxis(np.asarray(x, np.float32).astype(ml_dtypes.bfloat16).astype(np.float64), axis, -1)
    blocks = v.reshape(v.shape[:-1] + (-1, 32))
    amax = np.abs(blocks).max(-1, keepdims=True)
    byte = np.maximum(np.where(amax > 0, np.frexp(amax)[1] - 1 + 127, 0) - down, 1)
    scale = np.exp2(byte - 127.0)
    codes = (blocks / scale).astype(np.float32).astype(dtype).astype(np.float64)
    return np.moveaxis((codes * scale).reshape(v.shape), -1, axis)


WIDE = False


def mx_kscale(k):
    if not WIDE:
        return np.ones(k)
    levels = np.array([10, -10, 5, -5, 0])
    a = np.random.permutation(np.resize(levels, k // 512 * 4)).reshape(k // 512, 4)
    idx = np.arange(k)
    return np.exp2(a[idx // 512, idx % 128 // 32])


BF16 = ml_dtypes.bfloat16


def bf(x):
    return np.asarray(x, np.float32).astype(BF16)


def f64(x):
    return np.asarray(x).astype(np.float64)


B, S, D, H, HD = 1, 1024, 1024, 8, 128
E = H * HD


def setup_inputs():
    t = mx_kscale(E)
    ind_q = np.random.uniform(size=(B, S)) > 0.2
    ind_k = np.random.uniform(size=(B, S)) > 0.2
    ind_v = np.random.uniform(size=(B, S)) > 0.2
    q = np.random.standard_normal((B, H, S, HD)) * 1.75 * ind_q[:, None, :, None]
    k = np.random.standard_normal((B, H, S, HD)) * 1.75 * ind_k[:, None, :, None]
    v = np.random.standard_normal((B, H, S, HD)) + 0.5 * np.random.standard_normal((1, H, 1, HD))
    return {"q_masked": bf(q), "k_masked": bf(k), "v_proj": bf(v * t.reshape(H, 1, HD)),
            "ind_k": bf(ind_k), "ind_v": bf(ind_v),
            "Wo": bf(np.random.standard_normal((E, D)) / np.sqrt(E) / t[:, None])}


def reference(q_masked, k_masked, v_proj, ind_k, ind_v, Wo):
    v = f64(v_proj) * f64(ind_v)[:, None, :, None]
    s = f64(q_masked) @ f64(k_masked).transpose(0, 1, 3, 2) / np.sqrt(HD)
    e = np.exp(s - s.max(-1, keepdims=True))
    attn = e / e.sum(-1, keepdims=True)
    attn = attn * f64(ind_k)[:, None, None, :]
    denom = attn.sum(-1, keepdims=True)
    attn = attn / np.where(denom == 0.0, 1.0, denom)
    o = mxq(attn, 3, "e4m3") @ mxq(v, 2, "e4m3")
    c = o.transpose(0, 2, 1, 3).reshape(B, S, E)
    return mxq(c, 2, "e4m3") @ mxq(f64(Wo), 0, "e4m3")

@@ -1,0 +1,340 @@
+import math
+from contextlib import ExitStack
+
+import concourse.mybir as mybir
+from concourse.masks import make_identity
+
+BF16 = mybir.dt.bfloat16
+F32 = mybir.dt.float32
+U32 = mybir.dt.uint32
+U8 = mybir.dt.uint8
+FP8X4 = mybir.dt.float8_e4m3fn_x4
+ALU = mybir.AluOpType
+ACT = mybir.ActivationFunctionType
+
+P = 128
+PACK = 4
+K_PASS = P * PACK
+BANK = 512
+
+HEADS = 8
+SEQ = 1024
+HEAD_DIM = 128
+D_OUT = 1024
+KEY_PASSES = SEQ // K_PASS
+FEATURE_PASSES = HEADS * HEAD_DIM // K_PASS
+HEADS_PER_PASS = K_PASS // HEAD_DIM
+
+Q_HALF = 512
+Q_HALVES = SEQ // Q_HALF
+TILES = Q_HALF // P
+
+SCALE = 1.0 / math.sqrt(HEAD_DIM)
+MASKED_SCORE = -1.0e30
+
+FLOPS = 3 * 2 * SEQ * SEQ * HEADS * HEAD_DIM
+
+
+def tile_scaleddotproductattention_pa_kernel(
+    tc, q_masked, k_masked, v_proj, ind_k, ind_v, Wo, out
+):
+    nc = tc.nc
+    with ExitStack() as stack:
+        const = stack.enter_context(tc.tile_pool(name="const", bufs=1))
+        keep = stack.enter_context(tc.tile_pool(name="keep", bufs=1))
+        raw = stack.enter_context(tc.tile_pool(name="raw", bufs=2))
+        work = stack.enter_context(tc.tile_pool(name="work", bufs=2))
+        stats = stack.enter_context(tc.tile_pool(name="stats", bufs=6))
+        score_psum = stack.enter_context(tc.psum_pool(name="score_psum", bufs=2))
+        flip_psum = stack.enter_context(tc.psum_pool(name="flip_psum", bufs=2))
+        acc_psum = stack.enter_context(tc.psum_pool(name="acc_psum", bufs=2))
+        stack.enter_context(tc.manual_schedule())
+
+        q_t = keep.tile([P, HEADS, SEQ], BF16)
+        k_t = keep.tile([P, HEADS, SEQ], BF16)
+        v_codes = keep.tile([P, HEADS, KEY_PASSES * HEAD_DIM], U32, align_bytes=64)
+        v_scales = keep.tile([P, HEADS, KEY_PASSES * HEAD_DIM], U8, align_bytes=64)
+        wo_codes = keep.tile([P, FEATURE_PASSES, D_OUT], U32, align_bytes=64)
+        wo_scales = keep.tile([P, FEATURE_PASSES, D_OUT], U8, align_bytes=64)
+
+        raw_of_head = {}
+        wo_raw_of_pass = {}
+
+        def load_head(h):
+            k_raw = raw.tile([P, SEQ // P, HEAD_DIM], BF16)
+            nc.sync.dma_start(out=k_raw[:], in_=k_masked[0, h].rearrange("(t p) d -> p t d", p=P))
+            q_raw = raw.tile([P, SEQ // P, HEAD_DIM], BF16)
+            nc.sync.dma_start(out=q_raw[:], in_=q_masked[0, h].rearrange("(t p) d -> p t d", p=P))
+            v_raw = raw.tile([P, 2 * KEY_PASSES, 2 * HEAD_DIM], BF16)
+            nc.sync.dma_start(
+                out=v_raw[:], in_=v_proj[0, h].rearrange("(c p e) d -> p c (e d)", p=P, e=2)
+            )
+            raw_of_head[h] = (k_raw, q_raw, v_raw)
+
+        def load_wo(g):
+            wo_raw = raw.tile([P, PACK, D_OUT], BF16)
+            rows = Wo[g * K_PASS : (g + 1) * K_PASS, :]
+            nc.sync.dma_start(out=wo_raw[:], in_=rows.rearrange("(t p) n -> p t n", p=P))
+            wo_raw_of_pass[g] = wo_raw
+
+        load_head(0)
+        load_head(1)
+
+        ident_bf16 = const.tile([P, P], BF16)
+        make_identity(nc, ident_bf16[:])
+        ident_f32 = const.tile([P, P], F32)
+        make_identity(nc, ident_f32[:])
+
+        ind_k_rows = const.tile([P, SEQ], BF16)
+        nc.scalar.dma_start(out=ind_k_rows[:], in_=ind_k[0].partition_broadcast(P))
+        mask_bias = const.tile([P, SEQ], BF16)
+        nc.vector.tensor_scalar(
+            out=mask_bias[:],
+            in0=ind_k_rows[:],
+            scalar1=-1.0,
+            scalar2=-MASKED_SCORE,
+            op0=ALU.add,
+            op1=ALU.mult,
+        )
+        any_valid = const.tile([P, 1], F32)
+        nc.vector.reduce_max(out=any_valid[:], in_=ind_k_rows[:], axis=mybir.AxisListType.X)
+        ind_v_words = const.tile([P, 2 * KEY_PASSES, 2], BF16)
+        nc.scalar.dma_start(out=ind_v_words[:], in_=ind_v[0].rearrange("(c p e) -> p c e", p=P, e=2))
+
+        def transpose_quarter(h, quarter):
+            k_raw, q_raw, v_raw = raw_of_head[h]
+            source = k_raw if quarter < 2 else q_raw
+            target = k_t if quarter < 2 else q_t
+            first = (quarter % 2) * 4
+            flipped = flip_psum.tile([P, 4, P], BF16, tag="flipped")
+            for i in range(4):
+                nc.tensor.transpose(flipped[:, i, :], source[:, first + i, :], ident_bf16[:])
+            nc.scalar.copy(
+                out=target[:, h, first * P : (first + 4) * P],
+                in_=flipped[:].rearrange("p i s -> p (i s)"),
+            )
+
+        v_grouped_of_head = {}
+
+        def mask_and_group_v(h):
+            k_raw, q_raw, v_raw = raw_of_head[h]
+            v_grouped = work.tile([P, KEY_PASSES * HEAD_DIM * PACK], BF16, align_bytes=64)
+            nc.gpsimd.tensor_tensor(
+                out=v_grouped[:].rearrange("p (g d t) -> p g d t", g=KEY_PASSES, t=PACK),
+                in0=v_raw[:].rearrange("p (g u) (e d) -> p g d (u e)", u=2, e=2),
+                in1=ind_v_words[:]
+                .rearrange("p (g u) e -> p g (u e)", u=2)
+                .unsqueeze(2)
+                .to_broadcast([P, KEY_PASSES, HEAD_DIM, PACK]),
+                op=ALU.mult,
+            )
+            v_grouped_of_head[h] = v_grouped
+
+        def quantise_v(h):
+            nc.vector.quantize_mx(
+                out=v_codes[:, h, :].bitcast(FP8X4),
+                scales=v_scales[:, h, :],
+                in_=v_grouped_of_head[h][:],
+            )
+
+        WO_QUARTER = D_OUT // 4
+        wo_grouped_of_quarter = {}
+
+        def group_wo(g, quarter):
+            cols = slice(quarter * WO_QUARTER, (quarter + 1) * WO_QUARTER)
+            wo_grouped = work.tile([P, WO_QUARTER * PACK], BF16, align_bytes=64)
+            nc.gpsimd.tensor_scalar(
+                out=wo_grouped[:].rearrange("p (n t) -> p n t", t=PACK),
+                in0=wo_raw_of_pass[g][:, :, cols].rearrange("p t n -> p n t"),
+                scalar1=1.0,
+                scalar2=0.0,
+                op0=ALU.mult,
+                op1=ALU.add,
+            )
+            wo_grouped_of_quarter[(g, quarter)] = wo_grouped
+
+        def quantise_wo(g, quarter):
+            cols = slice(quarter * WO_QUARTER, (quarter + 1) * WO_QUARTER)
+            nc.vector.quantize_mx(
+                out=wo_codes[:, g, cols].bitcast(FP8X4),
+                scales=wo_scales[:, g, cols],
+                in_=wo_grouped_of_quarter[(g, quarter)][:],
+            )
+
+        scores_of = {}
+        weights_of = {}
+        row_sum_of = {}
+        a_bf16_of = {}
+        a_grouped_of = {}
+        c_heads_of = {}
+        c_mx_of = {}
+
+        def scores(qh, h, j):
+            queries = slice(qh * Q_HALF + j * P, qh * Q_HALF + (j + 1) * P)
+            score_lo = score_psum.tile([P, BANK], F32)
+            nc.tensor.matmul(score_lo[:], lhsT=q_t[:, h, queries], rhs=k_t[:, h, 0:BANK], start=True, stop=True)
+            score_hi = score_psum.tile([P, BANK], F32)
+            nc.tensor.matmul(score_hi[:], lhsT=q_t[:, h, queries], rhs=k_t[:, h, BANK:SEQ], start=True, stop=True)
+            scores_of[(qh, h, j)] = (score_lo, score_hi)
+
+        def exponentials(qh, h, j):
+            score_lo, score_hi = scores_of[(qh, h, j)]
+            weights = work.tile([P, SEQ], F32, bufs=4)
+            for score, keys in ((score_lo, slice(0, BANK)), (score_hi, slice(BANK, SEQ))):
+                nc.vector.scalar_tensor_tensor(
+                    out=weights[:, keys], in0=score[:], scalar=SCALE, in1=mask_bias[:, keys], op0=ALU.mult, op1=ALU.add
+                )
+            neg_max = stats.tile([P, 1], F32)
+            nc.vector.tensor_reduce(
+                out=neg_max[:], in_=weights[:], axis=mybir.AxisListType.X, op=ALU.max, negate=True
+            )
+            row_sum = stats.tile([P, 1], F32)
+            nc.scalar.activation(
+                out=weights[:], in_=weights[:], func=ACT.Exp, bias=neg_max[:], scale=1.0, accum_out=row_sum[:]
+            )
+            weights_of[(qh, h, j)] = weights
+            row_sum_of[(qh, h, j)] = row_sum
+
+        def normalise(qh, h, j):
+            weights = weights_of[(qh, h, j)]
+            inv_sum = stats.tile([P, 1], F32)
+            nc.vector.reciprocal(out=inv_sum[:], in_=row_sum_of[(qh, h, j)][:])
+            a_bf16 = work.tile([P, SEQ], BF16, bufs=3)
+            nc.gpsimd.tensor_scalar(
+                out=a_bf16[:], in0=weights[:], scalar1=inv_sum[:], scalar2=any_valid[:], op0=ALU.mult, op1=ALU.mult
+            )
+            a_bf16_of[(qh, h, j)] = a_bf16
+
+        def keys_to_partitions(qh, h, j):
+            a_words = a_bf16_of[(qh, h, j)][:].bitcast(F32)
+            flipped = flip_psum.tile([P, 2 * KEY_PASSES, P], F32, tag="flipped")
+            for c in range(2 * KEY_PASSES):
+                nc.tensor.transpose(flipped[:, c, :], a_words[:, c * P : (c + 1) * P], ident_f32[:])
+            if j == 0:
+                a_grouped = work.tile([P, KEY_PASSES * Q_HALF * PACK], BF16, align_bytes=64)
+                a_grouped_of[(qh, h)] = a_grouped
+            grouped_words = a_grouped_of[(qh, h)][:].bitcast(F32).rearrange("p (g q u) -> p g q u", g=KEY_PASSES, u=2)
+            nc.scalar.copy(
+                out=grouped_words[:, :, j * P : (j + 1) * P, :],
+                in_=flipped[:].rearrange("p (g u) q -> p g q u", u=2),
+            )
+
+        def weighted_values(qh, h):
+            a_grouped = a_grouped_of[(qh, h)]
+            a_codes = work.tile([P, KEY_PASSES, Q_HALF], U32, align_bytes=64)
+            a_scales = work.tile([P, KEY_PASSES, Q_HALF], U8, align_bytes=64)
+            width = Q_HALF * PACK
+            for g in range(KEY_PASSES):
+                nc.vector.quantize_mx(
+                    out=a_codes[:, g, :].bitcast(FP8X4),
+                    scales=a_scales[:, g, :],
+                    in_=a_grouped[:, g * width : (g + 1) * width],
+                )
+            o_t = acc_psum.tile([P, Q_HALF], F32, tag="acc")
+            for g in range(KEY_PASSES):
+                features = slice(g * HEAD_DIM, (g + 1) * HEAD_DIM)
+                nc.tensor.matmul_mx(
+                    out=o_t[:],
+                    lhsT=v_codes[:, h, features].bitcast(FP8X4),
+                    lhsT_scale=v_scales[:, h, features],
+                    rhs=a_codes[:, g, :].bitcast(FP8X4),
+                    rhs_scale=a_scales[:, g, :],
+                    start=(g == 0),
+                    stop=(g == KEY_PASSES - 1),
+                )
+            if h == 0:
+                c_heads = work.tile([P, HEADS, Q_HALF], BF16)
+                c_heads_of[qh] = c_heads
+            nc.scalar.copy(out=c_heads_of[qh][:, h, :], in_=o_t[:])
+
+        def quantise_heads(qh, g):
+            if g == 0:
+                c_grouped = work.tile([P, FEATURE_PASSES, Q_HALF * PACK], BF16, align_bytes=64)
+                c_codes = work.tile([P, FEATURE_PASSES, Q_HALF], U32, align_bytes=64)
+                c_scales = work.tile([P, FEATURE_PASSES, Q_HALF], U8, align_bytes=64)
+                c_mx_of[qh] = (c_grouped, c_codes, c_scales)
+            c_grouped, c_codes, c_scales = c_mx_of[qh]
+            four_heads = c_heads_of[qh][:, g * HEADS_PER_PASS : (g + 1) * HEADS_PER_PASS, :]
+            nc.vector.tensor_copy(
+                out=c_grouped[:, g, :].rearrange("p (q t) -> p q t", t=PACK),
+                in_=four_heads.rearrange("p t q -> p q t"),
+            )
+            nc.vector.quantize_mx(
+                out=c_codes[:, g, :].bitcast(FP8X4), scales=c_scales[:, g, :], in_=c_grouped[:, g, :]
+            )
+
+        def project(qh, j):
+            c_grouped, c_codes, c_scales = c_mx_of[qh]
+            queries = slice(j * P, (j + 1) * P)
+            result = work.tile([P, D_OUT], F32, bufs=3)
+            for half in range(D_OUT // BANK):
+                cols = slice(half * BANK, (half + 1) * BANK)
+                acc = acc_psum.tile([P, BANK], F32, tag="acc")
+                for g in range(FEATURE_PASSES):
+                    nc.tensor.matmul_mx(
+                        out=acc[:],
+                        lhsT=c_codes[:, g, queries].bitcast(FP8X4),
+                        lhsT_scale=c_scales[:, g, queries],
+                        rhs=wo_codes[:, g, cols].bitcast(FP8X4),
+                        rhs_scale=wo_scales[:, g, cols],
+                        start=(g == 0),
+                        stop=(g == FEATURE_PASSES - 1),
+                    )
+                if half == 0:
+                    nc.scalar.copy(out=result[:, cols], in_=acc[:])
+                else:
+                    nc.vector.tensor_copy(out=result[:, cols], in_=acc[:])
+            rows = slice(qh * Q_HALF + j * P, qh * Q_HALF + (j + 1) * P)
+            nc.sync.dma_start(out=out[0, rows, :], in_=result[:])
+
+        mask_and_group_v(0)
+        for quarter in range(4):
+            transpose_quarter(0, quarter)
+        quantise_v(0)
+
+        tiles = [(qh, h, j) for qh in range(Q_HALVES) for h in range(HEADS) for j in range(TILES)]
+        PROJECT_LAG = 6 + TILES - 1
+
+        def entered(step, lag):
+            return tiles[step - lag] if 0 <= step - lag < len(tiles) else None
+
+        for step in range(len(tiles) + PROJECT_LAG + 1):
+            if entered(step, 0):
+                scores(*entered(step, 0))
+            if entered(step, 1):
+                exponentials(*entered(step, 1))
+            if entered(step, 2):
+                normalise(*entered(step, 2))
+            if entered(step, 3):
+                keys_to_partitions(*entered(step, 3))
+            if entered(step, 4):
+                qh, h, j = entered(step, 4)
+                if j == TILES - 1:
+                    weighted_values(qh, h)
+            if entered(step, 5):
+                qh, h, j = entered(step, 5)
+                if j == TILES - 1 and h % HEADS_PER_PASS == HEADS_PER_PASS - 1:
+                    quantise_heads(qh, h // HEADS_PER_PASS)
+            if entered(step, PROJECT_LAG):
+                qh, h, j = entered(step, PROJECT_LAG)
+                if h == HEADS - 1:
+                    project(qh, j)
+
+            if entered(step, 0) and entered(step, 0)[0] == 0:
+                qh, h, j = entered(step, 0)
+                if j == 0 and h + 2 < HEADS:
+                    load_head(h + 2)
+                if j == 0 and HEADS - 4 <= h < HEADS - 4 + FEATURE_PASSES:
+                    load_wo(h - (HEADS - 4))
+                if h + 1 < HEADS:
+                    transpose_quarter(h + 1, j)
+                    if j == 0:
+                        mask_and_group_v(h + 1)
+                if h >= HEADS - FEATURE_PASSES:
+                    group_wo(h - (HEADS - FEATURE_PASSES), j)
+            if entered(step, 2) and entered(step, 2)[0] == 0:
+                qh, h, j = entered(step, 2)
+                if h + 1 < HEADS and j == 0:
+                    quantise_v(h + 1)
+                if h >= HEADS - FEATURE_PASSES:
+                    quantise_wo(h - (HEADS - FEATURE_PASSES), j)

@@ -44,7 +44,7 @@ def tile_scaleddotproductattention_pa_kernel(
         keep = stack.enter_context(tc.tile_pool(name="keep", bufs=1))
         raw = stack.enter_context(tc.tile_pool(name="raw", bufs=2))
         work = stack.enter_context(tc.tile_pool(name="work", bufs=2))
-        stats = stack.enter_context(tc.tile_pool(name="stats", bufs=6))
+        stats = stack.enter_context(tc.tile_pool(name="stats", bufs=8))
         score_psum = stack.enter_context(tc.psum_pool(name="score_psum", bufs=2))
         flip_psum = stack.enter_context(tc.psum_pool(name="flip_psum", bufs=2))
         acc_psum = stack.enter_context(tc.psum_pool(name="acc_psum", bufs=2))
@@ -57,19 +57,25 @@ def tile_scaleddotproductattention_pa_kernel(
         wo_codes = keep.tile([P, FEATURE_PASSES, D_OUT], U32, align_bytes=64)
         wo_scales = keep.tile([P, FEATURE_PASSES, D_OUT], U8, align_bytes=64)
 
-        raw_of_head = {}
+        q_raw_of = {}
+        k_raw_of = {}
+        v_raw_of = {}
         wo_raw_of_pass = {}
 
-        def load_head(h):
-            k_raw = raw.tile([P, SEQ // P, HEAD_DIM], BF16)
-            nc.sync.dma_start(out=k_raw[:], in_=k_masked[0, h].rearrange("(t p) d -> p t d", p=P))
-            q_raw = raw.tile([P, SEQ // P, HEAD_DIM], BF16)
-            nc.sync.dma_start(out=q_raw[:], in_=q_masked[0, h].rearrange("(t p) d -> p t d", p=P))
-            v_raw = raw.tile([P, 2 * KEY_PASSES, 2 * HEAD_DIM], BF16)
-            nc.sync.dma_start(
-                out=v_raw[:], in_=v_proj[0, h].rearrange("(c p e) d -> p c (e d)", p=P, e=2)
-            )
-            raw_of_head[h] = (k_raw, q_raw, v_raw)
+        def load(qh, h):
+            q_raw = raw.tile([P, TILES, HEAD_DIM], BF16)
+            queries = q_masked[0, h, qh * Q_HALF : (qh + 1) * Q_HALF, :]
+            nc.sync.dma_start(out=q_raw[:], in_=queries.rearrange("(t p) d -> p t d", p=P))
+            q_raw_of[(qh, h)] = q_raw
+            if qh == 0:
+                k_raw = raw.tile([P, SEQ // P, HEAD_DIM], BF16)
+                nc.sync.dma_start(out=k_raw[:], in_=k_masked[0, h].rearrange("(t p) d -> p t d", p=P))
+                k_raw_of[h] = k_raw
+                v_raw = raw.tile([P, 2 * KEY_PASSES, 2 * HEAD_DIM], BF16)
+                nc.sync.dma_start(
+                    out=v_raw[:], in_=v_proj[0, h].rearrange("(c p e) d -> p c (e d)", p=P, e=2)
+                )
+                v_raw_of[h] = v_raw
 
         def load_wo(g):
             wo_raw = raw.tile([P, PACK, D_OUT], BF16)
@@ -77,8 +83,9 @@ def tile_scaleddotproductattention_pa_kernel(
             nc.sync.dma_start(out=wo_raw[:], in_=rows.rearrange("(t p) n -> p t n", p=P))
             wo_raw_of_pass[g] = wo_raw
 
-        load_head(0)
-        load_head(1)
+        half_heads = [(qh, h) for qh in range(Q_HALVES) for h in range(HEADS)]
+        load(*half_heads[0])
+        load(*half_heads[1])
 
         ident_bf16 = const.tile([P, P], BF16)
         make_identity(nc, ident_bf16[:])
@@ -101,23 +108,22 @@ def tile_scaleddotproductattention_pa_kernel(
         ind_v_words = const.tile([P, 2 * KEY_PASSES, 2], BF16)
         nc.scalar.dma_start(out=ind_v_words[:], in_=ind_v[0].rearrange("(c p e) -> p c e", p=P, e=2))
 
-        def transpose_quarter(h, quarter):
-            k_raw, q_raw, v_raw = raw_of_head[h]
-            source = k_raw if quarter < 2 else q_raw
-            target = k_t if quarter < 2 else q_t
-            first = (quarter % 2) * 4
+        def features_to_partitions(four_row_tiles, columns):
             flipped = flip_psum.tile([P, 4, P], BF16, tag="flipped")
             for i in range(4):
-                nc.tensor.transpose(flipped[:, i, :], source[:, first + i, :], ident_bf16[:])
-            nc.scalar.copy(
-                out=target[:, h, first * P : (first + 4) * P],
-                in_=flipped[:].rearrange("p i s -> p (i s)"),
-            )
+                nc.tensor.transpose(flipped[:, i, :], four_row_tiles[:, i, :], ident_bf16[:])
+            nc.scalar.copy(out=columns, in_=flipped[:].rearrange("p i s -> p (i s)"))
+
+        def transpose_q(qh, h):
+            features_to_partitions(q_raw_of[(qh, h)], q_t[:, h, qh * Q_HALF : (qh + 1) * Q_HALF])
+
+        def transpose_k(h, half):
+            features_to_partitions(k_raw_of[h][:, half * 4 : (half + 1) * 4, :], k_t[:, h, half * BANK : (half + 1) * BANK])
 
         v_grouped_of_head = {}
 
         def mask_and_group_v(h):
-            k_raw, q_raw, v_raw = raw_of_head[h]
+            v_raw = v_raw_of[h]
             v_grouped = work.tile([P, KEY_PASSES * HEAD_DIM * PACK], BF16, align_bytes=64)
             nc.gpsimd.tensor_tensor(
                 out=v_grouped[:].rearrange("p (g d t) -> p g d t", g=KEY_PASSES, t=PACK),
@@ -177,13 +183,17 @@ def tile_scaleddotproductattention_pa_kernel(
             nc.tensor.matmul(score_hi[:], lhsT=q_t[:, h, queries], rhs=k_t[:, h, BANK:SEQ], start=True, stop=True)
             scores_of[(qh, h, j)] = (score_lo, score_hi)
 
-        def exponentials(qh, h, j):
+        def mask(qh, h, j):
             score_lo, score_hi = scores_of[(qh, h, j)]
-            weights = work.tile([P, SEQ], F32, bufs=4)
+            weights = work.tile([P, SEQ], F32, bufs=6)
             for score, keys in ((score_lo, slice(0, BANK)), (score_hi, slice(BANK, SEQ))):
                 nc.vector.scalar_tensor_tensor(
                     out=weights[:, keys], in0=score[:], scalar=SCALE, in1=mask_bias[:, keys], op0=ALU.mult, op1=ALU.add
                 )
+            weights_of[(qh, h, j)] = weights
+
+        def exponentials(qh, h, j):
+            weights = weights_of[(qh, h, j)]
             neg_max = stats.tile([P, 1], F32)
             nc.vector.tensor_reduce(
                 out=neg_max[:], in_=weights[:], axis=mybir.AxisListType.X, op=ALU.max, negate=True
@@ -192,14 +202,13 @@ def tile_scaleddotproductattention_pa_kernel(
             nc.scalar.activation(
                 out=weights[:], in_=weights[:], func=ACT.Exp, bias=neg_max[:], scale=1.0, accum_out=row_sum[:]
             )
-            weights_of[(qh, h, j)] = weights
             row_sum_of[(qh, h, j)] = row_sum
 
         def normalise(qh, h, j):
             weights = weights_of[(qh, h, j)]
             inv_sum = stats.tile([P, 1], F32)
             nc.vector.reciprocal(out=inv_sum[:], in_=row_sum_of[(qh, h, j)][:])
-            a_bf16 = work.tile([P, SEQ], BF16, bufs=3)
+            a_bf16 = work.tile([P, SEQ], BF16, bufs=4)
             nc.gpsimd.tensor_scalar(
                 out=a_bf16[:], in0=weights[:], scalar1=inv_sum[:], scalar2=any_valid[:], op0=ALU.mult, op1=ALU.mult
             )
@@ -280,20 +289,17 @@ def tile_scaleddotproductattention_pa_kernel(
                         start=(g == 0),
                         stop=(g == FEATURE_PASSES - 1),
                     )
-                if half == 0:
-                    nc.scalar.copy(out=result[:, cols], in_=acc[:])
-                else:
-                    nc.vector.tensor_copy(out=result[:, cols], in_=acc[:])
+                nc.scalar.copy(out=result[:, cols], in_=acc[:])
             rows = slice(qh * Q_HALF + j * P, qh * Q_HALF + (j + 1) * P)
             nc.sync.dma_start(out=out[0, rows, :], in_=result[:])
 
+        transpose_q(0, 0)
+        transpose_k(0, 0)
+        transpose_k(0, 1)
         mask_and_group_v(0)
-        for quarter in range(4):
-            transpose_quarter(0, quarter)
-        quantise_v(0)
 
-        tiles = [(qh, h, j) for qh in range(Q_HALVES) for h in range(HEADS) for j in range(TILES)]
-        PROJECT_LAG = 6 + TILES - 1
+        tiles = [(qh, h, j) for (qh, h) in half_heads for j in range(TILES)]
+        PROJECT_LAG = 3 * TILES + 5
 
         def entered(step, lag):
             return tiles[step - lag] if 0 <= step - lag < len(tiles) else None
@@ -302,17 +308,19 @@ def tile_scaleddotproductattention_pa_kernel(
             if entered(step, 0):
                 scores(*entered(step, 0))
             if entered(step, 1):
-                exponentials(*entered(step, 1))
+                mask(*entered(step, 1))
             if entered(step, 2):
-                normalise(*entered(step, 2))
-            if entered(step, 3):
-                keys_to_partitions(*entered(step, 3))
+                exponentials(*entered(step, 2))
             if entered(step, 4):
-                qh, h, j = entered(step, 4)
+                normalise(*entered(step, 4))
+            if entered(step, 6):
+                keys_to_partitions(*entered(step, 6))
+            if entered(step, 8):
+                qh, h, j = entered(step, 8)
                 if j == TILES - 1:
                     weighted_values(qh, h)
-            if entered(step, 5):
-                qh, h, j = entered(step, 5)
+            if entered(step, 10):
+                qh, h, j = entered(step, 10)
                 if j == TILES - 1 and h % HEADS_PER_PASS == HEADS_PER_PASS - 1:
                     quantise_heads(qh, h // HEADS_PER_PASS)
             if entered(step, PROJECT_LAG):
@@ -320,21 +328,25 @@ def tile_scaleddotproductattention_pa_kernel(
                 if h == HEADS - 1:
                     project(qh, j)
 
-            if entered(step, 0) and entered(step, 0)[0] == 0:
+            if entered(step, 0):
                 qh, h, j = entered(step, 0)
-                if j == 0 and h + 2 < HEADS:
-                    load_head(h + 2)
-                if j == 0 and HEADS - 4 <= h < HEADS - 4 + FEATURE_PASSES:
-                    load_wo(h - (HEADS - 4))
-                if h + 1 < HEADS:
-                    transpose_quarter(h + 1, j)
-                    if j == 0:
-                        mask_and_group_v(h + 1)
-                if h >= HEADS - FEATURE_PASSES:
-                    group_wo(h - (HEADS - FEATURE_PASSES), j)
-            if entered(step, 2) and entered(step, 2)[0] == 0:
+                position = half_heads.index((qh, h))
+                following = half_heads[position + 1 : position + 3]
+                if j == 0 and len(following) == 2:
+                    load(*following[1])
+                if j == 0 and len(following) >= 1:
+                    transpose_q(*following[0])
+                if j in (1, 2) and len(following) >= 1 and following[0][0] == 0:
+                    transpose_k(following[0][1], j - 1)
+                if j == 3 and len(following) >= 1 and following[0][0] == 0:
+                    mask_and_group_v(following[0][1])
+                if qh == 0 and j == 0 and h >= HEADS - FEATURE_PASSES:
+                    load_wo(h - (HEADS - FEATURE_PASSES))
+                if qh == 1 and h < FEATURE_PASSES:
+                    group_wo(h, j)
+            if entered(step, 2):
                 qh, h, j = entered(step, 2)
-                if h + 1 < HEADS and j == 0:
-                    quantise_v(h + 1)
-                if h >= HEADS - FEATURE_PASSES:
-                    quantise_wo(h - (HEADS - FEATURE_PASSES), j)
+                if qh == 0 and j == 0:
+                    quantise_v(h)
+                if qh == 1 and h < FEATURE_PASSES:
+                    quantise_wo(h, j)

@@ -23,11 +23,10 @@ HEAD_DIM = 128
 D_OUT = 1024
 KEY_PASSES = SEQ // K_PASS
 FEATURE_PASSES = HEADS * HEAD_DIM // K_PASS
-HEADS_PER_PASS = K_PASS // HEAD_DIM
-
-Q_HALF = 512
-Q_HALVES = SEQ // Q_HALF
-TILES = Q_HALF // P
+GROUP = K_PASS // HEAD_DIM
+Q_TILES = SEQ // P
+EARLY_Q_TILES = GROUP
+EARLY_QUERIES = EARLY_Q_TILES * P
 
 SCALE = 1.0 / math.sqrt(HEAD_DIM)
 MASKED_SCORE = -1.0e30
@@ -50,42 +49,61 @@ def tile_scaleddotproductattention_pa_kernel(
         acc_psum = stack.enter_context(tc.psum_pool(name="acc_psum", bufs=2))
         stack.enter_context(tc.manual_schedule())
 
+        tiles = [(h, t) for h in range(HEADS) for t in range(EARLY_Q_TILES)]
+        tiles += [(h, t) for t in range(EARLY_Q_TILES, Q_TILES) for h in range(HEADS)]
+        groups = [tiles[first : first + GROUP] for first in range(0, len(tiles), GROUP)]
+
+        def one_head(group):
+            return group < HEADS
+
+        def group_view(by_head_and_query, group):
+            h, t = groups[group][0]
+            if one_head(group):
+                return by_head_and_query[:, h, t * P : (t + GROUP) * P].rearrange("p (i s) -> p i s", s=P)
+            return by_head_and_query[:, h : h + GROUP, t * P : (t + 1) * P]
+
         q_t = keep.tile([P, HEADS, SEQ], BF16)
         k_t = keep.tile([P, HEADS, SEQ], BF16)
         v_codes = keep.tile([P, HEADS, KEY_PASSES * HEAD_DIM], U32, align_bytes=64)
         v_scales = keep.tile([P, HEADS, KEY_PASSES * HEAD_DIM], U8, align_bytes=64)
         wo_codes = keep.tile([P, FEATURE_PASSES, D_OUT], U32, align_bytes=64)
         wo_scales = keep.tile([P, FEATURE_PASSES, D_OUT], U8, align_bytes=64)
+        c_early = keep.tile([P, HEADS, EARLY_QUERIES], BF16)
+        c_codes = keep.tile([P, FEATURE_PASSES, SEQ], U32, align_bytes=64)
+        c_scales = keep.tile([P, FEATURE_PASSES, SEQ], U8, align_bytes=64)
 
         q_raw_of = {}
         k_raw_of = {}
         v_raw_of = {}
-        wo_raw_of_pass = {}
+        wo_raw_of = {}
 
-        def load(qh, h):
-            q_raw = raw.tile([P, TILES, HEAD_DIM], BF16)
-            queries = q_masked[0, h, qh * Q_HALF : (qh + 1) * Q_HALF, :]
-            nc.sync.dma_start(out=q_raw[:], in_=queries.rearrange("(t p) d -> p t d", p=P))
-            q_raw_of[(qh, h)] = q_raw
-            if qh == 0:
-                k_raw = raw.tile([P, SEQ // P, HEAD_DIM], BF16)
-                nc.sync.dma_start(out=k_raw[:], in_=k_masked[0, h].rearrange("(t p) d -> p t d", p=P))
-                k_raw_of[h] = k_raw
-                v_raw = raw.tile([P, 2 * KEY_PASSES, 2 * HEAD_DIM], BF16)
-                nc.sync.dma_start(
-                    out=v_raw[:], in_=v_proj[0, h].rearrange("(c p e) d -> p c (e d)", p=P, e=2)
-                )
-                v_raw_of[h] = v_raw
+        def load_q(group):
+            h, t = groups[group][0]
+            q_raw = raw.tile([P, GROUP, HEAD_DIM], BF16)
+            if one_head(group):
+                rows = q_masked[0, h, t * P : (t + GROUP) * P, :].rearrange("(i p) d -> p i d", p=P)
+            else:
+                rows = q_masked[0, h : h + GROUP, t * P : (t + 1) * P, :].rearrange("i p d -> p i d")
+            nc.sync.dma_start(out=q_raw[:], in_=rows)
+            q_raw_of[group] = q_raw
+
+        def load_k_and_v(h):
+            k_raw = raw.tile([P, SEQ // P, HEAD_DIM], BF16)
+            nc.sync.dma_start(out=k_raw[:], in_=k_masked[0, h].rearrange("(i p) d -> p i d", p=P))
+            k_raw_of[h] = k_raw
+            v_raw = raw.tile([P, 2 * KEY_PASSES, 2 * HEAD_DIM], BF16)
+            nc.sync.dma_start(out=v_raw[:], in_=v_proj[0, h].rearrange("(c p e) d -> p c (e d)", p=P, e=2))
+            v_raw_of[h] = v_raw
 
         def load_wo(g):
             wo_raw = raw.tile([P, PACK, D_OUT], BF16)
             rows = Wo[g * K_PASS : (g + 1) * K_PASS, :]
-            nc.sync.dma_start(out=wo_raw[:], in_=rows.rearrange("(t p) n -> p t n", p=P))
-            wo_raw_of_pass[g] = wo_raw
+            nc.sync.dma_start(out=wo_raw[:], in_=rows.rearrange("(i p) n -> p i n", p=P))
+            wo_raw_of[g] = wo_raw
 
-        half_heads = [(qh, h) for qh in range(Q_HALVES) for h in range(HEADS)]
-        load(*half_heads[0])
-        load(*half_heads[1])
+        for group in range(2):
+            load_q(group)
+            load_k_and_v(group)
 
         ident_bf16 = const.tile([P, P], BF16)
         make_identity(nc, ident_bf16[:])
@@ -108,25 +126,26 @@ def tile_scaleddotproductattention_pa_kernel(
         ind_v_words = const.tile([P, 2 * KEY_PASSES, 2], BF16)
         nc.scalar.dma_start(out=ind_v_words[:], in_=ind_v[0].rearrange("(c p e) -> p c e", p=P, e=2))
 
-        def features_to_partitions(four_row_tiles, columns):
-            flipped = flip_psum.tile([P, 4, P], BF16, tag="flipped")
-            for i in range(4):
+        def features_to_partitions(four_row_tiles, four_blocks):
+            flipped = flip_psum.tile([P, GROUP, P], BF16, tag="flipped")
+            for i in range(GROUP):
                 nc.tensor.transpose(flipped[:, i, :], four_row_tiles[:, i, :], ident_bf16[:])
-            nc.scalar.copy(out=columns, in_=flipped[:].rearrange("p i s -> p (i s)"))
+            nc.scalar.copy(out=four_blocks, in_=flipped[:])
 
-        def transpose_q(qh, h):
-            features_to_partitions(q_raw_of[(qh, h)], q_t[:, h, qh * Q_HALF : (qh + 1) * Q_HALF])
+        def transpose_q(group):
+            features_to_partitions(q_raw_of[group], group_view(q_t, group))
 
         def transpose_k(h, half):
-            features_to_partitions(k_raw_of[h][:, half * 4 : (half + 1) * 4, :], k_t[:, h, half * BANK : (half + 1) * BANK])
+            keys = k_t[:, h, half * BANK : (half + 1) * BANK].rearrange("p (i s) -> p i s", s=P)
+            features_to_partitions(k_raw_of[h][:, half * GROUP : (half + 1) * GROUP, :], keys)
 
-        v_grouped_of_head = {}
+        v_grouped_of = {}
 
         def mask_and_group_v(h):
             v_raw = v_raw_of[h]
             v_grouped = work.tile([P, KEY_PASSES * HEAD_DIM * PACK], BF16, align_bytes=64)
             nc.gpsimd.tensor_tensor(
-                out=v_grouped[:].rearrange("p (g d t) -> p g d t", g=KEY_PASSES, t=PACK),
+                out=v_grouped[:].rearrange("p (g d w) -> p g d w", g=KEY_PASSES, w=PACK),
                 in0=v_raw[:].rearrange("p (g u) (e d) -> p g d (u e)", u=2, e=2),
                 in1=ind_v_words[:]
                 .rearrange("p (g u) e -> p g (u e)", u=2)
@@ -134,37 +153,38 @@ def tile_scaleddotproductattention_pa_kernel(
                 .to_broadcast([P, KEY_PASSES, HEAD_DIM, PACK]),
                 op=ALU.mult,
             )
-            v_grouped_of_head[h] = v_grouped
+            v_grouped_of[h] = v_grouped
 
         def quantise_v(h):
             nc.vector.quantize_mx(
-                out=v_codes[:, h, :].bitcast(FP8X4),
-                scales=v_scales[:, h, :],
-                in_=v_grouped_of_head[h][:],
+                out=v_codes[:, h, :].bitcast(FP8X4), scales=v_scales[:, h, :], in_=v_grouped_of[h][:]
             )
 
         WO_QUARTER = D_OUT // 4
-        wo_grouped_of_quarter = {}
+        wo_grouped_of = {}
 
-        def group_wo(g, quarter):
-            cols = slice(quarter * WO_QUARTER, (quarter + 1) * WO_QUARTER)
-            wo_grouped = work.tile([P, WO_QUARTER * PACK], BF16, align_bytes=64)
+        def side_by_side(grouped, four_rows):
             nc.gpsimd.tensor_scalar(
-                out=wo_grouped[:].rearrange("p (n t) -> p n t", t=PACK),
-                in0=wo_raw_of_pass[g][:, :, cols].rearrange("p t n -> p n t"),
+                out=grouped.rearrange("p (n i) -> p n i", i=PACK),
+                in0=four_rows.rearrange("p i n -> p n i"),
                 scalar1=1.0,
                 scalar2=0.0,
                 op0=ALU.mult,
                 op1=ALU.add,
             )
-            wo_grouped_of_quarter[(g, quarter)] = wo_grouped
 
-        def quantise_wo(g, quarter):
+        def group_wo(eighth):
+            g, quarter = divmod(eighth, 4)
+            cols = slice(quarter * WO_QUARTER, (quarter + 1) * WO_QUARTER)
+            wo_grouped = work.tile([P, WO_QUARTER * PACK], BF16, align_bytes=64)
+            side_by_side(wo_grouped[:], wo_raw_of[g][:, :, cols])
+            wo_grouped_of[eighth] = wo_grouped
+
+        def quantise_wo(eighth):
+            g, quarter = divmod(eighth, 4)
             cols = slice(quarter * WO_QUARTER, (quarter + 1) * WO_QUARTER)
             nc.vector.quantize_mx(
-                out=wo_codes[:, g, cols].bitcast(FP8X4),
-                scales=wo_scales[:, g, cols],
-                in_=wo_grouped_of_quarter[(g, quarter)][:],
+                out=wo_codes[:, g, cols].bitcast(FP8X4), scales=wo_scales[:, g, cols], in_=wo_grouped_of[eighth][:]
             )
 
         scores_of = {}
@@ -172,28 +192,39 @@ def tile_scaleddotproductattention_pa_kernel(
         row_sum_of = {}
         a_bf16_of = {}
         a_grouped_of = {}
-        c_heads_of = {}
-        c_mx_of = {}
+        a_mx_of = {}
+        c_grouped_of = {}
 
-        def scores(qh, h, j):
-            queries = slice(qh * Q_HALF + j * P, qh * Q_HALF + (j + 1) * P)
+        def masked_by_tensor(place):
+            return place % 6 == 5
+
+        def scores(place):
+            h, t = tiles[place]
+            queries = slice(t * P, (t + 1) * P)
             score_lo = score_psum.tile([P, BANK], F32)
-            nc.tensor.matmul(score_lo[:], lhsT=q_t[:, h, queries], rhs=k_t[:, h, 0:BANK], start=True, stop=True)
             score_hi = score_psum.tile([P, BANK], F32)
-            nc.tensor.matmul(score_hi[:], lhsT=q_t[:, h, queries], rhs=k_t[:, h, BANK:SEQ], start=True, stop=True)
-            scores_of[(qh, h, j)] = (score_lo, score_hi)
+            for score, keys in ((score_lo, slice(0, BANK)), (score_hi, slice(BANK, SEQ))):
+                nc.tensor.matmul(
+                    score[:], lhsT=q_t[:, h, queries], rhs=k_t[:, h, keys], start=True, stop=not masked_by_tensor(place)
+                )
+                if masked_by_tensor(place):
+                    nc.tensor.matmul(score[:], lhsT=ident_bf16[:], rhs=mask_bias[:, keys], start=False, stop=True)
+            scores_of[place] = (score_lo, score_hi)
 
-        def mask(qh, h, j):
-            score_lo, score_hi = scores_of[(qh, h, j)]
+        def scale_and_mask(place):
+            score_lo, score_hi = scores_of[place]
             weights = work.tile([P, SEQ], F32, bufs=6)
             for score, keys in ((score_lo, slice(0, BANK)), (score_hi, slice(BANK, SEQ))):
-                nc.vector.scalar_tensor_tensor(
-                    out=weights[:, keys], in0=score[:], scalar=SCALE, in1=mask_bias[:, keys], op0=ALU.mult, op1=ALU.add
-                )
-            weights_of[(qh, h, j)] = weights
+                if masked_by_tensor(place):
+                    nc.scalar.activation(out=weights[:, keys], in_=score[:], func=ACT.Copy, scale=SCALE)
+                else:
+                    nc.vector.scalar_tensor_tensor(
+                        out=weights[:, keys], in0=score[:], scalar=SCALE, in1=mask_bias[:, keys], op0=ALU.mult, op1=ALU.add
+                    )
+            weights_of[place] = weights
 
-        def exponentials(qh, h, j):
-            weights = weights_of[(qh, h, j)]
+        def exponentials(place):
+            weights = weights_of[place]
             neg_max = stats.tile([P, 1], F32)
             nc.vector.tensor_reduce(
                 out=neg_max[:], in_=weights[:], axis=mybir.AxisListType.X, op=ALU.max, negate=True
@@ -202,79 +233,76 @@ def tile_scaleddotproductattention_pa_kernel(
             nc.scalar.activation(
                 out=weights[:], in_=weights[:], func=ACT.Exp, bias=neg_max[:], scale=1.0, accum_out=row_sum[:]
             )
-            row_sum_of[(qh, h, j)] = row_sum
+            row_sum_of[place] = row_sum
 
-        def normalise(qh, h, j):
-            weights = weights_of[(qh, h, j)]
+        def normalise(place):
             inv_sum = stats.tile([P, 1], F32)
-            nc.vector.reciprocal(out=inv_sum[:], in_=row_sum_of[(qh, h, j)][:])
+            nc.vector.reciprocal(out=inv_sum[:], in_=row_sum_of[place][:])
             a_bf16 = work.tile([P, SEQ], BF16, bufs=4)
             nc.gpsimd.tensor_scalar(
-                out=a_bf16[:], in0=weights[:], scalar1=inv_sum[:], scalar2=any_valid[:], op0=ALU.mult, op1=ALU.mult
+                out=a_bf16[:], in0=weights_of[place][:], scalar1=inv_sum[:], scalar2=any_valid[:], op0=ALU.mult, op1=ALU.mult
             )
-            a_bf16_of[(qh, h, j)] = a_bf16
+            a_bf16_of[place] = a_bf16
 
-        def keys_to_partitions(qh, h, j):
-            a_words = a_bf16_of[(qh, h, j)][:].bitcast(F32)
+        def keys_to_partitions(place):
+            a_words = a_bf16_of[place][:].bitcast(F32)
             flipped = flip_psum.tile([P, 2 * KEY_PASSES, P], F32, tag="flipped")
             for c in range(2 * KEY_PASSES):
                 nc.tensor.transpose(flipped[:, c, :], a_words[:, c * P : (c + 1) * P], ident_f32[:])
-            if j == 0:
-                a_grouped = work.tile([P, KEY_PASSES * Q_HALF * PACK], BF16, align_bytes=64)
-                a_grouped_of[(qh, h)] = a_grouped
-            grouped_words = a_grouped_of[(qh, h)][:].bitcast(F32).rearrange("p (g q u) -> p g q u", g=KEY_PASSES, u=2)
+            a_grouped = work.tile([P, KEY_PASSES * P * PACK], BF16, align_bytes=64, bufs=4)
             nc.scalar.copy(
-                out=grouped_words[:, :, j * P : (j + 1) * P, :],
+                out=a_grouped[:].bitcast(F32).rearrange("p (g q u) -> p g q u", g=KEY_PASSES, u=2),
                 in_=flipped[:].rearrange("p (g u) q -> p g q u", u=2),
             )
+            a_grouped_of[place] = a_grouped
 
-        def weighted_values(qh, h):
-            a_grouped = a_grouped_of[(qh, h)]
-            a_codes = work.tile([P, KEY_PASSES, Q_HALF], U32, align_bytes=64)
-            a_scales = work.tile([P, KEY_PASSES, Q_HALF], U8, align_bytes=64)
-            width = Q_HALF * PACK
-            for g in range(KEY_PASSES):
-                nc.vector.quantize_mx(
-                    out=a_codes[:, g, :].bitcast(FP8X4),
-                    scales=a_scales[:, g, :],
-                    in_=a_grouped[:, g * width : (g + 1) * width],
-                )
-            o_t = acc_psum.tile([P, Q_HALF], F32, tag="acc")
-            for g in range(KEY_PASSES):
-                features = slice(g * HEAD_DIM, (g + 1) * HEAD_DIM)
-                nc.tensor.matmul_mx(
-                    out=o_t[:],
-                    lhsT=v_codes[:, h, features].bitcast(FP8X4),
-                    lhsT_scale=v_scales[:, h, features],
-                    rhs=a_codes[:, g, :].bitcast(FP8X4),
-                    rhs_scale=a_scales[:, g, :],
-                    start=(g == 0),
-                    stop=(g == KEY_PASSES - 1),
-                )
-            if h == 0:
-                c_heads = work.tile([P, HEADS, Q_HALF], BF16)
-                c_heads_of[qh] = c_heads
-            nc.scalar.copy(out=c_heads_of[qh][:, h, :], in_=o_t[:])
-
-        def quantise_heads(qh, g):
-            if g == 0:
-                c_grouped = work.tile([P, FEATURE_PASSES, Q_HALF * PACK], BF16, align_bytes=64)
-                c_codes = work.tile([P, FEATURE_PASSES, Q_HALF], U32, align_bytes=64)
-                c_scales = work.tile([P, FEATURE_PASSES, Q_HALF], U8, align_bytes=64)
-                c_mx_of[qh] = (c_grouped, c_codes, c_scales)
-            c_grouped, c_codes, c_scales = c_mx_of[qh]
-            four_heads = c_heads_of[qh][:, g * HEADS_PER_PASS : (g + 1) * HEADS_PER_PASS, :]
-            nc.vector.tensor_copy(
-                out=c_grouped[:, g, :].rearrange("p (q t) -> p q t", t=PACK),
-                in_=four_heads.rearrange("p t q -> p q t"),
-            )
+        def quantise_weights(place):
+            group, i = divmod(place, GROUP)
+            if i == 0:
+                a_codes = work.tile([P, GROUP, KEY_PASSES * P], U32, align_bytes=64)
+                a_scales = work.tile([P, GROUP, KEY_PASSES * P], U8, align_bytes=64)
+                a_mx_of[group] = (a_codes, a_scales)
+            a_codes, a_scales = a_mx_of[group]
             nc.vector.quantize_mx(
-                out=c_codes[:, g, :].bitcast(FP8X4), scales=c_scales[:, g, :], in_=c_grouped[:, g, :]
+                out=a_codes[:, i, :].bitcast(FP8X4), scales=a_scales[:, i, :], in_=a_grouped_of[place][:]
             )
 
-        def project(qh, j):
-            c_grouped, c_codes, c_scales = c_mx_of[qh]
-            queries = slice(j * P, (j + 1) * P)
+        def weighted_values(group):
+            a_codes, a_scales = a_mx_of[group]
+            o_t = acc_psum.tile([P, GROUP, P], F32, tag="acc")
+            for i, (h, t) in enumerate(groups[group]):
+                for g in range(KEY_PASSES):
+                    block = slice(g * P, (g + 1) * P)
+                    nc.tensor.matmul_mx(
+                        out=o_t[:, i, :],
+                        lhsT=v_codes[:, h, block].bitcast(FP8X4),
+                        lhsT_scale=v_scales[:, h, block],
+                        rhs=a_codes[:, i, block].bitcast(FP8X4),
+                        rhs_scale=a_scales[:, i, block],
+                        start=(g == 0),
+                        stop=(g == KEY_PASSES - 1),
+                    )
+            if one_head(group):
+                nc.scalar.copy(out=group_view(c_early, group), in_=o_t[:])
+            else:
+                c_grouped = work.tile([P, P * PACK], BF16, align_bytes=64, tag="c_grouped_late")
+                nc.scalar.copy(
+                    out=c_grouped[:].rearrange("p (q i) -> p q i", i=PACK), in_=o_t[:].rearrange("p i q -> p q i")
+                )
+                c_grouped_of[group] = c_grouped
+
+        def group_early_heads(g):
+            c_grouped = work.tile([P, EARLY_QUERIES * PACK], BF16, align_bytes=64, tag="c_grouped_early")
+            side_by_side(c_grouped[:], c_early[:, g * GROUP : (g + 1) * GROUP, :])
+            c_grouped_of[("early", g)] = c_grouped
+
+        def quantise_heads(g, queries, c_grouped):
+            nc.vector.quantize_mx(
+                out=c_codes[:, g, queries].bitcast(FP8X4), scales=c_scales[:, g, queries], in_=c_grouped[:]
+            )
+
+        def project(t):
+            queries = slice(t * P, (t + 1) * P)
             result = work.tile([P, D_OUT], F32, bufs=3)
             for half in range(D_OUT // BANK):
                 cols = slice(half * BANK, (half + 1) * BANK)
@@ -289,64 +317,80 @@ def tile_scaleddotproductattention_pa_kernel(
                         start=(g == 0),
                         stop=(g == FEATURE_PASSES - 1),
                     )
-                nc.scalar.copy(out=result[:, cols], in_=acc[:])
-            rows = slice(qh * Q_HALF + j * P, qh * Q_HALF + (j + 1) * P)
-            nc.sync.dma_start(out=out[0, rows, :], in_=result[:])
+                if t == Q_TILES - 1 and half == 1:
+                    nc.vector.tensor_copy(out=result[:, cols], in_=acc[:])
+                else:
+                    nc.scalar.copy(out=result[:, cols], in_=acc[:])
+            nc.sync.dma_start(out=out[0, queries, :], in_=result[:])
 
-        transpose_q(0, 0)
+        transpose_q(0)
         transpose_k(0, 0)
         transpose_k(0, 1)
         mask_and_group_v(0)
 
-        tiles = [(qh, h, j) for (qh, h) in half_heads for j in range(TILES)]
-        PROJECT_LAG = 3 * TILES + 5
+        WO_FIRST_GROUP = HEADS
+        WO_GROUPS = 4
+        EARLY_PROJECT_LAG = (WO_GROUPS + 1) * GROUP + 1
 
         def entered(step, lag):
-            return tiles[step - lag] if 0 <= step - lag < len(tiles) else None
+            return step - lag if 0 <= step - lag < len(tiles) else None
 
-        for step in range(len(tiles) + PROJECT_LAG + 1):
-            if entered(step, 0):
-                scores(*entered(step, 0))
-            if entered(step, 1):
-                mask(*entered(step, 1))
-            if entered(step, 2):
-                exponentials(*entered(step, 2))
-            if entered(step, 4):
-                normalise(*entered(step, 4))
-            if entered(step, 6):
-                keys_to_partitions(*entered(step, 6))
-            if entered(step, 8):
-                qh, h, j = entered(step, 8)
-                if j == TILES - 1:
-                    weighted_values(qh, h)
-            if entered(step, 10):
-                qh, h, j = entered(step, 10)
-                if j == TILES - 1 and h % HEADS_PER_PASS == HEADS_PER_PASS - 1:
-                    quantise_heads(qh, h // HEADS_PER_PASS)
-            if entered(step, PROJECT_LAG):
-                qh, h, j = entered(step, PROJECT_LAG)
-                if h == HEADS - 1:
-                    project(qh, j)
+        def closes_group(place):
+            return place is not None and place % GROUP == GROUP - 1
 
-            if entered(step, 0):
-                qh, h, j = entered(step, 0)
-                position = half_heads.index((qh, h))
-                following = half_heads[position + 1 : position + 3]
-                if j == 0 and len(following) == 2:
-                    load(*following[1])
-                if j == 0 and len(following) >= 1:
-                    transpose_q(*following[0])
-                if j in (1, 2) and len(following) >= 1 and following[0][0] == 0:
-                    transpose_k(following[0][1], j - 1)
-                if j == 3 and len(following) >= 1 and following[0][0] == 0:
-                    mask_and_group_v(following[0][1])
-                if qh == 0 and j == 0 and h >= HEADS - FEATURE_PASSES:
-                    load_wo(h - (HEADS - FEATURE_PASSES))
-                if qh == 1 and h < FEATURE_PASSES:
-                    group_wo(h, j)
-            if entered(step, 2):
-                qh, h, j = entered(step, 2)
-                if qh == 0 and j == 0:
-                    quantise_v(h)
-                if qh == 1 and h < FEATURE_PASSES:
-                    quantise_wo(h, j)
+        for step in range(len(tiles) + EARLY_PROJECT_LAG + 1):
+            if entered(step, 0) is not None:
+                scores(entered(step, 0))
+            if entered(step, 1) is not None:
+                scale_and_mask(entered(step, 1))
+            if entered(step, 2) is not None:
+                exponentials(entered(step, 2))
+            if entered(step, 4) is not None:
+                normalise(entered(step, 4))
+            if entered(step, 6) is not None:
+                keys_to_partitions(entered(step, 6))
+            if entered(step, 8) is not None:
+                quantise_weights(entered(step, 8))
+            if closes_group(entered(step, 10)):
+                weighted_values(entered(step, 10) // GROUP)
+            if closes_group(entered(step, 12)):
+                group = entered(step, 12) // GROUP
+                h, t = groups[group][0]
+                if not one_head(group):
+                    quantise_heads(h // GROUP, slice(t * P, (t + 1) * P), c_grouped_of[group])
+                elif h % GROUP == GROUP - 1:
+                    group_early_heads(h // GROUP)
+            if closes_group(entered(step, 14)):
+                group = entered(step, 14) // GROUP
+                h, t = groups[group][GROUP - 1]
+                if not one_head(group) and h == HEADS - 1:
+                    project(t)
+                if one_head(group) and h % GROUP == GROUP - 1:
+                    quantise_heads(h // GROUP, slice(0, EARLY_QUERIES), c_grouped_of[("early", h // GROUP)])
+            if entered(step, EARLY_PROJECT_LAG) is not None:
+                h, t = tiles[entered(step, EARLY_PROJECT_LAG)]
+                if t < EARLY_Q_TILES and h == HEADS - 1:
+                    project(t)
+
+            if entered(step, 0) is not None:
+                group, i = divmod(entered(step, 0), GROUP)
+                if i == 0 and group + 2 < len(groups):
+                    load_q(group + 2)
+                    if one_head(group + 2):
+                        load_k_and_v(group + 2)
+                if i == 0 and group + 1 < len(groups):
+                    transpose_q(group + 1)
+                if i in (1, 2) and one_head(group + 1):
+                    transpose_k(group + 1, i - 1)
+                if i == 3 and one_head(group + 1):
+                    mask_and_group_v(group + 1)
+                if i == 0 and WO_FIRST_GROUP - FEATURE_PASSES <= group < WO_FIRST_GROUP:
+                    load_wo(group - (WO_FIRST_GROUP - FEATURE_PASSES))
+                if i % 2 == 0 and WO_FIRST_GROUP <= group < WO_FIRST_GROUP + WO_GROUPS:
+                    group_wo((entered(step, 0) - WO_FIRST_GROUP * GROUP) // 2)
+            if entered(step, 2) is not None:
+                group, i = divmod(entered(step, 2), GROUP)
+                if i == 0 and one_head(group):
+                    quantise_v(group)
+                if i % 2 == 0 and WO_FIRST_GROUP <= group < WO_FIRST_GROUP + WO_GROUPS:
+                    quantise_wo((entered(step, 2) - WO_FIRST_GROUP * GROUP) // 2)

@@ -160,7 +160,7 @@ def tile_scaleddotproductattention_pa_kernel(
                 out=v_codes[:, h, :].bitcast(FP8X4), scales=v_scales[:, h, :], in_=v_grouped_of[h][:]
             )
 
-        WO_QUARTER = D_OUT // 4
+        WO_PIECES = 2 * FEATURE_PASSES
         wo_grouped_of = {}
 
         def side_by_side(grouped, four_rows):
@@ -173,22 +173,23 @@ def tile_scaleddotproductattention_pa_kernel(
                 op1=ALU.add,
             )
 
-        def group_wo(eighth):
-            g, quarter = divmod(eighth, 4)
-            cols = slice(quarter * WO_QUARTER, (quarter + 1) * WO_QUARTER)
-            wo_grouped = work.tile([P, WO_QUARTER * PACK], BF16, align_bytes=64)
+        def group_wo(piece):
+            g, half = divmod(piece, 2)
+            cols = slice(half * BANK, (half + 1) * BANK)
+            wo_grouped = work.tile([P, BANK * PACK], BF16, align_bytes=64)
             side_by_side(wo_grouped[:], wo_raw_of[g][:, :, cols])
-            wo_grouped_of[eighth] = wo_grouped
+            wo_grouped_of[piece] = wo_grouped
 
-        def quantise_wo(eighth):
-            g, quarter = divmod(eighth, 4)
-            cols = slice(quarter * WO_QUARTER, (quarter + 1) * WO_QUARTER)
+        def quantise_wo(piece):
+            g, half = divmod(piece, 2)
+            cols = slice(half * BANK, (half + 1) * BANK)
             nc.vector.quantize_mx(
-                out=wo_codes[:, g, cols].bitcast(FP8X4), scales=wo_scales[:, g, cols], in_=wo_grouped_of[eighth][:]
+                out=wo_codes[:, g, cols].bitcast(FP8X4), scales=wo_scales[:, g, cols], in_=wo_grouped_of[piece][:]
             )
 
         scores_of = {}
         weights_of = {}
+        neg_max_of = {}
         row_sum_of = {}
         a_bf16_of = {}
         a_grouped_of = {}
@@ -213,7 +214,7 @@ def tile_scaleddotproductattention_pa_kernel(
 
         def scale_and_mask(place):
             score_lo, score_hi = scores_of[place]
-            weights = work.tile([P, SEQ], F32, bufs=6)
+            weights = work.tile([P, SEQ], F32, bufs=7)
             for score, keys in ((score_lo, slice(0, BANK)), (score_hi, slice(BANK, SEQ))):
                 if masked_by_tensor(place):
                     nc.scalar.activation(out=weights[:, keys], in_=score[:], func=ACT.Copy, scale=SCALE)
@@ -223,15 +224,18 @@ def tile_scaleddotproductattention_pa_kernel(
                     )
             weights_of[place] = weights
 
-        def exponentials(place):
-            weights = weights_of[place]
+        def row_maximum(place):
             neg_max = stats.tile([P, 1], F32)
             nc.vector.tensor_reduce(
-                out=neg_max[:], in_=weights[:], axis=mybir.AxisListType.X, op=ALU.max, negate=True
+                out=neg_max[:], in_=weights_of[place][:], axis=mybir.AxisListType.X, op=ALU.max, negate=True
             )
+            neg_max_of[place] = neg_max
+
+        def exponentials(place):
+            weights = weights_of[place]
             row_sum = stats.tile([P, 1], F32)
             nc.scalar.activation(
-                out=weights[:], in_=weights[:], func=ACT.Exp, bias=neg_max[:], scale=1.0, accum_out=row_sum[:]
+                out=weights[:], in_=weights[:], func=ACT.Exp, bias=neg_max_of[place][:], scale=1.0, accum_out=row_sum[:]
             )
             row_sum_of[place] = row_sum
 
@@ -249,23 +253,24 @@ def tile_scaleddotproductattention_pa_kernel(
             flipped = flip_psum.tile([P, 2 * KEY_PASSES, P], F32, tag="flipped")
             for c in range(2 * KEY_PASSES):
                 nc.tensor.transpose(flipped[:, c, :], a_words[:, c * P : (c + 1) * P], ident_f32[:])
-            a_grouped = work.tile([P, KEY_PASSES * P * PACK], BF16, align_bytes=64, bufs=4)
-            nc.scalar.copy(
-                out=a_grouped[:].bitcast(F32).rearrange("p (g q u) -> p g q u", g=KEY_PASSES, u=2),
-                in_=flipped[:].rearrange("p (g u) q -> p g q u", u=2),
-            )
-            a_grouped_of[place] = a_grouped
-
-        def quantise_weights(place):
             group, i = divmod(place, GROUP)
             if i == 0:
-                a_codes = work.tile([P, GROUP, KEY_PASSES * P], U32, align_bytes=64)
-                a_scales = work.tile([P, GROUP, KEY_PASSES * P], U8, align_bytes=64)
-                a_mx_of[group] = (a_codes, a_scales)
-            a_codes, a_scales = a_mx_of[group]
-            nc.vector.quantize_mx(
-                out=a_codes[:, i, :].bitcast(FP8X4), scales=a_scales[:, i, :], in_=a_grouped_of[place][:]
+                a_grouped = work.tile([P, GROUP, KEY_PASSES * P * PACK], BF16, align_bytes=64)
+                a_grouped_of[group] = a_grouped
+            nc.scalar.copy(
+                out=a_grouped_of[group][:, i, :].bitcast(F32).rearrange("p (g q u) -> p g q u", g=KEY_PASSES, u=2),
+                in_=flipped[:].rearrange("p (g u) q -> p g q u", u=2),
             )
+
+        def quantise_weights(group):
+            a_codes = work.tile([P, GROUP, KEY_PASSES * P], U32, align_bytes=64)
+            a_scales = work.tile([P, GROUP, KEY_PASSES * P], U8, align_bytes=64)
+            nc.vector.quantize_mx(
+                out=a_codes[:].rearrange("p i w -> p (i w)").bitcast(FP8X4),
+                scales=a_scales[:].rearrange("p i w -> p (i w)"),
+                in_=a_grouped_of[group][:].rearrange("p i w -> p (i w)"),
+            )
+            a_mx_of[group] = (a_codes, a_scales)
 
         def weighted_values(group):
             a_codes, a_scales = a_mx_of[group]
@@ -301,7 +306,7 @@ def tile_scaleddotproductattention_pa_kernel(
                 out=c_codes[:, g, queries].bitcast(FP8X4), scales=c_scales[:, g, queries], in_=c_grouped[:]
             )
 
-        def project(t):
+        def project(t, vector_helps):
             queries = slice(t * P, (t + 1) * P)
             result = work.tile([P, D_OUT], F32, bufs=3)
             for half in range(D_OUT // BANK):
@@ -317,20 +322,39 @@ def tile_scaleddotproductattention_pa_kernel(
                         start=(g == 0),
                         stop=(g == FEATURE_PASSES - 1),
                     )
-                if t == Q_TILES - 1 and half == 1:
+                if vector_helps and half == 1:
                     nc.vector.tensor_copy(out=result[:, cols], in_=acc[:])
                 else:
                     nc.scalar.copy(out=result[:, cols], in_=acc[:])
             nc.sync.dma_start(out=out[0, queries, :], in_=result[:])
 
+        def prepare_on_gpsimd(group):
+            if group + 1 < HEADS:
+                mask_and_group_v(group + 1)
+            elif group == HEADS - 1:
+                group_early_heads(0)
+            elif group - HEADS < WO_PIECES:
+                group_wo(group - HEADS)
+            elif group - HEADS == WO_PIECES:
+                group_early_heads(1)
+
+        def quantise_prepared(group):
+            if group + 1 < HEADS:
+                quantise_v(group + 1)
+            elif group == HEADS - 1:
+                quantise_heads(0, slice(0, EARLY_QUERIES), c_grouped_of[("early", 0)])
+            elif group - HEADS < WO_PIECES:
+                quantise_wo(group - HEADS)
+            elif group - HEADS == WO_PIECES:
+                quantise_heads(1, slice(0, EARLY_QUERIES), c_grouped_of[("early", 1)])
+
         transpose_q(0)
         transpose_k(0, 0)
         transpose_k(0, 1)
-        mask_and_group_v(0)
+        prepare_on_gpsimd(-1)
 
-        WO_FIRST_GROUP = HEADS
-        WO_GROUPS = 4
-        EARLY_PROJECT_LAG = (WO_GROUPS + 1) * GROUP + 1
+        EARLY_PROJECT_STEP = (HEADS + WO_PIECES + 2) * GROUP + 2
+        LAST_LAG = 14
 
         def entered(step, lag):
             return step - lag if 0 <= step - lag < len(tiles) else None
@@ -338,19 +362,21 @@ def tile_scaleddotproductattention_pa_kernel(
         def closes_group(place):
             return place is not None and place % GROUP == GROUP - 1
 
-        for step in range(len(tiles) + EARLY_PROJECT_LAG + 1):
+        for step in range(len(tiles) + LAST_LAG + 1):
             if entered(step, 0) is not None:
                 scores(entered(step, 0))
             if entered(step, 1) is not None:
                 scale_and_mask(entered(step, 1))
             if entered(step, 2) is not None:
-                exponentials(entered(step, 2))
-            if entered(step, 4) is not None:
-                normalise(entered(step, 4))
-            if entered(step, 6) is not None:
-                keys_to_partitions(entered(step, 6))
-            if entered(step, 8) is not None:
-                quantise_weights(entered(step, 8))
+                row_maximum(entered(step, 2))
+            if entered(step, 3) is not None:
+                exponentials(entered(step, 3))
+            if entered(step, 5) is not None:
+                normalise(entered(step, 5))
+            if entered(step, 7) is not None:
+                keys_to_partitions(entered(step, 7))
+            if closes_group(entered(step, 8)):
+                quantise_weights(entered(step, 8) // GROUP)
             if closes_group(entered(step, 10)):
                 weighted_values(entered(step, 10) // GROUP)
             if closes_group(entered(step, 12)):
@@ -358,19 +384,13 @@ def tile_scaleddotproductattention_pa_kernel(
                 h, t = groups[group][0]
                 if not one_head(group):
                     quantise_heads(h // GROUP, slice(t * P, (t + 1) * P), c_grouped_of[group])
-                elif h % GROUP == GROUP - 1:
-                    group_early_heads(h // GROUP)
-            if closes_group(entered(step, 14)):
-                group = entered(step, 14) // GROUP
-                h, t = groups[group][GROUP - 1]
-                if not one_head(group) and h == HEADS - 1:
-                    project(t)
-                if one_head(group) and h % GROUP == GROUP - 1:
-                    quantise_heads(h // GROUP, slice(0, EARLY_QUERIES), c_grouped_of[("early", h // GROUP)])
-            if entered(step, EARLY_PROJECT_LAG) is not None:
-                h, t = tiles[entered(step, EARLY_PROJECT_LAG)]
-                if t < EARLY_Q_TILES and h == HEADS - 1:
-                    project(t)
+            if closes_group(entered(step, LAST_LAG)):
+                h, t = tiles[entered(step, LAST_LAG)]
+                if t >= EARLY_Q_TILES and h == HEADS - 1:
+                    project(t, vector_helps=step > len(tiles))
+            if step >= EARLY_PROJECT_STEP and (step - EARLY_PROJECT_STEP) % GROUP == 0:
+                if (step - EARLY_PROJECT_STEP) // GROUP < EARLY_Q_TILES:
+                    project((step - EARLY_PROJECT_STEP) // GROUP, vector_helps=step > len(tiles))
 
             if entered(step, 0) is not None:
                 group, i = divmod(entered(step, 0), GROUP)
@@ -382,15 +402,8 @@ def tile_scaleddotproductattention_pa_kernel(
                     transpose_q(group + 1)
                 if i in (1, 2) and one_head(group + 1):
                     transpose_k(group + 1, i - 1)
-                if i == 3 and one_head(group + 1):
-                    mask_and_group_v(group + 1)
-                if i == 0 and WO_FIRST_GROUP - FEATURE_PASSES <= group < WO_FIRST_GROUP:
-                    load_wo(group - (WO_FIRST_GROUP - FEATURE_PASSES))
-                if i % 2 == 0 and WO_FIRST_GROUP <= group < WO_FIRST_GROUP + WO_GROUPS:
-                    group_wo((entered(step, 0) - WO_FIRST_GROUP * GROUP) // 2)
-            if entered(step, 2) is not None:
-                group, i = divmod(entered(step, 2), GROUP)
-                if i == 0 and one_head(group):
-                    quantise_v(group)
-                if i % 2 == 0 and WO_FIRST_GROUP <= group < WO_FIRST_GROUP + WO_GROUPS:
-                    quantise_wo((entered(step, 2) - WO_FIRST_GROUP * GROUP) // 2)
+                if i == 0 and HEADS - FEATURE_PASSES <= group < HEADS:
+                    load_wo(group - (HEADS - FEATURE_PASSES))
+                if i == GROUP - 1:
+                    quantise_prepared(group - 1)
+                    prepare_on_gpsimd(group)

@@ -25,11 +25,10 @@ KEY_PASSES = SEQ // K_PASS
 FEATURE_PASSES = HEADS * HEAD_DIM // K_PASS
 GROUP = K_PASS // HEAD_DIM
 Q_TILES = SEQ // P
-EARLY_Q_TILES = GROUP
-EARLY_QUERIES = EARLY_Q_TILES * P
+KEY_HALVES = SEQ // BANK
 
 SCALE = 1.0 / math.sqrt(HEAD_DIM)
-MASKED_SCORE = -1.0e30
+SCORE_BANKS = 8
 
 FLOPS = 3 * 2 * SEQ * SEQ * HEADS * HEAD_DIM
 
@@ -41,34 +40,33 @@ def tile_scaleddotproductattention_pa_kernel(
     with ExitStack() as stack:
         const = stack.enter_context(tc.tile_pool(name="const", bufs=1))
         keep = stack.enter_context(tc.tile_pool(name="keep", bufs=1))
-        raw = stack.enter_context(tc.tile_pool(name="raw", bufs=2))
+        raw = stack.enter_context(tc.tile_pool(name="raw", bufs=4))
         work = stack.enter_context(tc.tile_pool(name="work", bufs=2))
         stats = stack.enter_context(tc.tile_pool(name="stats", bufs=8))
-        score_psum = stack.enter_context(tc.psum_pool(name="score_psum", bufs=2))
-        flip_psum = stack.enter_context(tc.psum_pool(name="flip_psum", bufs=2))
-        acc_psum = stack.enter_context(tc.psum_pool(name="acc_psum", bufs=2))
+        score_psum = stack.enter_context(tc.psum_pool(name="score_psum", bufs=SCORE_BANKS))
         stack.enter_context(tc.manual_schedule())
 
-        tiles = [(h, t) for h in range(HEADS) for t in range(EARLY_Q_TILES)]
-        tiles += [(h, t) for t in range(EARLY_Q_TILES, Q_TILES) for h in range(HEADS)]
-        groups = [tiles[first : first + GROUP] for first in range(0, len(tiles), GROUP)]
+        groups = [(g, t) for g in range(FEATURE_PASSES) for t in range(Q_TILES)]
+        END = GROUP * len(groups)
 
-        def one_head(group):
-            return group < HEADS
+        LAST = len(groups) - 1
+        ON_SCALAR = ()
+        AT_THE_END = {END - 3: "vector", END - 2: "scalar", END - 1: "vector"}
+        NORM_LAG = 4
+        FLIP_LAG = 6
+        MASK_LAG = 7
 
-        def group_view(by_head_and_query, group):
-            h, t = groups[group][0]
-            if one_head(group):
-                return by_head_and_query[:, h, t * P : (t + GROUP) * P].rearrange("p (i s) -> p i s", s=P)
-            return by_head_and_query[:, h : h + GROUP, t * P : (t + 1) * P]
+        def head_and_queries(place):
+            group, i = divmod(place, GROUP)
+            g, t = groups[group]
+            return g * GROUP + i, slice(t * P, (t + 1) * P)
 
-        q_t = keep.tile([P, HEADS, SEQ], BF16)
         k_t = keep.tile([P, HEADS, SEQ], BF16)
+        stand_in = keep.tile([P, HEADS], BF16)
         v_codes = keep.tile([P, HEADS, KEY_PASSES * HEAD_DIM], U32, align_bytes=64)
         v_scales = keep.tile([P, HEADS, KEY_PASSES * HEAD_DIM], U8, align_bytes=64)
         wo_codes = keep.tile([P, FEATURE_PASSES, D_OUT], U32, align_bytes=64)
         wo_scales = keep.tile([P, FEATURE_PASSES, D_OUT], U8, align_bytes=64)
-        c_early = keep.tile([P, HEADS, EARLY_QUERIES], BF16)
         c_codes = keep.tile([P, FEATURE_PASSES, SEQ], U32, align_bytes=64)
         c_scales = keep.tile([P, FEATURE_PASSES, SEQ], U8, align_bytes=64)
 
@@ -78,75 +76,169 @@ def tile_scaleddotproductattention_pa_kernel(
         wo_raw_of = {}
 
         def load_q(group):
-            h, t = groups[group][0]
+            g, t = groups[group]
             q_raw = raw.tile([P, GROUP, HEAD_DIM], BF16)
-            if one_head(group):
-                rows = q_masked[0, h, t * P : (t + GROUP) * P, :].rearrange("(i p) d -> p i d", p=P)
-            else:
-                rows = q_masked[0, h : h + GROUP, t * P : (t + 1) * P, :].rearrange("i p d -> p i d")
-            nc.sync.dma_start(out=q_raw[:], in_=rows)
+            rows = q_masked[0, g * GROUP : (g + 1) * GROUP, t * P : (t + 1) * P, :]
+            nc.sync.dma_start(out=q_raw[:], in_=rows.rearrange("i p d -> p i d"))
             q_raw_of[group] = q_raw
 
-        def load_k_and_v(h):
+        def load_k(h):
             k_raw = raw.tile([P, SEQ // P, HEAD_DIM], BF16)
             nc.sync.dma_start(out=k_raw[:], in_=k_masked[0, h].rearrange("(i p) d -> p i d", p=P))
             k_raw_of[h] = k_raw
+
+        def load_v(h):
             v_raw = raw.tile([P, 2 * KEY_PASSES, 2 * HEAD_DIM], BF16)
             nc.sync.dma_start(out=v_raw[:], in_=v_proj[0, h].rearrange("(c p e) d -> p c (e d)", p=P, e=2))
             v_raw_of[h] = v_raw
 
         def load_wo(g):
-            wo_raw = raw.tile([P, PACK, D_OUT], BF16)
+            wo_raw = raw.tile([P, PACK, D_OUT], BF16, bufs=2)
             rows = Wo[g * K_PASS : (g + 1) * K_PASS, :]
             nc.sync.dma_start(out=wo_raw[:], in_=rows.rearrange("(i p) n -> p i n", p=P))
             wo_raw_of[g] = wo_raw
 
-        for group in range(2):
-            load_q(group)
-            load_k_and_v(group)
+        ind_k_rows = const.tile([P, SEQ], BF16)
+        nc.scalar.dma_start(out=ind_k_rows[:], in_=ind_k[0].partition_broadcast(P))
+        load_k(0)
+        load_q(0)
+        for h in range(1, GROUP):
+            load_k(h)
+        ind_v_words = const.tile([P, 2 * KEY_PASSES, 2], BF16)
+        nc.scalar.dma_start(out=ind_v_words[:], in_=ind_v[0].rearrange("(c p e) -> p c e", p=P, e=2))
+        ind_k_words = const.tile([P, 2 * KEY_PASSES, 2], BF16)
+        nc.scalar.dma_start(out=ind_k_words[:], in_=ind_k[0].rearrange("(c p e) -> p c e", p=P, e=2))
+        load_q(1)
+        for h in range(GROUP):
+            load_v(h)
 
+        ones = const.tile([P, 1], BF16)
+        nc.vector.memset(ones[:], 1.0)
+        table_loader = const.tile([P, 1], F32)
+        nc.scalar.activation(out=table_loader[:], in_=ones[:], func=ACT.Exp)
         ident_bf16 = const.tile([P, P], BF16)
         make_identity(nc, ident_bf16[:])
         ident_f32 = const.tile([P, P], F32)
         make_identity(nc, ident_f32[:])
-
-        ind_k_rows = const.tile([P, SEQ], BF16)
-        nc.scalar.dma_start(out=ind_k_rows[:], in_=ind_k[0].partition_broadcast(P))
-        mask_bias = const.tile([P, SEQ], BF16)
+        valid_keys = const.tile([P, 1], F32)
+        nc.vector.reduce_sum(out=valid_keys[:], in_=ind_k_rows[:], axis=mybir.AxisListType.X)
+        inv_valid = const.tile([P, 1], F32)
+        nc.vector.tensor_scalar(out=inv_valid[:], in0=valid_keys[:], scalar1=1.0, scalar2=None, op0=ALU.max)
+        masked_rows = const.tile([P, SEQ], BF16)
         nc.vector.tensor_scalar(
-            out=mask_bias[:],
-            in0=ind_k_rows[:],
-            scalar1=-1.0,
-            scalar2=-MASKED_SCORE,
-            op0=ALU.add,
-            op1=ALU.mult,
+            out=masked_rows[:], in0=ind_k_rows[:], scalar1=-1.0, scalar2=1.0, op0=ALU.mult, op1=ALU.add
         )
+        nc.vector.reciprocal(out=inv_valid[:], in_=inv_valid[:])
         any_valid = const.tile([P, 1], F32)
-        nc.vector.reduce_max(out=any_valid[:], in_=ind_k_rows[:], axis=mybir.AxisListType.X)
-        ind_v_words = const.tile([P, 2 * KEY_PASSES, 2], BF16)
-        nc.scalar.dma_start(out=ind_v_words[:], in_=ind_v[0].rearrange("(c p e) -> p c e", p=P, e=2))
+        nc.vector.tensor_scalar(out=any_valid[:], in0=valid_keys[:], scalar1=1.0, scalar2=None, op0=ALU.min)
+        neg_masked = const.tile([P, 1], F32)
+        nc.vector.tensor_scalar(
+            out=neg_masked[:], in0=valid_keys[:], scalar1=-float(SEQ), scalar2=any_valid[:], op0=ALU.add, op1=ALU.mult
+        )
+        key_mask = const.tile([P, KEY_PASSES, P, PACK], BF16)
 
-        def features_to_partitions(four_row_tiles, four_blocks):
-            flipped = flip_psum.tile([P, GROUP, P], BF16, tag="flipped")
+        def build_key_mask():
+            nc.vector.tensor_copy(
+                out=key_mask[:],
+                in_=ind_k_words[:]
+                .rearrange("p (g u) e -> p g (u e)", u=2)
+                .unsqueeze(2)
+                .to_broadcast([P, KEY_PASSES, P, PACK]),
+            )
+
+        in_psum = {}
+
+        def features_to_partitions(pool, tag, four_row_tiles):
+            flipped = pool.tile([P, GROUP, P], BF16, tag=tag, name="flipped")
             for i in range(GROUP):
                 nc.tensor.transpose(flipped[:, i, :], four_row_tiles[:, i, :], ident_bf16[:])
-            nc.scalar.copy(out=four_blocks, in_=flipped[:])
+            return flipped
 
-        def transpose_q(group):
-            features_to_partitions(q_raw_of[group], group_view(q_t, group))
+        q_t_of = {}
+        mean_of = {}
+        stand_in_rows_of = {}
+        stand_in_scores_of = {}
 
-        def transpose_k(h, half):
-            keys = k_t[:, h, half * BANK : (half + 1) * BANK].rearrange("p (i s) -> p i s", s=P)
-            features_to_partitions(k_raw_of[h][:, half * GROUP : (half + 1) * GROUP, :], keys)
+        Q_WORDS = GROUP * P // 2
+
+        def small_products(next_group, heads, group):
+            bank = score_psum.tile([P, BANK], F32, tag="score")
+            if next_group is not None:
+                q_view = bank[:, 0:Q_WORDS].bitcast(BF16).rearrange("p (i q) -> p i q", i=GROUP)
+                for i in range(GROUP):
+                    nc.tensor.transpose(q_view[:, i, :], q_raw_of[next_group][:, i, :], ident_bf16[:])
+            for j, h in enumerate(heads):
+                for i in range(SEQ // P):
+                    nc.tensor.matmul(
+                        bank[:, Q_WORDS + j : Q_WORDS + j + 1],
+                        lhsT=k_raw_of[h][:, i, :],
+                        rhs=ones[:],
+                        start=(i == 0),
+                        stop=(i == SEQ // P - 1),
+                    )
+            if group is not None:
+                for i in range(GROUP):
+                    h, queries = head_and_queries(group * GROUP + i)
+                    nc.tensor.matmul(
+                        bank[:, Q_WORDS + GROUP + i : Q_WORDS + GROUP + i + 1],
+                        lhsT=q_t_of[group][:, i, :],
+                        rhs=stand_in[:, h : h + 1],
+                        start=True,
+                        stop=True,
+                    )
+            in_psum["small"] = bank
+
+        def take_small_products(next_group, heads, group):
+            bank = in_psum["small"]
+            if group is not None:
+                stand_in_scores = stats.tile([P, GROUP], F32)
+                nc.scalar.copy(out=stand_in_scores[:], in_=bank[:, Q_WORDS + GROUP : Q_WORDS + 2 * GROUP])
+                stand_in_scores_of[group] = stand_in_scores
+            if heads:
+                mean = stats.tile([P, len(heads)], F32)
+                nc.scalar.activation(
+                    out=mean[:], in_=bank[:, Q_WORDS : Q_WORDS + len(heads)], func=ACT.Copy, scale=inv_valid[:]
+                )
+                for j, h in enumerate(heads):
+                    mean_of[h] = mean[:, j : j + 1]
+            if next_group is not None:
+                q_t = work.tile([P, GROUP, P], BF16, bufs=3)
+                nc.scalar.copy(
+                    out=q_t[:],
+                    in_=bank[:, 0:Q_WORDS].bitcast(BF16).rearrange("p (i q) -> p i q", i=GROUP),
+                )
+                q_t_of[next_group] = q_t
+            if heads:
+                nc.scalar.copy(out=stand_in[:, heads[0] : heads[-1] + 1], in_=mean[:])
+
+        def make_rows(h):
+            stand_in_rows = work.tile([P, SEQ], BF16)
+            nc.vector.tensor_scalar(
+                out=stand_in_rows[:], in0=masked_rows[:], scalar1=mean_of[h], scalar2=None, op0=ALU.mult
+            )
+            stand_in_rows_of[h] = stand_in_rows
+
+        def transpose_k(h, half, pool, tag):
+            in_psum[("k", half)] = features_to_partitions(
+                pool, tag, k_raw_of[h][:, half * GROUP : (half + 1) * GROUP, :]
+            )
+
+        def take_k(h, half):
+            keys = slice(half * BANK, (half + 1) * BANK)
+            nc.vector.tensor_tensor(
+                out=k_t[:, h, keys],
+                in0=in_psum[("k", half)][:].rearrange("p i s -> p (i s)"),
+                in1=stand_in_rows_of[h][:, keys],
+                op=ALU.add,
+            )
 
         v_grouped_of = {}
 
         def mask_and_group_v(h):
-            v_raw = v_raw_of[h]
-            v_grouped = work.tile([P, KEY_PASSES * HEAD_DIM * PACK], BF16, align_bytes=64)
+            v_grouped = work.tile([P, KEY_PASSES * HEAD_DIM * PACK], BF16, align_bytes=64, bufs=5)
             nc.gpsimd.tensor_tensor(
                 out=v_grouped[:].rearrange("p (g d w) -> p g d w", g=KEY_PASSES, w=PACK),
-                in0=v_raw[:].rearrange("p (g u) (e d) -> p g d (u e)", u=2, e=2),
+                in0=v_raw_of[h][:].rearrange("p (g u) (e d) -> p g d (u e)", u=2, e=2),
                 in1=ind_v_words[:]
                 .rearrange("p (g u) e -> p g (u e)", u=2)
                 .unsqueeze(2)
@@ -163,21 +255,18 @@ def tile_scaleddotproductattention_pa_kernel(
         WO_PIECES = 2 * FEATURE_PASSES
         wo_grouped_of = {}
 
-        def side_by_side(grouped, four_rows):
+        def group_wo(piece):
+            g, half = divmod(piece, 2)
+            cols = slice(half * BANK, (half + 1) * BANK)
+            wo_grouped = work.tile([P, BANK * PACK], BF16, align_bytes=64)
             nc.gpsimd.tensor_scalar(
-                out=grouped.rearrange("p (n i) -> p n i", i=PACK),
-                in0=four_rows.rearrange("p i n -> p n i"),
+                out=wo_grouped[:].rearrange("p (n i) -> p n i", i=PACK),
+                in0=wo_raw_of[g][:, :, cols].rearrange("p i n -> p n i"),
                 scalar1=1.0,
                 scalar2=0.0,
                 op0=ALU.mult,
                 op1=ALU.add,
             )
-
-        def group_wo(piece):
-            g, half = divmod(piece, 2)
-            cols = slice(half * BANK, (half + 1) * BANK)
-            wo_grouped = work.tile([P, BANK * PACK], BF16, align_bytes=64)
-            side_by_side(wo_grouped[:], wo_raw_of[g][:, :, cols])
             wo_grouped_of[piece] = wo_grouped
 
         def quantise_wo(piece):
@@ -188,98 +277,162 @@ def tile_scaleddotproductattention_pa_kernel(
             )
 
         scores_of = {}
-        weights_of = {}
+        maxima_of = {}
         neg_max_of = {}
+        weights_of = {}
         row_sum_of = {}
+        inv_sum_of = {}
         a_bf16_of = {}
+        flipped_of = {}
         a_grouped_of = {}
         a_mx_of = {}
+        o_t_of = {}
         c_grouped_of = {}
 
-        def masked_by_tensor(place):
-            return place % 6 == 5
-
         def scores(place):
-            h, t = tiles[place]
-            queries = slice(t * P, (t + 1) * P)
-            score_lo = score_psum.tile([P, BANK], F32)
-            score_hi = score_psum.tile([P, BANK], F32)
-            for score, keys in ((score_lo, slice(0, BANK)), (score_hi, slice(BANK, SEQ))):
+            h, queries = head_and_queries(place)
+            group, i = divmod(place, GROUP)
+            halves = []
+            for half in range(KEY_HALVES):
+                score = score_psum.tile([P, BANK], F32, tag="score")
                 nc.tensor.matmul(
-                    score[:], lhsT=q_t[:, h, queries], rhs=k_t[:, h, keys], start=True, stop=not masked_by_tensor(place)
+                    score[:],
+                    lhsT=q_t_of[group][:, i, :],
+                    rhs=k_t[:, h, half * BANK : (half + 1) * BANK],
+                    start=True,
+                    stop=True,
                 )
-                if masked_by_tensor(place):
-                    nc.tensor.matmul(score[:], lhsT=ident_bf16[:], rhs=mask_bias[:, keys], start=False, stop=True)
-            scores_of[place] = (score_lo, score_hi)
-
-        def scale_and_mask(place):
-            score_lo, score_hi = scores_of[place]
-            weights = work.tile([P, SEQ], F32, bufs=7)
-            for score, keys in ((score_lo, slice(0, BANK)), (score_hi, slice(BANK, SEQ))):
-                if masked_by_tensor(place):
-                    nc.scalar.activation(out=weights[:, keys], in_=score[:], func=ACT.Copy, scale=SCALE)
-                else:
-                    nc.vector.scalar_tensor_tensor(
-                        out=weights[:, keys], in0=score[:], scalar=SCALE, in1=mask_bias[:, keys], op0=ALU.mult, op1=ALU.add
-                    )
-            weights_of[place] = weights
+                halves.append(score)
+            scores_of[place] = halves
 
         def row_maximum(place):
+            maxima = stats.tile([P, KEY_HALVES], F32)
+            for half in range(KEY_HALVES):
+                nc.vector.tensor_reduce(
+                    out=maxima[:, half : half + 1],
+                    in_=scores_of[place][half][:],
+                    axis=mybir.AxisListType.X,
+                    op=ALU.max,
+                    negate=True,
+                )
+            maxima_of[place] = maxima
+
+        def join_maxima(place):
+            maxima = maxima_of[place]
             neg_max = stats.tile([P, 1], F32)
-            nc.vector.tensor_reduce(
-                out=neg_max[:], in_=weights_of[place][:], axis=mybir.AxisListType.X, op=ALU.max, negate=True
+            nc.vector.tensor_scalar(
+                out=neg_max[:], in0=maxima[:, 0:1], scalar1=maxima[:, 1:2], scalar2=SCALE, op0=ALU.min, op1=ALU.mult
             )
             neg_max_of[place] = neg_max
 
         def exponentials(place):
-            weights = weights_of[place]
-            row_sum = stats.tile([P, 1], F32)
+            group, i = divmod(place, GROUP)
+            stand_in_exp = stats.tile([P, 1], F32)
             nc.scalar.activation(
-                out=weights[:], in_=weights[:], func=ACT.Exp, bias=neg_max_of[place][:], scale=1.0, accum_out=row_sum[:]
+                out=stand_in_exp[:],
+                in_=stand_in_scores_of[group][:, i : i + 1],
+                func=ACT.Exp,
+                bias=neg_max_of[place][:],
+                scale=SCALE,
+            )
+            weights = work.tile([P, SEQ], F32, bufs=5)
+            sums = stats.tile([P, KEY_HALVES], F32)
+            for half in range(KEY_HALVES):
+                nc.scalar.activation(
+                    out=weights[:, half * BANK : (half + 1) * BANK],
+                    in_=scores_of[place][half][:],
+                    func=ACT.Exp,
+                    bias=neg_max_of[place][:],
+                    scale=SCALE,
+                    accum_out=sums[:, half : half + 1],
+                )
+            first_sum = stats.tile([P, 1], F32)
+            nc.scalar.activation(
+                out=first_sum[:], in_=stand_in_exp[:], func=ACT.Identity, scale=neg_masked[:], bias=sums[:, 0:1]
+            )
+            weights_of[place] = weights
+            row_sum_of[place] = (first_sum, sums)
+
+        def join_sums(place):
+            first_sum, sums = row_sum_of[place]
+            row_sum = stats.tile([P, 1], F32)
+            nc.vector.tensor_scalar(
+                out=row_sum[:], in0=first_sum[:], scalar1=sums[:, 1:2], scalar2=None, op0=ALU.add
             )
             row_sum_of[place] = row_sum
 
-        def normalise(place):
+        def invert_sum(place):
             inv_sum = stats.tile([P, 1], F32)
             nc.vector.reciprocal(out=inv_sum[:], in_=row_sum_of[place][:])
+            inv_sum_of[place] = inv_sum
+
+        def normaliser(place):
+            if place in AT_THE_END:
+                return AT_THE_END[place]
+            return "scalar" if place % GROUP in ON_SCALAR else "gpsimd"
+
+        def normalise(place):
             a_bf16 = work.tile([P, SEQ], BF16, bufs=4)
-            nc.gpsimd.tensor_scalar(
-                out=a_bf16[:], in0=weights_of[place][:], scalar1=inv_sum[:], scalar2=any_valid[:], op0=ALU.mult, op1=ALU.mult
-            )
+            weights = weights_of[place]
+            inv_sum = inv_sum_of[place]
+            if normaliser(place) == "gpsimd":
+                nc.gpsimd.tensor_scalar(
+                    out=a_bf16[:], in0=weights[:], scalar1=inv_sum[:], scalar2=1.0, op0=ALU.mult, op1=ALU.mult
+                )
+            elif normaliser(place) == "scalar":
+                nc.scalar.activation(out=a_bf16[:], in_=weights[:], func=ACT.Copy, scale=inv_sum[:])
+            else:
+                nc.vector.tensor_scalar(out=a_bf16[:], in0=weights[:], scalar1=inv_sum[:], scalar2=None, op0=ALU.mult)
             a_bf16_of[place] = a_bf16
 
         def keys_to_partitions(place):
             a_words = a_bf16_of[place][:].bitcast(F32)
-            flipped = flip_psum.tile([P, 2 * KEY_PASSES, P], F32, tag="flipped")
-            for c in range(2 * KEY_PASSES):
-                nc.tensor.transpose(flipped[:, c, :], a_words[:, c * P : (c + 1) * P], ident_f32[:])
+            flipped = score_psum.tile([P, 2, KEY_PASSES * P], F32, tag="score")
+            for g in range(KEY_PASSES):
+                for u in range(2):
+                    c = 2 * g + u
+                    nc.tensor.transpose(
+                        flipped[:, u, g * P : (g + 1) * P], a_words[:, c * P : (c + 1) * P], ident_f32[:]
+                    )
+            flipped_of[place] = flipped
+
+        def mask_weights(place, g):
             group, i = divmod(place, GROUP)
-            if i == 0:
+            half = slice(g * P, (g + 1) * P)
+            values = slice(g * P * PACK, (g + 1) * P * PACK)
+            if i == 0 and g == 0:
                 a_grouped = work.tile([P, GROUP, KEY_PASSES * P * PACK], BF16, align_bytes=64)
                 a_grouped_of[group] = a_grouped
-            nc.scalar.copy(
-                out=a_grouped_of[group][:, i, :].bitcast(F32).rearrange("p (g q u) -> p g q u", g=KEY_PASSES, u=2),
-                in_=flipped[:].rearrange("p (g u) q -> p g q u", u=2),
+            nc.vector.tensor_tensor(
+                out=a_grouped_of[group][:, i, values].rearrange("p (x u e) -> p x u e", u=2, e=2),
+                in0=flipped_of[place][:, :, half].bitcast(BF16).rearrange("p u (x e) -> p x u e", e=2),
+                in1=key_mask[:].rearrange("p g q (u e) -> p g q u e", u=2)[:, g, :, :, :],
+                op=ALU.mult,
             )
 
-        def quantise_weights(group):
-            a_codes = work.tile([P, GROUP, KEY_PASSES * P], U32, align_bytes=64)
-            a_scales = work.tile([P, GROUP, KEY_PASSES * P], U8, align_bytes=64)
-            nc.vector.quantize_mx(
-                out=a_codes[:].rearrange("p i w -> p (i w)").bitcast(FP8X4),
-                scales=a_scales[:].rearrange("p i w -> p (i w)"),
-                in_=a_grouped_of[group][:].rearrange("p i w -> p (i w)"),
-            )
-            a_mx_of[group] = (a_codes, a_scales)
-
-        def weighted_values(group):
+        def quantise_weights(group, first, last):
+            if first == 0:
+                a_codes = work.tile([P, GROUP, KEY_PASSES * P], U32, align_bytes=64)
+                a_scales = work.tile([P, GROUP, KEY_PASSES * P], U8, align_bytes=64)
+                a_mx_of[group] = (a_codes, a_scales)
             a_codes, a_scales = a_mx_of[group]
-            o_t = acc_psum.tile([P, GROUP, P], F32, tag="acc")
-            for i, (h, t) in enumerate(groups[group]):
+            nc.vector.quantize_mx(
+                out=a_codes[:, first:last, :].rearrange("p i w -> p (i w)").bitcast(FP8X4),
+                scales=a_scales[:, first:last, :].rearrange("p i w -> p (i w)"),
+                in_=a_grouped_of[group][:, first:last, :].rearrange("p i w -> p (i w)"),
+            )
+
+        def weighted_values(group, first, last):
+            if first == 0:
+                o_t = score_psum.tile([P, GROUP, P], F32, tag="score", name="o_t")
+                o_t_of[group] = o_t
+            a_codes, a_scales = a_mx_of[group]
+            for i in range(first, last):
+                h, queries = head_and_queries(group * GROUP + i)
                 for g in range(KEY_PASSES):
                     block = slice(g * P, (g + 1) * P)
                     nc.tensor.matmul_mx(
-                        out=o_t[:, i, :],
+                        out=o_t_of[group][:, i, :],
                         lhsT=v_codes[:, h, block].bitcast(FP8X4),
                         lhsT_scale=v_scales[:, h, block],
                         rhs=a_codes[:, i, block].bitcast(FP8X4),
@@ -287,123 +440,191 @@ def tile_scaleddotproductattention_pa_kernel(
                         start=(g == 0),
                         stop=(g == KEY_PASSES - 1),
                     )
-            if one_head(group):
-                nc.scalar.copy(out=group_view(c_early, group), in_=o_t[:])
-            else:
-                c_grouped = work.tile([P, P * PACK], BF16, align_bytes=64, tag="c_grouped_late")
-                nc.scalar.copy(
-                    out=c_grouped[:].rearrange("p (q i) -> p q i", i=PACK), in_=o_t[:].rearrange("p i q -> p q i")
-                )
-                c_grouped_of[group] = c_grouped
 
-        def group_early_heads(g):
-            c_grouped = work.tile([P, EARLY_QUERIES * PACK], BF16, align_bytes=64, tag="c_grouped_early")
-            side_by_side(c_grouped[:], c_early[:, g * GROUP : (g + 1) * GROUP, :])
-            c_grouped_of[("early", g)] = c_grouped
+        def take_values(group):
+            c_grouped = work.tile([P, P * PACK], BF16, align_bytes=64)
+            nc.scalar.copy(
+                out=c_grouped[:].rearrange("p (q i) -> p q i", i=PACK),
+                in_=o_t_of[group][:].rearrange("p i q -> p q i"),
+            )
+            c_grouped_of[group] = c_grouped
 
-        def quantise_heads(g, queries, c_grouped):
+        def quantise_heads(group):
+            g, t = groups[group]
+            queries = slice(t * P, (t + 1) * P)
             nc.vector.quantize_mx(
-                out=c_codes[:, g, queries].bitcast(FP8X4), scales=c_scales[:, g, queries], in_=c_grouped[:]
+                out=c_codes[:, g, queries].bitcast(FP8X4), scales=c_scales[:, g, queries], in_=c_grouped_of[group][:]
             )
 
-        def project(t, vector_helps):
+        def project(t, half, pool, tag):
             queries = slice(t * P, (t + 1) * P)
-            result = work.tile([P, D_OUT], F32, bufs=3)
-            for half in range(D_OUT // BANK):
-                cols = slice(half * BANK, (half + 1) * BANK)
-                acc = acc_psum.tile([P, BANK], F32, tag="acc")
-                for g in range(FEATURE_PASSES):
-                    nc.tensor.matmul_mx(
-                        out=acc[:],
-                        lhsT=c_codes[:, g, queries].bitcast(FP8X4),
-                        lhsT_scale=c_scales[:, g, queries],
-                        rhs=wo_codes[:, g, cols].bitcast(FP8X4),
-                        rhs_scale=wo_scales[:, g, cols],
-                        start=(g == 0),
-                        stop=(g == FEATURE_PASSES - 1),
-                    )
-                if vector_helps and half == 1:
-                    nc.vector.tensor_copy(out=result[:, cols], in_=acc[:])
-                else:
-                    nc.scalar.copy(out=result[:, cols], in_=acc[:])
-            nc.sync.dma_start(out=out[0, queries, :], in_=result[:])
+            cols = slice(half * BANK, (half + 1) * BANK)
+            acc = pool.tile([P, BANK], F32, tag=tag, name="acc")
+            for g in range(FEATURE_PASSES):
+                nc.tensor.matmul_mx(
+                    out=acc[:],
+                    lhsT=c_codes[:, g, queries].bitcast(FP8X4),
+                    lhsT_scale=c_scales[:, g, queries],
+                    rhs=wo_codes[:, g, cols].bitcast(FP8X4),
+                    rhs_scale=wo_scales[:, g, cols],
+                    start=(g == 0),
+                    stop=(g == FEATURE_PASSES - 1),
+                )
+            in_psum[("out", t, half)] = acc
 
-        def prepare_on_gpsimd(group):
-            if group + 1 < HEADS:
-                mask_and_group_v(group + 1)
-            elif group == HEADS - 1:
-                group_early_heads(0)
-            elif group - HEADS < WO_PIECES:
-                group_wo(group - HEADS)
-            elif group - HEADS == WO_PIECES:
-                group_early_heads(1)
+        def take_result(t, half, on_vector):
+            queries = slice(t * P, (t + 1) * P)
+            cols = slice(half * BANK, (half + 1) * BANK)
+            result = work.tile([P, BANK], F32, bufs=4)
+            if on_vector:
+                nc.vector.tensor_copy(out=result[:], in_=in_psum[("out", t, half)][:])
+            else:
+                nc.scalar.copy(out=result[:], in_=in_psum[("out", t, half)][:])
+            nc.sync.dma_start(out=out[0, queries, cols], in_=result[:])
 
-        def quantise_prepared(group):
-            if group + 1 < HEADS:
-                quantise_v(group + 1)
-            elif group == HEADS - 1:
-                quantise_heads(0, slice(0, EARLY_QUERIES), c_grouped_of[("early", 0)])
-            elif group - HEADS < WO_PIECES:
-                quantise_wo(group - HEADS)
-            elif group - HEADS == WO_PIECES:
-                quantise_heads(1, slice(0, EARLY_QUERIES), c_grouped_of[("early", 1)])
 
-        transpose_q(0)
-        transpose_k(0, 0)
-        transpose_k(0, 1)
-        prepare_on_gpsimd(-1)
-
-        EARLY_PROJECT_STEP = (HEADS + WO_PIECES + 2) * GROUP + 2
-        LAST_LAG = 14
+        prepared_in = {}
+        for h in range(GROUP, HEADS):
+            prepared_in[h - GROUP] = (mask_and_group_v, quantise_v, h)
+        for piece in range(WO_PIECES):
+            prepared_in[GROUP + piece] = (group_wo, quantise_wo, piece)
 
         def entered(step, lag):
-            return step - lag if 0 <= step - lag < len(tiles) else None
+            return step - lag if 0 <= step - lag < END else None
 
-        def closes_group(place):
-            return place is not None and place % GROUP == GROUP - 1
+        def closed_group(step, lag):
+            place = entered(step, lag)
+            return place // GROUP if place is not None and place % GROUP == GROUP - 1 else None
 
-        for step in range(len(tiles) + LAST_LAG + 1):
+        def prepare_k(h):
+            make_rows(h)
+            for half in range(KEY_HALVES):
+                transpose_k(h, half, score_psum, "score")
+            for half in range(KEY_HALVES):
+                take_k(h, half)
+
+        small_products(0, [0], None)
+        take_small_products(0, [0], None)
+        small_products(None, [1], None)
+        take_small_products(None, [1], None)
+        prepare_k(0)
+        prepare_k(1)
+        for h in range(GROUP):
+            mask_and_group_v(h)
+
+        taken_next = []
+
+        for step in range(END + 8):
+            take_now, taken_next = taken_next, []
+            group, i = divmod(step, GROUP)
+            following = group + 1 if group < LAST else None
+
+            def tensor_side_jobs():
+                if i == 0 and 0 < step < END:
+                    heads = [GROUP + group - 1] if GROUP + group - 1 < HEADS else []
+                    small_products(following, heads, group)
+                    taken_next.append((take_small_products, (following, heads, group)))
+                if step == 1:
+                    small_products(None, [], 0)
+                    taken_next.append((take_small_products, (None, [], 0)))
+                h = GROUP + group - 1
+                if i in (2, 3) and GROUP <= h < HEADS:
+                    if i == 2:
+                        make_rows(h)
+                    transpose_k(h, i - 2, score_psum, "score")
+                    taken_next.append((take_k, (h, i - 2)))
+                if closed_group(step, 10) is not None and closed_group(step, 10) < LAST - 1:
+                    weighted_values(closed_group(step, 10), 0, GROUP)
+                    taken_next.append((take_values, (closed_group(step, 10),)))
+                for half in range(2):
+                    done = closed_group(step, 15 + half)
+                    if done is not None and done < LAST - 1 and groups[done][0] == FEATURE_PASSES - 1:
+                        t = groups[done][1]
+                        project(t, half, score_psum, "score")
+                        taken_next.append((take_result, (t, half, False)))
+
             if entered(step, 0) is not None:
-                scores(entered(step, 0))
+                scores(step)
+            if step == 0:
+                small_products(1, [2, 3], None)
+                take_small_products(1, [2, 3], None)
+            if step < END:
+                tensor_side_jobs()
+            if entered(step, FLIP_LAG) is not None:
+                keys_to_partitions(step - FLIP_LAG)
+
             if entered(step, 1) is not None:
-                scale_and_mask(entered(step, 1))
-            if entered(step, 2) is not None:
-                row_maximum(entered(step, 2))
-            if entered(step, 3) is not None:
-                exponentials(entered(step, 3))
-            if entered(step, 5) is not None:
-                normalise(entered(step, 5))
-            if entered(step, 7) is not None:
-                keys_to_partitions(entered(step, 7))
-            if closes_group(entered(step, 8)):
-                quantise_weights(entered(step, 8) // GROUP)
-            if closes_group(entered(step, 10)):
-                weighted_values(entered(step, 10) // GROUP)
-            if closes_group(entered(step, 12)):
-                group = entered(step, 12) // GROUP
-                h, t = groups[group][0]
-                if not one_head(group):
-                    quantise_heads(h // GROUP, slice(t * P, (t + 1) * P), c_grouped_of[group])
-            if closes_group(entered(step, LAST_LAG)):
-                h, t = tiles[entered(step, LAST_LAG)]
-                if t >= EARLY_Q_TILES and h == HEADS - 1:
-                    project(t, vector_helps=step > len(tiles))
-            if step >= EARLY_PROJECT_STEP and (step - EARLY_PROJECT_STEP) % GROUP == 0:
-                if (step - EARLY_PROJECT_STEP) // GROUP < EARLY_Q_TILES:
-                    project((step - EARLY_PROJECT_STEP) // GROUP, vector_helps=step > len(tiles))
+                row_maximum(step - 1)
+            for take, args in take_now:
+                if take is take_k:
+                    take(*args)
+            if 1 <= step < GROUP - 1:
+                prepare_k(step + 1)
+            if step == GROUP - 1:
+                build_key_mask()
+            if entered(step, NORM_LAG) is not None:
+                join_sums(step - NORM_LAG)
+            if entered(step, MASK_LAG) is not None:
+                mask_weights(step - MASK_LAG, 0)
+            if entered(step, 1) is not None:
+                join_maxima(step - 1)
+            if entered(step, MASK_LAG) is not None:
+                mask_weights(step - MASK_LAG, 1)
+            if entered(step, NORM_LAG) is not None:
+                invert_sum(step - NORM_LAG)
+                if normaliser(step - NORM_LAG) != "scalar":
+                    normalise(step - NORM_LAG)
+            if closed_group(step, 12) is not None and closed_group(step, 12) < LAST - 1:
+                quantise_heads(closed_group(step, 12))
+            if closed_group(step, 8) is not None and closed_group(step, 8) != LAST:
+                quantise_weights(closed_group(step, 8), 0, GROUP)
+            if step == 7:
+                for h in range(GROUP):
+                    quantise_v(h)
+            if closed_group(step, 0) is not None and group - 1 in prepared_in:
+                lay_out, quantise, what = prepared_in[group - 1]
+                quantise(what)
 
-            if entered(step, 0) is not None:
-                group, i = divmod(entered(step, 0), GROUP)
-                if i == 0 and group + 2 < len(groups):
-                    load_q(group + 2)
-                    if one_head(group + 2):
-                        load_k_and_v(group + 2)
-                if i == 0 and group + 1 < len(groups):
-                    transpose_q(group + 1)
-                if i in (1, 2) and one_head(group + 1):
-                    transpose_k(group + 1, i - 1)
-                if i == 0 and HEADS - FEATURE_PASSES <= group < HEADS:
-                    load_wo(group - (HEADS - FEATURE_PASSES))
-                if i == GROUP - 1:
-                    quantise_prepared(group - 1)
-                    prepare_on_gpsimd(group)
+            for take, args in take_now:
+                if take is not take_k:
+                    take(*args)
+            if entered(step, 2) is not None:
+                exponentials(step - 2)
+            if entered(step, NORM_LAG) is not None and normaliser(step - NORM_LAG) == "scalar":
+                normalise(step - NORM_LAG)
+
+            if entered(step, 8) is not None and (step - 8) // GROUP == LAST:
+                j = (step - 8) % GROUP
+                quantise_weights(LAST, j, j + 1)
+                if j == 0:
+                    weighted_values(LAST - 1, 0, GROUP)
+                    take_values(LAST - 1)
+                weighted_values(LAST, j, j + 1)
+                if j == GROUP - 1:
+                    quantise_heads(LAST - 1)
+                    take_values(LAST)
+                    quantise_heads(LAST)
+            if step >= END:
+                tensor_side_jobs()
+            if step == END + 7:
+                for half in range(2):
+                    project(groups[LAST - 1][1], half, score_psum, "score")
+                    taken_next.append((take_result, (groups[LAST - 1][1], half, half == 0)))
+                for take, args in taken_next:
+                    take(*args)
+                for half in range(2):
+                    project(groups[LAST][1], half, score_psum, "score")
+                for half in range(2):
+                    take_result(groups[LAST][1], half, half == 0)
+
+            if i == 0 and group + 2 < len(groups):
+                load_q(group + 2)
+            if i == 0 and GROUP <= GROUP + group < HEADS:
+                load_k(GROUP + group)
+            if i == 1 and GROUP <= GROUP + group < HEADS:
+                load_v(GROUP + group)
+            if i == 0 and group - 3 in range(FEATURE_PASSES):
+                load_wo(group - 3)
+            if closed_group(step, 0) is not None and group in prepared_in:
+                lay_out, quantise, what = prepared_in[group]
+                lay_out(what)

@@ -29,6 +29,7 @@ KEY_HALVES = SEQ // BANK
 
 SCALE = 1.0 / math.sqrt(HEAD_DIM)
 SCORE_BANKS = 8
+MASKED_SCORE = -1.0e30
 
 FLOPS = 3 * 2 * SEQ * SEQ * HEADS * HEAD_DIM
 
@@ -51,10 +52,21 @@ def tile_scaleddotproductattention_pa_kernel(
 
         LAST = len(groups) - 1
         ON_SCALAR = ()
+        FOLDED = ()
+        FOLD_FROM = 4
+        SCALAR_FROM = 0
+        SCALAR_TO = 8
         AT_THE_END = {END - 3: "vector", END - 2: "scalar", END - 1: "vector"}
         NORM_LAG = 4
-        FLIP_LAG = 6
-        MASK_LAG = 7
+        PAIR = 2
+        QUANT_LAG = 8
+        AT_ONCE = 4
+        MASK_EVERY = 0
+        V_ON_GPSIMD = 2
+        V_STEP = 3
+        V_QUANT_STEP = 7
+        FLIP_LAG = 7
+        MASK_LAG = 8
 
         def head_and_queries(place):
             group, i = divmod(place, GROUP)
@@ -120,6 +132,10 @@ def tile_scaleddotproductattention_pa_kernel(
         make_identity(nc, ident_bf16[:])
         ident_f32 = const.tile([P, P], F32)
         make_identity(nc, ident_f32[:])
+        neg_ident = const.tile([P, P], BF16)
+        nc.gpsimd.tensor_scalar(
+            out=neg_ident[:], in0=ident_bf16[:], scalar1=MASKED_SCORE, scalar2=1.0, op0=ALU.mult, op1=ALU.mult
+        )
         valid_keys = const.tile([P, 1], F32)
         nc.vector.reduce_sum(out=valid_keys[:], in_=ind_k_rows[:], axis=mybir.AxisListType.X)
         inv_valid = const.tile([P, 1], F32)
@@ -234,9 +250,9 @@ def tile_scaleddotproductattention_pa_kernel(
 
         v_grouped_of = {}
 
-        def mask_and_group_v(h):
+        def mask_and_group_v(h, engine=nc.gpsimd):
             v_grouped = work.tile([P, KEY_PASSES * HEAD_DIM * PACK], BF16, align_bytes=64, bufs=5)
-            nc.gpsimd.tensor_tensor(
+            engine.tensor_tensor(
                 out=v_grouped[:].rearrange("p (g d w) -> p g d w", g=KEY_PASSES, w=PACK),
                 in0=v_raw_of[h][:].rearrange("p (g u) (e d) -> p g d (u e)", u=2, e=2),
                 in1=ind_v_words[:]
@@ -289,6 +305,9 @@ def tile_scaleddotproductattention_pa_kernel(
         o_t_of = {}
         c_grouped_of = {}
 
+        def masked_by_tensor(place):
+            return MASK_EVERY > 0 and place % MASK_EVERY == MASK_EVERY - 1
+
         def scores(place):
             h, queries = head_and_queries(place)
             group, i = divmod(place, GROUP)
@@ -300,12 +319,23 @@ def tile_scaleddotproductattention_pa_kernel(
                     lhsT=q_t_of[group][:, i, :],
                     rhs=k_t[:, h, half * BANK : (half + 1) * BANK],
                     start=True,
-                    stop=True,
+                    stop=not masked_by_tensor(place),
                 )
+                if masked_by_tensor(place):
+                    nc.tensor.matmul(
+                        score[:],
+                        lhsT=neg_ident[:],
+                        rhs=masked_rows[:, half * BANK : (half + 1) * BANK],
+                        start=False,
+                        stop=True,
+                    )
                 halves.append(score)
             scores_of[place] = halves
 
         def row_maximum(place):
+            if folded(place):
+                fold(place)
+                return
             maxima = stats.tile([P, KEY_HALVES], F32)
             for half in range(KEY_HALVES):
                 nc.vector.tensor_reduce(
@@ -317,7 +347,42 @@ def tile_scaleddotproductattention_pa_kernel(
                 )
             maxima_of[place] = maxima
 
+        hi_bf16_of = {}
+        folded_of = {}
+
+        def folded(place):
+            return place % GROUP in FOLDED and FOLD_FROM <= place < END - 1
+
+        def copy_hi(place):
+            hi_bf16 = work.tile([P, BANK], BF16)
+            nc.scalar.copy(out=hi_bf16[:], in_=scores_of[place][1][:])
+            hi_bf16_of[place] = hi_bf16
+
+        def fold(place):
+            fold_bf16 = work.tile([P, BANK], BF16)
+            nc.vector.tensor_tensor(
+                out=fold_bf16[:], in0=scores_of[place][0][:], in1=hi_bf16_of[place][:], op=ALU.max
+            )
+            folded_of[place] = fold_bf16
+
+        def fold_maximum(place):
+            neg_max = stats.tile([P, 1], F32)
+            scrap = work.tile([P, BANK], BF16)
+            nc.vector.tensor_scalar(
+                out=scrap[:],
+                in0=folded_of[place][:],
+                scalar1=-SCALE,
+                scalar2=None,
+                op0=ALU.mult,
+                op1=ALU.min,
+                accum_out=neg_max[:],
+            )
+            neg_max_of[place] = neg_max
+
         def join_maxima(place):
+            if folded(place):
+                fold_maximum(place)
+                return
             maxima = maxima_of[place]
             neg_max = stats.tile([P, 1], F32)
             nc.vector.tensor_scalar(
@@ -327,14 +392,15 @@ def tile_scaleddotproductattention_pa_kernel(
 
         def exponentials(place):
             group, i = divmod(place, GROUP)
-            stand_in_exp = stats.tile([P, 1], F32)
-            nc.scalar.activation(
-                out=stand_in_exp[:],
-                in_=stand_in_scores_of[group][:, i : i + 1],
-                func=ACT.Exp,
-                bias=neg_max_of[place][:],
-                scale=SCALE,
-            )
+            if not masked_by_tensor(place):
+                stand_in_exp = stats.tile([P, 1], F32)
+                nc.scalar.activation(
+                    out=stand_in_exp[:],
+                    in_=stand_in_scores_of[group][:, i : i + 1],
+                    func=ACT.Exp,
+                    bias=neg_max_of[place][:],
+                    scale=SCALE,
+                )
             weights = work.tile([P, SEQ], F32, bufs=5)
             sums = stats.tile([P, KEY_HALVES], F32)
             for half in range(KEY_HALVES):
@@ -346,43 +412,51 @@ def tile_scaleddotproductattention_pa_kernel(
                     scale=SCALE,
                     accum_out=sums[:, half : half + 1],
                 )
+            weights_of[place] = weights
+            if masked_by_tensor(place):
+                sums_of[place] = (sums[:, 0:1], sums)
+                return
             first_sum = stats.tile([P, 1], F32)
             nc.scalar.activation(
                 out=first_sum[:], in_=stand_in_exp[:], func=ACT.Identity, scale=neg_masked[:], bias=sums[:, 0:1]
             )
-            weights_of[place] = weights
-            row_sum_of[place] = (first_sum, sums)
+            sums_of[place] = (first_sum[:], sums)
+
+        sums_of = {}
 
         def join_sums(place):
-            first_sum, sums = row_sum_of[place]
-            row_sum = stats.tile([P, 1], F32)
-            nc.vector.tensor_scalar(
-                out=row_sum[:], in0=first_sum[:], scalar1=sums[:, 1:2], scalar2=None, op0=ALU.add
+            first_sum, sums = sums_of[place]
+            j = place % PAIR
+            if j == 0:
+                row_sums = stats.tile([P, PAIR], F32)
+                row_sum_of[place // PAIR] = row_sums
+            nc.scalar.activation(
+                out=row_sum_of[place // PAIR][:, j : j + 1], in_=first_sum, func=ACT.Identity, bias=sums[:, 1:2]
             )
-            row_sum_of[place] = row_sum
 
-        def invert_sum(place):
-            inv_sum = stats.tile([P, 1], F32)
-            nc.vector.reciprocal(out=inv_sum[:], in_=row_sum_of[place][:])
-            inv_sum_of[place] = inv_sum
+        def invert_sums(pair):
+            inv_sums = stats.tile([P, PAIR], F32)
+            nc.vector.reciprocal(out=inv_sums[:], in_=row_sum_of[pair][:])
+            inv_sum_of[pair] = inv_sums
 
         def normaliser(place):
             if place in AT_THE_END:
                 return AT_THE_END[place]
-            return "scalar" if place % GROUP in ON_SCALAR else "gpsimd"
+            return "scalar" if place % GROUP in ON_SCALAR and place // GROUP in range(SCALAR_FROM, SCALAR_TO) else "gpsimd"
 
         def normalise(place):
             a_bf16 = work.tile([P, SEQ], BF16, bufs=4)
             weights = weights_of[place]
-            inv_sum = inv_sum_of[place]
+            j = place % PAIR
+            inv_sum = inv_sum_of[place // PAIR][:, j : j + 1]
             if normaliser(place) == "gpsimd":
                 nc.gpsimd.tensor_scalar(
-                    out=a_bf16[:], in0=weights[:], scalar1=inv_sum[:], scalar2=1.0, op0=ALU.mult, op1=ALU.mult
+                    out=a_bf16[:], in0=weights[:], scalar1=inv_sum, scalar2=any_valid[:], op0=ALU.mult, op1=ALU.mult
                 )
             elif normaliser(place) == "scalar":
-                nc.scalar.activation(out=a_bf16[:], in_=weights[:], func=ACT.Copy, scale=inv_sum[:])
+                nc.scalar.activation(out=a_bf16[:], in_=weights[:], func=ACT.Copy, scale=inv_sum)
             else:
-                nc.vector.tensor_scalar(out=a_bf16[:], in0=weights[:], scalar1=inv_sum[:], scalar2=None, op0=ALU.mult)
+                nc.vector.tensor_scalar(out=a_bf16[:], in0=weights[:], scalar1=inv_sum, scalar2=None, op0=ALU.mult)
             a_bf16_of[place] = a_bf16
 
         def keys_to_partitions(place):
@@ -396,17 +470,21 @@ def tile_scaleddotproductattention_pa_kernel(
                     )
             flipped_of[place] = flipped
 
-        def mask_weights(place, g):
+        def mask_weights(place):
             group, i = divmod(place, GROUP)
-            half = slice(g * P, (g + 1) * P)
-            values = slice(g * P * PACK, (g + 1) * P * PACK)
-            if i == 0 and g == 0:
+            if i == 0:
                 a_grouped = work.tile([P, GROUP, KEY_PASSES * P * PACK], BF16, align_bytes=64)
                 a_grouped_of[group] = a_grouped
+            if masked_by_tensor(place):
+                nc.scalar.copy(
+                    out=a_grouped_of[group][:, i, :].bitcast(F32).rearrange("p (x u) -> p x u", u=2),
+                    in_=flipped_of[place][:].rearrange("p u x -> p x u"),
+                )
+                return
             nc.vector.tensor_tensor(
-                out=a_grouped_of[group][:, i, values].rearrange("p (x u e) -> p x u e", u=2, e=2),
-                in0=flipped_of[place][:, :, half].bitcast(BF16).rearrange("p u (x e) -> p x u e", e=2),
-                in1=key_mask[:].rearrange("p g q (u e) -> p g q u e", u=2)[:, g, :, :, :],
+                out=a_grouped_of[group][:, i, :].rearrange("p (x u e) -> p x u e", u=2, e=2),
+                in0=flipped_of[place][:].bitcast(BF16).rearrange("p u (x e) -> p x u e", e=2),
+                in1=key_mask[:].rearrange("p g q (u e) -> p (g q) u e", u=2),
                 op=ALU.mult,
             )
 
@@ -509,12 +587,12 @@ def tile_scaleddotproductattention_pa_kernel(
         take_small_products(None, [1], None)
         prepare_k(0)
         prepare_k(1)
-        for h in range(GROUP):
+        for h in range(V_ON_GPSIMD):
             mask_and_group_v(h)
 
         taken_next = []
 
-        for step in range(END + 8):
+        for step in range(END + QUANT_LAG):
             take_now, taken_next = taken_next, []
             group, i = divmod(step, GROUP)
             following = group + 1 if group < LAST else None
@@ -533,11 +611,11 @@ def tile_scaleddotproductattention_pa_kernel(
                         make_rows(h)
                     transpose_k(h, i - 2, score_psum, "score")
                     taken_next.append((take_k, (h, i - 2)))
-                if closed_group(step, 10) is not None and closed_group(step, 10) < LAST - 1:
-                    weighted_values(closed_group(step, 10), 0, GROUP)
-                    taken_next.append((take_values, (closed_group(step, 10),)))
+                if closed_group(step, QUANT_LAG + 2) is not None and closed_group(step, QUANT_LAG + 2) < LAST - 1:
+                    weighted_values(closed_group(step, QUANT_LAG + 2), 0, GROUP)
+                    taken_next.append((take_values, (closed_group(step, QUANT_LAG + 2),)))
                 for half in range(2):
-                    done = closed_group(step, 15 + half)
+                    done = closed_group(step, QUANT_LAG + 7 + half)
                     if done is not None and done < LAST - 1 and groups[done][0] == FEATURE_PASSES - 1:
                         t = groups[done][1]
                         project(t, half, score_psum, "score")
@@ -553,6 +631,8 @@ def tile_scaleddotproductattention_pa_kernel(
             if entered(step, FLIP_LAG) is not None:
                 keys_to_partitions(step - FLIP_LAG)
 
+            if entered(step, 3) is not None:
+                join_sums(step - 3)
             if entered(step, 1) is not None:
                 row_maximum(step - 1)
             for take, args in take_now:
@@ -562,23 +642,26 @@ def tile_scaleddotproductattention_pa_kernel(
                 prepare_k(step + 1)
             if step == GROUP - 1:
                 build_key_mask()
-            if entered(step, NORM_LAG) is not None:
-                join_sums(step - NORM_LAG)
+            h = step - V_STEP + V_ON_GPSIMD
+            if V_ON_GPSIMD <= h < GROUP:
+                mask_and_group_v(h, nc.vector)
             if entered(step, MASK_LAG) is not None:
-                mask_weights(step - MASK_LAG, 0)
+                mask_weights(step - MASK_LAG)
             if entered(step, 1) is not None:
                 join_maxima(step - 1)
-            if entered(step, MASK_LAG) is not None:
-                mask_weights(step - MASK_LAG, 1)
-            if entered(step, NORM_LAG) is not None:
-                invert_sum(step - NORM_LAG)
-                if normaliser(step - NORM_LAG) != "scalar":
-                    normalise(step - NORM_LAG)
-            if closed_group(step, 12) is not None and closed_group(step, 12) < LAST - 1:
-                quantise_heads(closed_group(step, 12))
-            if closed_group(step, 8) is not None and closed_group(step, 8) != LAST:
-                quantise_weights(closed_group(step, 8), 0, GROUP)
-            if step == 7:
+            inverted = []
+            if entered(step, NORM_LAG) is not None and step % PAIR == (NORM_LAG + PAIR - 1) % PAIR:
+                invert_sums((step - NORM_LAG) // PAIR)
+                inverted = [step - NORM_LAG - PAIR + 1 + j for j in range(PAIR)]
+                for place in inverted:
+                    if normaliser(place) != "scalar":
+                        normalise(place)
+            if closed_group(step, QUANT_LAG + 4) is not None and closed_group(step, QUANT_LAG + 4) < LAST - 1:
+                quantise_heads(closed_group(step, QUANT_LAG + 4))
+            place = entered(step, QUANT_LAG)
+            if place is not None and place // GROUP != LAST and (place + 1) % AT_ONCE == 0:
+                quantise_weights(place // GROUP, place % GROUP + 1 - AT_ONCE, place % GROUP + 1)
+            if step == V_QUANT_STEP:
                 for h in range(GROUP):
                     quantise_v(h)
             if closed_group(step, 0) is not None and group - 1 in prepared_in:
@@ -590,11 +673,14 @@ def tile_scaleddotproductattention_pa_kernel(
                     take(*args)
             if entered(step, 2) is not None:
                 exponentials(step - 2)
-            if entered(step, NORM_LAG) is not None and normaliser(step - NORM_LAG) == "scalar":
-                normalise(step - NORM_LAG)
+            if entered(step, 0) is not None and folded(step):
+                copy_hi(step)
+            for place in inverted:
+                if normaliser(place) == "scalar":
+                    normalise(place)
 
-            if entered(step, 8) is not None and (step - 8) // GROUP == LAST:
-                j = (step - 8) % GROUP
+            if entered(step, QUANT_LAG) is not None and (step - QUANT_LAG) // GROUP == LAST:
+                j = (step - QUANT_LAG) % GROUP
                 quantise_weights(LAST, j, j + 1)
                 if j == 0:
                     weighted_values(LAST - 1, 0, GROUP)
@@ -606,7 +692,7 @@ def tile_scaleddotproductattention_pa_kernel(
                     quantise_heads(LAST)
             if step >= END:
                 tensor_side_jobs()
-            if step == END + 7:
+            if step == END - 1 + QUANT_LAG:
                 for half in range(2):
                     project(groups[LAST - 1][1], half, score_psum, "score")
                     taken_next.append((take_result, (groups[LAST - 1][1], half, half == 0)))

@@ -61,7 +61,12 @@ def tile_scaleddotproductattention_pa_kernel(
         PAIR = 2
         QUANT_LAG = 8
         AT_ONCE = 4
-        MASK_EVERY = 0
+        V_ORDER = "RKEJNQ"
+        V_ORDER_CLOSING = "RKEJQN"
+        MASK_I = 3
+        MASK_FROM = 0
+        MASK_TO = 10
+        COPY_LATE = 0
         V_ON_GPSIMD = 2
         V_STEP = 3
         V_QUANT_STEP = 7
@@ -306,7 +311,7 @@ def tile_scaleddotproductattention_pa_kernel(
         c_grouped_of = {}
 
         def masked_by_tensor(place):
-            return MASK_EVERY > 0 and place % MASK_EVERY == MASK_EVERY - 1
+            return place % GROUP == MASK_I and MASK_FROM <= place // GROUP < MASK_TO
 
         def scores(place):
             h, queries = head_and_queries(place)
@@ -351,7 +356,7 @@ def tile_scaleddotproductattention_pa_kernel(
         folded_of = {}
 
         def folded(place):
-            return place % GROUP in FOLDED and FOLD_FROM <= place < END - 1
+            return place % GROUP in FOLDED and FOLD_FROM <= place < END - 1 and not masked_by_tensor(place)
 
         def copy_hi(place):
             hi_bf16 = work.tile([P, BANK], BF16)
@@ -553,7 +558,7 @@ def tile_scaleddotproductattention_pa_kernel(
         def take_result(t, half, on_vector):
             queries = slice(t * P, (t + 1) * P)
             cols = slice(half * BANK, (half + 1) * BANK)
-            result = work.tile([P, BANK], F32, bufs=4)
+            result = work.tile([P, BANK], F32, bufs=8)
             if on_vector:
                 nc.vector.tensor_copy(out=result[:], in_=in_psum[("out", t, half)][:])
             else:
@@ -633,40 +638,56 @@ def tile_scaleddotproductattention_pa_kernel(
 
             if entered(step, 3) is not None:
                 join_sums(step - 3)
-            if entered(step, 1) is not None:
-                row_maximum(step - 1)
-            for take, args in take_now:
-                if take is take_k:
-                    take(*args)
-            if 1 <= step < GROUP - 1:
-                prepare_k(step + 1)
-            if step == GROUP - 1:
-                build_key_mask()
-            h = step - V_STEP + V_ON_GPSIMD
-            if V_ON_GPSIMD <= h < GROUP:
-                mask_and_group_v(h, nc.vector)
-            if entered(step, MASK_LAG) is not None:
-                mask_weights(step - MASK_LAG)
-            if entered(step, 1) is not None:
-                join_maxima(step - 1)
+            def do_R():
+                if entered(step, 1) is not None:
+                    row_maximum(step - 1)
+
+            def do_K():
+                for take, args in take_now:
+                    if take is take_k:
+                        take(*args)
+                if 1 <= step < GROUP - 1:
+                    prepare_k(step + 1)
+                if step == GROUP - 1:
+                    build_key_mask()
+                h = step - V_STEP + V_ON_GPSIMD
+                if V_ON_GPSIMD <= h < GROUP:
+                    mask_and_group_v(h, nc.vector)
+
+            def do_E():
+                if entered(step, MASK_LAG) is not None:
+                    mask_weights(step - MASK_LAG)
+
+            def do_J():
+                if entered(step, 1) is not None:
+                    join_maxima(step - 1)
+
             inverted = []
-            if entered(step, NORM_LAG) is not None and step % PAIR == (NORM_LAG + PAIR - 1) % PAIR:
-                invert_sums((step - NORM_LAG) // PAIR)
-                inverted = [step - NORM_LAG - PAIR + 1 + j for j in range(PAIR)]
-                for place in inverted:
-                    if normaliser(place) != "scalar":
-                        normalise(place)
-            if closed_group(step, QUANT_LAG + 4) is not None and closed_group(step, QUANT_LAG + 4) < LAST - 1:
-                quantise_heads(closed_group(step, QUANT_LAG + 4))
-            place = entered(step, QUANT_LAG)
-            if place is not None and place // GROUP != LAST and (place + 1) % AT_ONCE == 0:
-                quantise_weights(place // GROUP, place % GROUP + 1 - AT_ONCE, place % GROUP + 1)
-            if step == V_QUANT_STEP:
-                for h in range(GROUP):
-                    quantise_v(h)
-            if closed_group(step, 0) is not None and group - 1 in prepared_in:
-                lay_out, quantise, what = prepared_in[group - 1]
-                quantise(what)
+
+            def do_N():
+                if entered(step, NORM_LAG) is not None and step % PAIR == (NORM_LAG + PAIR - 1) % PAIR:
+                    invert_sums((step - NORM_LAG) // PAIR)
+                    inverted.extend([step - NORM_LAG - PAIR + 1 + j for j in range(PAIR)])
+                    for place in inverted:
+                        if normaliser(place) != "scalar":
+                            normalise(place)
+
+            def do_Q():
+                if closed_group(step, QUANT_LAG + 4) is not None and closed_group(step, QUANT_LAG + 4) < LAST - 1:
+                    quantise_heads(closed_group(step, QUANT_LAG + 4))
+                place = entered(step, QUANT_LAG)
+                if place is not None and place // GROUP != LAST and (place + 1) % AT_ONCE == 0:
+                    quantise_weights(place // GROUP, place % GROUP + 1 - AT_ONCE, place % GROUP + 1)
+                if step == V_QUANT_STEP:
+                    for h in range(GROUP):
+                        quantise_v(h)
+                if closed_group(step, 0) is not None and group - 1 in prepared_in:
+                    lay_out, quantise, what = prepared_in[group - 1]
+                    quantise(what)
+
+            jobs = {"R": do_R, "K": do_K, "E": do_E, "J": do_J, "N": do_N, "Q": do_Q}
+            for letter in (V_ORDER_CLOSING if i == GROUP - 1 else V_ORDER):
+                jobs[letter]()
 
             for take, args in take_now:
                 if take is not take_k:

@@ -61,8 +61,10 @@ def tile_scaleddotproductattention_pa_kernel(
         PAIR = 2
         QUANT_LAG = 8
         AT_ONCE = 4
-        V_ORDER = "RKEJNQ"
-        V_ORDER_CLOSING = "RKEJQN"
+        V_ORDER = "RKTEJNQ"
+        T_LAG = 3
+        EARLY_T = True
+        V_ORDER_CLOSING = "RKTEJQN"
         MASK_I = 3
         MASK_FROM = 0
         MASK_TO = 10
@@ -397,7 +399,15 @@ def tile_scaleddotproductattention_pa_kernel(
 
         def exponentials(place):
             group, i = divmod(place, GROUP)
+            j = place % PAIR
+            if j == 0:
+                pair_sums = stats.tile([P, PAIR, KEY_HALVES], F32)
+                pair_sums_of[place // PAIR] = pair_sums
+            pair_sums = pair_sums_of[place // PAIR]
+            first = pair_sums[:, j, 0:1]
             if not masked_by_tensor(place):
+                first_raw = stats.tile([P, 1], F32)
+                first = first_raw[:]
                 stand_in_exp = stats.tile([P, 1], F32)
                 nc.scalar.activation(
                     out=stand_in_exp[:],
@@ -407,7 +417,6 @@ def tile_scaleddotproductattention_pa_kernel(
                     scale=SCALE,
                 )
             weights = work.tile([P, SEQ], F32, bufs=5)
-            sums = stats.tile([P, KEY_HALVES], F32)
             for half in range(KEY_HALVES):
                 nc.scalar.activation(
                     out=weights[:, half * BANK : (half + 1) * BANK],
@@ -415,29 +424,33 @@ def tile_scaleddotproductattention_pa_kernel(
                     func=ACT.Exp,
                     bias=neg_max_of[place][:],
                     scale=SCALE,
-                    accum_out=sums[:, half : half + 1],
+                    accum_out=first if half == 0 else pair_sums[:, j, 1:2],
                 )
             weights_of[place] = weights
-            if masked_by_tensor(place):
-                sums_of[place] = (sums[:, 0:1], sums)
-                return
-            first_sum = stats.tile([P, 1], F32)
-            nc.scalar.activation(
-                out=first_sum[:], in_=stand_in_exp[:], func=ACT.Identity, scale=neg_masked[:], bias=sums[:, 0:1]
-            )
-            sums_of[place] = (first_sum[:], sums)
+            if not masked_by_tensor(place):
+                stand_in_of[place] = (stand_in_exp, first)
 
-        sums_of = {}
+        pair_sums_of = {}
+        stand_in_of = {}
 
-        def join_sums(place):
-            first_sum, sums = sums_of[place]
-            j = place % PAIR
-            if j == 0:
-                row_sums = stats.tile([P, PAIR], F32)
-                row_sum_of[place // PAIR] = row_sums
-            nc.scalar.activation(
-                out=row_sum_of[place // PAIR][:, j : j + 1], in_=first_sum, func=ACT.Identity, bias=sums[:, 1:2]
+        def take_off_masked(place):
+            if not masked_by_tensor(place):
+                stand_in_exp, first = stand_in_of[place]
+                nc.vector.tensor_scalar(
+                    out=pair_sums_of[place // PAIR][:, place % PAIR, 0:1],
+                    in0=stand_in_exp[:],
+                    scalar1=neg_masked[:],
+                    scalar2=first,
+                    op0=ALU.mult,
+                    op1=ALU.add,
+                )
+
+        def join_sums(pair):
+            row_sums = stats.tile([P, PAIR], F32)
+            nc.vector.tensor_reduce(
+                out=row_sums[:], in_=pair_sums_of[pair][:], axis=mybir.AxisListType.X, op=ALU.add
             )
+            row_sum_of[pair] = row_sums
 
         def invert_sums(pair):
             inv_sums = stats.tile([P, PAIR], F32)
@@ -636,8 +649,6 @@ def tile_scaleddotproductattention_pa_kernel(
             if entered(step, FLIP_LAG) is not None:
                 keys_to_partitions(step - FLIP_LAG)
 
-            if entered(step, 3) is not None:
-                join_sums(step - 3)
             def do_R():
                 if entered(step, 1) is not None:
                     row_maximum(step - 1)
@@ -654,6 +665,16 @@ def tile_scaleddotproductattention_pa_kernel(
                 if V_ON_GPSIMD <= h < GROUP:
                     mask_and_group_v(h, nc.vector)
 
+            closes_pair = entered(step, NORM_LAG) is not None and step % PAIR == (NORM_LAG + PAIR - 1) % PAIR
+
+            def do_T():
+                if closes_pair and EARLY_T:
+                    join_sums((step - NORM_LAG) // PAIR)
+                if entered(step, T_LAG) is not None:
+                    take_off_masked(step - T_LAG)
+                if closes_pair and not EARLY_T:
+                    join_sums((step - NORM_LAG) // PAIR)
+
             def do_E():
                 if entered(step, MASK_LAG) is not None:
                     mask_weights(step - MASK_LAG)
@@ -665,7 +686,7 @@ def tile_scaleddotproductattention_pa_kernel(
             inverted = []
 
             def do_N():
-                if entered(step, NORM_LAG) is not None and step % PAIR == (NORM_LAG + PAIR - 1) % PAIR:
+                if closes_pair:
                     invert_sums((step - NORM_LAG) // PAIR)
                     inverted.extend([step - NORM_LAG - PAIR + 1 + j for j in range(PAIR)])
                     for place in inverted:
@@ -685,7 +706,7 @@ def tile_scaleddotproductattention_pa_kernel(
                     lay_out, quantise, what = prepared_in[group - 1]
                     quantise(what)
 
-            jobs = {"R": do_R, "K": do_K, "E": do_E, "J": do_J, "N": do_N, "Q": do_Q}
+            jobs = {"R": do_R, "K": do_K, "E": do_E, "J": do_J, "N": do_N, "T": do_T, "Q": do_Q}
             for letter in (V_ORDER_CLOSING if i == GROUP - 1 else V_ORDER):
                 jobs[letter]()
 

@@ -51,7 +51,7 @@ def tile_scaleddotproductattention_pa_kernel(
         END = GROUP * len(groups)
 
         LAST = len(groups) - 1
-        ON_SCALAR = ()
+        ON_SCALAR = (1, 3)
         FOLDED = ()
         FOLD_FROM = 4
         SCALAR_FROM = 0
@@ -61,6 +61,7 @@ def tile_scaleddotproductattention_pa_kernel(
         PAIR = 2
         QUANT_LAG = 8
         AT_ONCE = 4
+        SIDE_AT = {1: (0,), 3: (1,)}
         V_ORDER = "RKTEJNQ"
         T_LAG = 3
         EARLY_T = True
@@ -257,18 +258,20 @@ def tile_scaleddotproductattention_pa_kernel(
 
         v_grouped_of = {}
 
-        def mask_and_group_v(h, engine=nc.gpsimd):
-            v_grouped = work.tile([P, KEY_PASSES * HEAD_DIM * PACK], BF16, align_bytes=64, bufs=5)
-            engine.tensor_tensor(
-                out=v_grouped[:].rearrange("p (g d w) -> p g d w", g=KEY_PASSES, w=PACK),
-                in0=v_raw_of[h][:].rearrange("p (g u) (e d) -> p g d (u e)", u=2, e=2),
-                in1=ind_v_words[:]
-                .rearrange("p (g u) e -> p g (u e)", u=2)
-                .unsqueeze(2)
-                .to_broadcast([P, KEY_PASSES, HEAD_DIM, PACK]),
-                op=ALU.mult,
-            )
-            v_grouped_of[h] = v_grouped
+        def mask_and_group_v(h, part, engine=nc.gpsimd):
+            if part[0] == 0:
+                v_grouped = work.tile([P, KEY_PASSES * HEAD_DIM * PACK], BF16, align_bytes=64, bufs=5)
+                v_grouped_of[h] = v_grouped
+            for g in part:
+                engine.tensor_tensor(
+                    out=v_grouped_of[h][:].rearrange("p (g d w) -> p g d w", g=KEY_PASSES, w=PACK)[:, g, :, :],
+                    in0=v_raw_of[h][:].rearrange("p (g u) (e d) -> p g d (u e)", u=2, e=2)[:, g, :, :],
+                    in1=ind_v_words[:]
+                    .rearrange("p (g u) e -> p g (u e)", u=2)[:, g, :]
+                    .unsqueeze(1)
+                    .to_broadcast([P, HEAD_DIM, PACK]),
+                    op=ALU.mult,
+                )
 
         def quantise_v(h):
             nc.vector.quantize_mx(
@@ -278,19 +281,24 @@ def tile_scaleddotproductattention_pa_kernel(
         WO_PIECES = 2 * FEATURE_PASSES
         wo_grouped_of = {}
 
-        def group_wo(piece):
+        def group_wo(piece, part):
             g, half = divmod(piece, 2)
-            cols = slice(half * BANK, (half + 1) * BANK)
-            wo_grouped = work.tile([P, BANK * PACK], BF16, align_bytes=64)
-            nc.gpsimd.tensor_scalar(
-                out=wo_grouped[:].rearrange("p (n i) -> p n i", i=PACK),
-                in0=wo_raw_of[g][:, :, cols].rearrange("p i n -> p n i"),
-                scalar1=1.0,
-                scalar2=0.0,
-                op0=ALU.mult,
-                op1=ALU.add,
-            )
-            wo_grouped_of[piece] = wo_grouped
+            if part[0] == 0:
+                wo_grouped = work.tile([P, BANK * PACK], BF16, align_bytes=64)
+                wo_grouped_of[piece] = wo_grouped
+            WIDTH = BANK // 2
+            for b in part:
+                cols = slice(half * BANK + b * WIDTH, half * BANK + (b + 1) * WIDTH)
+                nc.gpsimd.tensor_scalar(
+                    out=wo_grouped_of[piece][:, b * WIDTH * PACK : (b + 1) * WIDTH * PACK].rearrange(
+                        "p (n i) -> p n i", i=PACK
+                    ),
+                    in0=wo_raw_of[g][:, :, cols].rearrange("p i n -> p n i"),
+                    scalar1=1.0,
+                    scalar2=0.0,
+                    op0=ALU.mult,
+                    op1=ALU.add,
+                )
 
         def quantise_wo(piece):
             g, half = divmod(piece, 2)
@@ -606,9 +614,10 @@ def tile_scaleddotproductattention_pa_kernel(
         prepare_k(0)
         prepare_k(1)
         for h in range(V_ON_GPSIMD):
-            mask_and_group_v(h)
+            mask_and_group_v(h, (0, 1))
 
         taken_next = []
+        for_scalar = []
 
         for step in range(END + QUANT_LAG):
             take_now, taken_next = taken_next, []
@@ -663,7 +672,7 @@ def tile_scaleddotproductattention_pa_kernel(
                     build_key_mask()
                 h = step - V_STEP + V_ON_GPSIMD
                 if V_ON_GPSIMD <= h < GROUP:
-                    mask_and_group_v(h, nc.vector)
+                    mask_and_group_v(h, (0, 1), nc.vector)
 
             closes_pair = entered(step, NORM_LAG) is not None and step % PAIR == (NORM_LAG + PAIR - 1) % PAIR
 
@@ -717,9 +726,9 @@ def tile_scaleddotproductattention_pa_kernel(
                 exponentials(step - 2)
             if entered(step, 0) is not None and folded(step):
                 copy_hi(step)
-            for place in inverted:
-                if normaliser(place) == "scalar":
-                    normalise(place)
+            for place in for_scalar:
+                normalise(place)
+            for_scalar = [place for place in inverted if normaliser(place) == "scalar"]
 
             if entered(step, QUANT_LAG) is not None and (step - QUANT_LAG) // GROUP == LAST:
                 j = (step - QUANT_LAG) % GROUP
@@ -753,6 +762,6 @@ def tile_scaleddotproductattention_pa_kernel(
                 load_v(GROUP + group)
             if i == 0 and group - 3 in range(FEATURE_PASSES):
                 load_wo(group - 3)
-            if closed_group(step, 0) is not None and group in prepared_in:
+            if group in prepared_in and step < END and i in SIDE_AT:
                 lay_out, quantise, what = prepared_in[group]
-                lay_out(what)
+                lay_out(what, SIDE_AT[i])

@@ -56,7 +56,7 @@ def tile_scaleddotproductattention_pa_kernel(
         FOLD_FROM = 4
         SCALAR_FROM = 0
         SCALAR_TO = 8
-        AT_THE_END = {END - 3: "vector", END - 2: "scalar", END - 1: "vector"}
+        AT_THE_END = {END - 3: "vector", END - 2: "scalar", END - 1: "scalar"}
         NORM_LAG = 4
         PAIR = 2
         QUANT_LAG = 8
@@ -64,13 +64,18 @@ def tile_scaleddotproductattention_pa_kernel(
         SIDE_AT = {1: (0,), 3: (1,)}
         V_ORDER = "RKTEJNQ"
         T_LAG = 3
+        E_FIRST = True
+        START_STEPS = 0
+        V_ORDER_START = "RJKTENQ"
+        C14_AT = 3
+        P14_AT = None
+        T_ON_SCALAR = True
         EARLY_T = True
         V_ORDER_CLOSING = "RKTEJQN"
-        MASK_I = 3
-        MASK_FROM = 0
-        MASK_TO = 10
+        UNPREPARED = (0,)
+        ALSO_BY_TENSOR = (32, 36)
         COPY_LATE = 0
-        V_ON_GPSIMD = 2
+        V_ON_GPSIMD = 3
         V_STEP = 3
         V_QUANT_STEP = 7
         FLIP_LAG = 7
@@ -144,14 +149,14 @@ def tile_scaleddotproductattention_pa_kernel(
         nc.gpsimd.tensor_scalar(
             out=neg_ident[:], in0=ident_bf16[:], scalar1=MASKED_SCORE, scalar2=1.0, op0=ALU.mult, op1=ALU.mult
         )
-        valid_keys = const.tile([P, 1], F32)
-        nc.vector.reduce_sum(out=valid_keys[:], in_=ind_k_rows[:], axis=mybir.AxisListType.X)
-        inv_valid = const.tile([P, 1], F32)
-        nc.vector.tensor_scalar(out=inv_valid[:], in0=valid_keys[:], scalar1=1.0, scalar2=None, op0=ALU.max)
         masked_rows = const.tile([P, SEQ], BF16)
         nc.vector.tensor_scalar(
             out=masked_rows[:], in0=ind_k_rows[:], scalar1=-1.0, scalar2=1.0, op0=ALU.mult, op1=ALU.add
         )
+        valid_keys = const.tile([P, 1], F32)
+        nc.vector.reduce_sum(out=valid_keys[:], in_=ind_k_rows[:], axis=mybir.AxisListType.X)
+        inv_valid = const.tile([P, 1], F32)
+        nc.vector.tensor_scalar(out=inv_valid[:], in0=valid_keys[:], scalar1=1.0, scalar2=None, op0=ALU.max)
         nc.vector.reciprocal(out=inv_valid[:], in_=inv_valid[:])
         any_valid = const.tile([P, 1], F32)
         nc.vector.tensor_scalar(out=any_valid[:], in0=valid_keys[:], scalar1=1.0, scalar2=None, op0=ALU.min)
@@ -185,6 +190,9 @@ def tile_scaleddotproductattention_pa_kernel(
 
         Q_WORDS = GROUP * P // 2
 
+        def with_stand_in(group):
+            return [i for i in range(GROUP) if head_and_queries(group * GROUP + i)[0] not in UNPREPARED]
+
         def small_products(next_group, heads, group):
             bank = score_psum.tile([P, BANK], F32, tag="score")
             if next_group is not None:
@@ -201,7 +209,7 @@ def tile_scaleddotproductattention_pa_kernel(
                         stop=(i == SEQ // P - 1),
                     )
             if group is not None:
-                for i in range(GROUP):
+                for i in with_stand_in(group):
                     h, queries = head_and_queries(group * GROUP + i)
                     nc.tensor.matmul(
                         bank[:, Q_WORDS + GROUP + i : Q_WORDS + GROUP + i + 1],
@@ -216,7 +224,10 @@ def tile_scaleddotproductattention_pa_kernel(
             bank = in_psum["small"]
             if group is not None:
                 stand_in_scores = stats.tile([P, GROUP], F32)
-                nc.scalar.copy(out=stand_in_scores[:], in_=bank[:, Q_WORDS + GROUP : Q_WORDS + 2 * GROUP])
+                first = with_stand_in(group)[0]
+                nc.scalar.copy(
+                    out=stand_in_scores[:, first:GROUP], in_=bank[:, Q_WORDS + GROUP + first : Q_WORDS + 2 * GROUP]
+                )
                 stand_in_scores_of[group] = stand_in_scores
             if heads:
                 mean = stats.tile([P, len(heads)], F32)
@@ -249,6 +260,10 @@ def tile_scaleddotproductattention_pa_kernel(
 
         def take_k(h, half):
             keys = slice(half * BANK, (half + 1) * BANK)
+            if h in UNPREPARED:
+                copy = nc.vector.tensor_copy if half == 0 else nc.scalar.copy
+                copy(out=k_t[:, h, keys], in_=in_psum[("k", half)][:].rearrange("p i s -> p (i s)"))
+                return
             nc.vector.tensor_tensor(
                 out=k_t[:, h, keys],
                 in0=in_psum[("k", half)][:].rearrange("p i s -> p (i s)"),
@@ -321,7 +336,8 @@ def tile_scaleddotproductattention_pa_kernel(
         c_grouped_of = {}
 
         def masked_by_tensor(place):
-            return place % GROUP == MASK_I and MASK_FROM <= place // GROUP < MASK_TO
+            h, queries = head_and_queries(place)
+            return h in UNPREPARED or place in ALSO_BY_TENSOR
 
         def scores(place):
             h, queries = head_and_queries(place)
@@ -436,13 +452,17 @@ def tile_scaleddotproductattention_pa_kernel(
                 )
             weights_of[place] = weights
             if not masked_by_tensor(place):
+                if T_ON_SCALAR:
+                    nc.scalar.activation(
+                        out=pair_sums[:, j, 0:1], in_=stand_in_exp[:], func=ACT.Identity, scale=neg_masked[:], bias=first
+                    )
                 stand_in_of[place] = (stand_in_exp, first)
 
         pair_sums_of = {}
         stand_in_of = {}
 
         def take_off_masked(place):
-            if not masked_by_tensor(place):
+            if not masked_by_tensor(place) and not T_ON_SCALAR:
                 stand_in_exp, first = stand_in_of[place]
                 nc.vector.tensor_scalar(
                     out=pair_sums_of[place // PAIR][:, place % PAIR, 0:1],
@@ -601,17 +621,18 @@ def tile_scaleddotproductattention_pa_kernel(
             return place // GROUP if place is not None and place % GROUP == GROUP - 1 else None
 
         def prepare_k(h):
-            make_rows(h)
+            if h not in UNPREPARED:
+                make_rows(h)
             for half in range(KEY_HALVES):
                 transpose_k(h, half, score_psum, "score")
             for half in range(KEY_HALVES):
                 take_k(h, half)
 
-        small_products(0, [0], None)
-        take_small_products(0, [0], None)
+        small_products(0, [], None)
+        take_small_products(0, [], None)
+        prepare_k(0)
         small_products(None, [1], None)
         take_small_products(None, [1], None)
-        prepare_k(0)
         prepare_k(1)
         for h in range(V_ON_GPSIMD):
             mask_and_group_v(h, (0, 1))
@@ -705,18 +726,23 @@ def tile_scaleddotproductattention_pa_kernel(
             def do_Q():
                 if closed_group(step, QUANT_LAG + 4) is not None and closed_group(step, QUANT_LAG + 4) < LAST - 1:
                     quantise_heads(closed_group(step, QUANT_LAG + 4))
-                place = entered(step, QUANT_LAG)
-                if place is not None and place // GROUP != LAST and (place + 1) % AT_ONCE == 0:
-                    quantise_weights(place // GROUP, place % GROUP + 1 - AT_ONCE, place % GROUP + 1)
                 if step == V_QUANT_STEP:
                     for h in range(GROUP):
                         quantise_v(h)
                 if closed_group(step, 0) is not None and group - 1 in prepared_in:
                     lay_out, quantise, what = prepared_in[group - 1]
                     quantise(what)
+                place = entered(step, QUANT_LAG)
+                if place is not None and place // GROUP != LAST and (place + 1) % AT_ONCE == 0:
+                    quantise_weights(place // GROUP, place % GROUP + 1 - AT_ONCE, place % GROUP + 1)
 
             jobs = {"R": do_R, "K": do_K, "E": do_E, "J": do_J, "N": do_N, "T": do_T, "Q": do_Q}
-            for letter in (V_ORDER_CLOSING if i == GROUP - 1 else V_ORDER):
+            order = V_ORDER_CLOSING if i == GROUP - 1 and step < END else V_ORDER
+            if entered(step, 1) is not None and folded(step - 1):
+                order = order.replace("E", "").replace("R", "ER") if E_FIRST else order
+            if step < START_STEPS:
+                order = V_ORDER_START
+            for letter in order:
                 jobs[letter]()
 
             for take, args in take_now:
@@ -737,15 +763,20 @@ def tile_scaleddotproductattention_pa_kernel(
                     weighted_values(LAST - 1, 0, GROUP)
                     take_values(LAST - 1)
                 weighted_values(LAST, j, j + 1)
-                if j == GROUP - 1:
+                if j == C14_AT:
                     quantise_heads(LAST - 1)
+                if j == P14_AT:
+                    for half in range(2):
+                        project(groups[LAST - 1][1], half, score_psum, "score")
+                if j == GROUP - 1:
                     take_values(LAST)
                     quantise_heads(LAST)
             if step >= END:
                 tensor_side_jobs()
             if step == END - 1 + QUANT_LAG:
                 for half in range(2):
-                    project(groups[LAST - 1][1], half, score_psum, "score")
+                    if P14_AT is None:
+                        project(groups[LAST - 1][1], half, score_psum, "score")
                     taken_next.append((take_result, (groups[LAST - 1][1], half, half == 0)))
                 for take, args in taken_next:
                     take(*args)

@@ -61,9 +61,16 @@ def tile_scaleddotproductattention_pa_kernel(
         PAIR = 2
         QUANT_LAG = 8
         AT_ONCE = 4
-        SIDE_AT = {1: (0,), 3: (1,)}
+        SIDE_AT = {3: (0, 1)}
         V_ORDER = "RKTEJNQ"
         T_LAG = 3
+        SPLIT_TAIL = 1
+        NORMS_FIRST = END
+        P13_AT = (15, 16)
+        QUARTERS = 1
+        COPY_LATE = 1
+        SC = 0
+        SIDE_FIRST = 0
         E_FIRST = True
         START_STEPS = 0
         V_ORDER_START = "RJKTENQ"
@@ -74,7 +81,7 @@ def tile_scaleddotproductattention_pa_kernel(
         V_ORDER_CLOSING = "RKTEJQN"
         UNPREPARED = (0,)
         ALSO_BY_TENSOR = (32, 36)
-        COPY_LATE = 0
+        COPY_LATE = 1
         V_ON_GPSIMD = 3
         V_STEP = 3
         V_QUANT_STEP = 7
@@ -567,10 +574,15 @@ def tile_scaleddotproductattention_pa_kernel(
 
         def take_values(group):
             c_grouped = work.tile([P, P * PACK], BF16, align_bytes=64)
-            nc.scalar.copy(
-                out=c_grouped[:].rearrange("p (q i) -> p q i", i=PACK),
-                in_=o_t_of[group][:].rearrange("p i q -> p q i"),
-            )
+            parts = 1 if group != LAST or not SPLIT_TAIL else 2
+            width = P // parts
+            for part in range(parts):
+                copy = nc.scalar.copy if part == 0 else nc.vector.tensor_copy
+                some = slice(part * width, (part + 1) * width)
+                copy(
+                    out=c_grouped[:].rearrange("p (q i) -> p q i", i=PACK)[:, some, :],
+                    in_=o_t_of[group][:].rearrange("p i q -> p q i")[:, some, :],
+                )
             c_grouped_of[group] = c_grouped
 
         def quantise_heads(group):
@@ -600,11 +612,14 @@ def tile_scaleddotproductattention_pa_kernel(
             queries = slice(t * P, (t + 1) * P)
             cols = slice(half * BANK, (half + 1) * BANK)
             result = work.tile([P, BANK], F32, bufs=8)
-            if on_vector:
-                nc.vector.tensor_copy(out=result[:], in_=in_psum[("out", t, half)][:])
-            else:
-                nc.scalar.copy(out=result[:], in_=in_psum[("out", t, half)][:])
-            nc.sync.dma_start(out=out[0, queries, cols], in_=result[:])
+            parts = 2 if QUARTERS and groups[LAST][1] == t else 1
+            width = BANK // parts
+            for part in range(parts):
+                some = slice(part * width, (part + 1) * width)
+                there = slice(half * BANK + part * width, half * BANK + (part + 1) * width)
+                copy = nc.vector.tensor_copy if on_vector else nc.scalar.copy
+                copy(out=result[:, some], in_=in_psum[("out", t, half)][:, some])
+                nc.sync.dma_start(out=out[0, queries, there], in_=result[:, some])
 
 
         prepared_in = {}
@@ -663,7 +678,7 @@ def tile_scaleddotproductattention_pa_kernel(
                     weighted_values(closed_group(step, QUANT_LAG + 2), 0, GROUP)
                     taken_next.append((take_values, (closed_group(step, QUANT_LAG + 2),)))
                 for half in range(2):
-                    done = closed_group(step, QUANT_LAG + 7 + half)
+                    done = closed_group(step, QUANT_LAG + 7 + half if step < END else P13_AT[half])
                     if done is not None and done < LAST - 1 and groups[done][0] == FEATURE_PASSES - 1:
                         t = groups[done][1]
                         project(t, half, score_psum, "score")
@@ -674,9 +689,11 @@ def tile_scaleddotproductattention_pa_kernel(
             if step == 0:
                 small_products(1, [2, 3], None)
                 take_small_products(1, [2, 3], None)
+            if SIDE_FIRST and entered(step, FLIP_LAG) is not None:
+                keys_to_partitions(step - FLIP_LAG)
             if step < END:
                 tensor_side_jobs()
-            if entered(step, FLIP_LAG) is not None:
+            if not SIDE_FIRST and entered(step, FLIP_LAG) is not None:
                 keys_to_partitions(step - FLIP_LAG)
 
             def do_R():
@@ -705,8 +722,10 @@ def tile_scaleddotproductattention_pa_kernel(
                 if closes_pair and not EARLY_T:
                     join_sums((step - NORM_LAG) // PAIR)
 
+            late_copy = COPY_LATE and entered(step, MASK_LAG) is not None and masked_by_tensor(step - MASK_LAG)
+
             def do_E():
-                if entered(step, MASK_LAG) is not None:
+                if entered(step, MASK_LAG) is not None and not late_copy:
                     mask_weights(step - MASK_LAG)
 
             def do_J():
@@ -745,16 +764,25 @@ def tile_scaleddotproductattention_pa_kernel(
             for letter in order:
                 jobs[letter]()
 
+            if SC == 2 or step >= NORMS_FIRST:
+                for place in for_scalar:
+                    normalise(place)
+                for_scalar = [place for place in inverted if normaliser(place) == "scalar"]
+            if SC == 1 and entered(step, 2) is not None:
+                exponentials(step - 2)
             for take, args in take_now:
                 if take is not take_k:
                     take(*args)
-            if entered(step, 2) is not None:
+            if SC in (0, 2) and entered(step, 2) is not None:
                 exponentials(step - 2)
             if entered(step, 0) is not None and folded(step):
                 copy_hi(step)
-            for place in for_scalar:
-                normalise(place)
-            for_scalar = [place for place in inverted if normaliser(place) == "scalar"]
+            if late_copy:
+                mask_weights(step - MASK_LAG)
+            if SC != 2 and step < NORMS_FIRST:
+                for place in for_scalar:
+                    normalise(place)
+                for_scalar = [place for place in inverted if normaliser(place) == "scalar"]
 
             if entered(step, QUANT_LAG) is not None and (step - QUANT_LAG) // GROUP == LAST:
                 j = (step - QUANT_LAG) % GROUP

@@ -61,7 +61,7 @@ def tile_scaleddotproductattention_pa_kernel(
         PAIR = 2
         QUANT_LAG = 8
         AT_ONCE = 4
-        SIDE_AT = {3: (0, 1)}
+        SIDE_AT = {1: (0,), 3: (1,)}
         V_ORDER = "RKTEJNQ"
         T_LAG = 3
         SPLIT_TAIL = 1

@@ -64,6 +64,9 @@ def tile_scaleddotproductattention_pa_kernel(
         SIDE_AT = {1: (0,), 3: (1,)}
         V_ORDER = "RKTEJNQ"
         T_LAG = 3
+        WARM_HALVES = (1,)
+        WARM_FROM = 8
+        WARM_N = 512
         SPLIT_TAIL = 1
         NORMS_FIRST = END
         P13_AT = (15, 16)
@@ -346,12 +349,26 @@ def tile_scaleddotproductattention_pa_kernel(
             h, queries = head_and_queries(place)
             return h in UNPREPARED or place in ALSO_BY_TENSOR
 
+        def keep_warm(bank):
+            moving = slice(0, 2)
+            nc.tensor.matmul_mx(
+                out=bank[:, 0:WARM_N],
+                lhsT=v_codes[:, 0, 0:P].bitcast(FP8X4),
+                lhsT_scale=v_scales[:, 0, 0:P],
+                rhs=v_codes[:, moving, :].rearrange("p h w -> p (h w)")[:, 0:WARM_N].bitcast(FP8X4),
+                rhs_scale=v_scales[:, moving, :].rearrange("p h w -> p (h w)")[:, 0:WARM_N],
+                start=True,
+                stop=True,
+            )
+
         def scores(place):
             h, queries = head_and_queries(place)
             group, i = divmod(place, GROUP)
             halves = []
             for half in range(KEY_HALVES):
                 score = score_psum.tile([P, BANK], F32, tag="score")
+                if half in WARM_HALVES and place >= WARM_FROM:
+                    keep_warm(score)
                 nc.tensor.matmul(
                     score[:],
                     lhsT=q_t_of[group][:, i, :],

@@ -26,12 +26,32 @@ FEATURE_PASSES = HEADS * HEAD_DIM // K_PASS
 GROUP = K_PASS // HEAD_DIM
 Q_TILES = SEQ // P
 KEY_HALVES = SEQ // BANK
+KEY_BLOCKS = SEQ // P
+PAIR = 2
 
 SCALE = 1.0 / math.sqrt(HEAD_DIM)
-SCORE_BANKS = 8
-MASKED_SCORE = -1.0e30
+BANKS = 8
+MASKED_SCORE = -(2.0**100)
 
 FLOPS = 3 * 2 * SEQ * SEQ * HEADS * HEAD_DIM
+
+WITH_STAND_IN = (5, 7)
+FLIP_LAG = 7
+EMPTY_LAG = 8
+QUANT_LAG = 8
+NORM_LAG = 4
+SIDE_AT = {1: (0,), 3: (1,)}
+V_ORDER = "RKTEJNQ"
+V_ORDER_CLOSING = "RKTEJQN"
+V_ON_GPSIMD = 4
+V_STEP = 3
+V_QUANT_STEP = 7
+NORM_ON_SCALAR = (1,)
+NORM_ON_SCALAR_GROUPS = 8
+EMPTY_ON_VECTOR = (3,)
+LAST_ON_VECTOR = 3
+P13_AT = (15, 16)
+C14_AT = 3
 
 
 def tile_scaleddotproductattention_pa_kernel(
@@ -44,57 +64,15 @@ def tile_scaleddotproductattention_pa_kernel(
         raw = stack.enter_context(tc.tile_pool(name="raw", bufs=4))
         work = stack.enter_context(tc.tile_pool(name="work", bufs=2))
         stats = stack.enter_context(tc.tile_pool(name="stats", bufs=8))
-        score_psum = stack.enter_context(tc.psum_pool(name="score_psum", bufs=SCORE_BANKS))
+        psum = stack.enter_context(tc.psum_pool(name="psum", bufs=BANKS))
         stack.enter_context(tc.manual_schedule())
 
         groups = [(g, t) for g in range(FEATURE_PASSES) for t in range(Q_TILES)]
         END = GROUP * len(groups)
-
         LAST = len(groups) - 1
-        ON_SCALAR = (1, 3)
-        FOLDED = ()
-        FOLD_FROM = 4
-        SCALAR_FROM = 0
-        SCALAR_TO = 8
-        AT_THE_END = {END - 3: "vector", END - 2: "scalar", END - 1: "scalar"}
-        NORM_LAG = 4
-        PAIR = 2
-        QUANT_LAG = 8
-        AT_ONCE = 4
-        SIDE_AT = {1: (0,), 3: (1,)}
-        V_ORDER = "RKTEJNQ"
-        T_LAG = 3
-        WARM_HALVES = (1,)
-        WARM_FROM = 8
-        WARM_N = 512
-        SPLIT_TAIL = 1
-        NORMS_FIRST = END
-        P13_AT = (15, 16)
-        QUARTERS = 1
-        COPY_LATE = 1
-        SC = 0
-        SIDE_FIRST = 0
-        E_FIRST = True
-        START_STEPS = 0
-        V_ORDER_START = "RJKTENQ"
-        C14_AT = 3
-        P14_AT = None
-        T_ON_SCALAR = True
-        EARLY_T = True
-        V_ORDER_CLOSING = "RKTEJQN"
-        UNPREPARED = (0,)
-        ALSO_BY_TENSOR = (32, 36)
-        COPY_LATE = 1
-        V_ON_GPSIMD = 3
-        V_STEP = 3
-        V_QUANT_STEP = 7
-        FLIP_LAG = 7
-        MASK_LAG = 8
 
-        def head_and_queries(place):
-            group, i = divmod(place, GROUP)
-            g, t = groups[group]
-            return g * GROUP + i, slice(t * P, (t + 1) * P)
+        def head_of(place):
+            return groups[place // GROUP][0] * GROUP + place % GROUP
 
         k_t = keep.tile([P, HEADS, SEQ], BF16)
         stand_in = keep.tile([P, HEADS], BF16)
@@ -118,7 +96,7 @@ def tile_scaleddotproductattention_pa_kernel(
             q_raw_of[group] = q_raw
 
         def load_k(h):
-            k_raw = raw.tile([P, SEQ // P, HEAD_DIM], BF16)
+            k_raw = raw.tile([P, KEY_BLOCKS, HEAD_DIM], BF16)
             nc.sync.dma_start(out=k_raw[:], in_=k_masked[0, h].rearrange("(i p) d -> p i d", p=P))
             k_raw_of[h] = k_raw
 
@@ -133,8 +111,9 @@ def tile_scaleddotproductattention_pa_kernel(
             nc.sync.dma_start(out=wo_raw[:], in_=rows.rearrange("(i p) n -> p i n", p=P))
             wo_raw_of[g] = wo_raw
 
-        ind_k_rows = const.tile([P, SEQ], BF16)
-        nc.scalar.dma_start(out=ind_k_rows[:], in_=ind_k[0].partition_broadcast(P))
+        ind_k_blocks = const.tile([P, P], BF16)
+        nc.vector.memset(ind_k_blocks[:], 0.0)
+        nc.scalar.dma_start(out=ind_k_blocks[0:KEY_BLOCKS, :], in_=ind_k[0].rearrange("(b p) -> b p", p=P))
         load_k(0)
         load_q(0)
         for h in range(1, GROUP):
@@ -146,35 +125,63 @@ def tile_scaleddotproductattention_pa_kernel(
         load_q(1)
         for h in range(GROUP):
             load_v(h)
+        ind_k_rows = const.tile([P, SEQ], BF16)
+        nc.scalar.dma_start(out=ind_k_rows[:], in_=ind_k[0].partition_broadcast(P))
 
-        ones = const.tile([P, 1], BF16)
+        ones = const.tile([P, P], BF16)
         nc.vector.memset(ones[:], 1.0)
         table_loader = const.tile([P, 1], F32)
-        nc.scalar.activation(out=table_loader[:], in_=ones[:], func=ACT.Exp)
+        nc.scalar.activation(out=table_loader[:], in_=ones[:, 0:1], func=ACT.Exp)
         ident_bf16 = const.tile([P, P], BF16)
         make_identity(nc, ident_bf16[:])
         ident_f32 = const.tile([P, P], F32)
         make_identity(nc, ident_f32[:])
-        neg_ident = const.tile([P, P], BF16)
-        nc.gpsimd.tensor_scalar(
-            out=neg_ident[:], in0=ident_bf16[:], scalar1=MASKED_SCORE, scalar2=1.0, op0=ALU.mult, op1=ALU.mult
-        )
-        masked_rows = const.tile([P, SEQ], BF16)
-        nc.vector.tensor_scalar(
-            out=masked_rows[:], in0=ind_k_rows[:], scalar1=-1.0, scalar2=1.0, op0=ALU.mult, op1=ALU.add
-        )
-        valid_keys = const.tile([P, 1], F32)
-        nc.vector.reduce_sum(out=valid_keys[:], in_=ind_k_rows[:], axis=mybir.AxisListType.X)
-        inv_valid = const.tile([P, 1], F32)
-        nc.vector.tensor_scalar(out=inv_valid[:], in0=valid_keys[:], scalar1=1.0, scalar2=None, op0=ALU.max)
-        nc.vector.reciprocal(out=inv_valid[:], in_=inv_valid[:])
+
+        neg_columns = const.tile([P, KEY_BLOCKS, P], F32)
+        ind_k_columns = const.tile([P, KEY_BLOCKS], BF16)
         any_valid = const.tile([P, 1], F32)
-        nc.vector.tensor_scalar(out=any_valid[:], in0=valid_keys[:], scalar1=1.0, scalar2=None, op0=ALU.min)
+        inv_valid = const.tile([P, 1], F32)
         neg_masked = const.tile([P, 1], F32)
+
+        flipped_ind = psum.tile([P, P], BF16, tag="bank")
+        nc.tensor.transpose(flipped_ind[:], ind_k_blocks[:], ident_bf16[:])
+        neg_column = const.tile([P, KEY_BLOCKS], F32)
         nc.vector.tensor_scalar(
-            out=neg_masked[:], in0=valid_keys[:], scalar1=-float(SEQ), scalar2=any_valid[:], op0=ALU.add, op1=ALU.mult
+            out=neg_column[:],
+            in0=flipped_ind[:, 0:KEY_BLOCKS],
+            scalar1=-1.0,
+            scalar2=-MASKED_SCORE,
+            op0=ALU.add,
+            op1=ALU.mult,
         )
+        half_blocks = KEY_BLOCKS // 2
+        for half, copy in ((0, nc.vector.tensor_copy), (1, nc.scalar.copy)):
+            blocks = slice(half * half_blocks, (half + 1) * half_blocks)
+            copy(
+                out=neg_columns[:, blocks, :],
+                in_=neg_column[:, blocks].unsqueeze(2).to_broadcast([P, half_blocks, P]),
+            )
+        nc.scalar.copy(out=ind_k_columns[:], in_=flipped_ind[:, 0:KEY_BLOCKS])
+
+        def count_valid_keys():
+            counts = psum.tile([P, KEY_BLOCKS], F32, tag="bank")
+            nc.tensor.matmul(counts[:], lhsT=ones[:], rhs=ind_k_columns[:], start=True, stop=True)
+            valid_keys = stats.tile([P, 1], F32)
+            nc.vector.reduce_sum(out=valid_keys[:], in_=counts[:], axis=mybir.AxisListType.X)
+            nc.vector.tensor_scalar(out=any_valid[:], in0=valid_keys[:], scalar1=1.0, scalar2=None, op0=ALU.min)
+            nc.vector.tensor_scalar(out=inv_valid[:], in0=valid_keys[:], scalar1=1.0, scalar2=None, op0=ALU.max)
+            nc.vector.tensor_scalar(
+                out=neg_masked[:],
+                in0=valid_keys[:],
+                scalar1=-float(SEQ),
+                scalar2=any_valid[:],
+                op0=ALU.add,
+                op1=ALU.mult,
+            )
+            nc.vector.reciprocal(out=inv_valid[:], in_=inv_valid[:])
+
         key_mask = const.tile([P, KEY_PASSES, P, PACK], BF16)
+        masked_rows = const.tile([P, SEQ], BF16)
 
         def build_key_mask():
             nc.vector.tensor_copy(
@@ -184,14 +191,11 @@ def tile_scaleddotproductattention_pa_kernel(
                 .unsqueeze(2)
                 .to_broadcast([P, KEY_PASSES, P, PACK]),
             )
+            nc.vector.tensor_scalar(
+                out=masked_rows[:], in0=ind_k_rows[:], scalar1=-1.0, scalar2=1.0, op0=ALU.mult, op1=ALU.add
+            )
 
         in_psum = {}
-
-        def features_to_partitions(pool, tag, four_row_tiles):
-            flipped = pool.tile([P, GROUP, P], BF16, tag=tag, name="flipped")
-            for i in range(GROUP):
-                nc.tensor.transpose(flipped[:, i, :], four_row_tiles[:, i, :], ident_bf16[:])
-            return flipped
 
         q_t_of = {}
         mean_of = {}
@@ -201,28 +205,28 @@ def tile_scaleddotproductattention_pa_kernel(
         Q_WORDS = GROUP * P // 2
 
         def with_stand_in(group):
-            return [i for i in range(GROUP) if head_and_queries(group * GROUP + i)[0] not in UNPREPARED]
+            return [i for i in range(GROUP) if head_of(group * GROUP + i) in WITH_STAND_IN]
 
         def small_products(next_group, heads, group):
-            bank = score_psum.tile([P, BANK], F32, tag="score")
+            bank = psum.tile([P, BANK], F32, tag="bank")
             if next_group is not None:
                 q_view = bank[:, 0:Q_WORDS].bitcast(BF16).rearrange("p (i q) -> p i q", i=GROUP)
                 for i in range(GROUP):
                     nc.tensor.transpose(q_view[:, i, :], q_raw_of[next_group][:, i, :], ident_bf16[:])
             for j, h in enumerate(heads):
-                for i in range(SEQ // P):
+                for i in range(KEY_BLOCKS):
                     nc.tensor.matmul(
                         bank[:, Q_WORDS + j : Q_WORDS + j + 1],
                         lhsT=k_raw_of[h][:, i, :],
-                        rhs=ones[:],
+                        rhs=ones[:, 0:1],
                         start=(i == 0),
-                        stop=(i == SEQ // P - 1),
+                        stop=(i == KEY_BLOCKS - 1),
                     )
             if group is not None:
-                for i in with_stand_in(group):
-                    h, queries = head_and_queries(group * GROUP + i)
+                for j, i in enumerate(with_stand_in(group)):
+                    h = head_of(group * GROUP + i)
                     nc.tensor.matmul(
-                        bank[:, Q_WORDS + GROUP + i : Q_WORDS + GROUP + i + 1],
+                        bank[:, Q_WORDS + GROUP + j : Q_WORDS + GROUP + j + 1],
                         lhsT=q_t_of[group][:, i, :],
                         rhs=stand_in[:, h : h + 1],
                         start=True,
@@ -232,12 +236,10 @@ def tile_scaleddotproductattention_pa_kernel(
 
         def take_small_products(next_group, heads, group):
             bank = in_psum["small"]
-            if group is not None:
-                stand_in_scores = stats.tile([P, GROUP], F32)
-                first = with_stand_in(group)[0]
-                nc.scalar.copy(
-                    out=stand_in_scores[:, first:GROUP], in_=bank[:, Q_WORDS + GROUP + first : Q_WORDS + 2 * GROUP]
-                )
+            if group is not None and with_stand_in(group):
+                count = len(with_stand_in(group))
+                stand_in_scores = stats.tile([P, count], F32)
+                nc.scalar.copy(out=stand_in_scores[:], in_=bank[:, Q_WORDS + GROUP : Q_WORDS + GROUP + count])
                 stand_in_scores_of[group] = stand_in_scores
             if heads:
                 mean = stats.tile([P, len(heads)], F32)
@@ -253,8 +255,8 @@ def tile_scaleddotproductattention_pa_kernel(
                     in_=bank[:, 0:Q_WORDS].bitcast(BF16).rearrange("p (i q) -> p i q", i=GROUP),
                 )
                 q_t_of[next_group] = q_t
-            if heads:
-                nc.scalar.copy(out=stand_in[:, heads[0] : heads[-1] + 1], in_=mean[:])
+            for j, h in enumerate(heads):
+                nc.scalar.copy(out=stand_in[:, h : h + 1], in_=mean[:, j : j + 1])
 
         def make_rows(h):
             stand_in_rows = work.tile([P, SEQ], BF16)
@@ -263,23 +265,24 @@ def tile_scaleddotproductattention_pa_kernel(
             )
             stand_in_rows_of[h] = stand_in_rows
 
-        def transpose_k(h, half, pool, tag):
-            in_psum[("k", half)] = features_to_partitions(
-                pool, tag, k_raw_of[h][:, half * GROUP : (half + 1) * GROUP, :]
-            )
+        def transpose_k(h, half):
+            flipped_k = psum.tile([P, GROUP, P], BF16, tag="bank")
+            for i in range(GROUP):
+                nc.tensor.transpose(flipped_k[:, i, :], k_raw_of[h][:, half * GROUP + i, :], ident_bf16[:])
+            in_psum[("k", half)] = flipped_k
 
         def take_k(h, half):
             keys = slice(half * BANK, (half + 1) * BANK)
-            if h in UNPREPARED:
-                copy = nc.vector.tensor_copy if half == 0 else nc.scalar.copy
-                copy(out=k_t[:, h, keys], in_=in_psum[("k", half)][:].rearrange("p i s -> p (i s)"))
+            if h in WITH_STAND_IN:
+                nc.vector.tensor_tensor(
+                    out=k_t[:, h, keys],
+                    in0=in_psum[("k", half)][:].rearrange("p i s -> p (i s)"),
+                    in1=stand_in_rows_of[h][:, keys],
+                    op=ALU.add,
+                )
                 return
-            nc.vector.tensor_tensor(
-                out=k_t[:, h, keys],
-                in0=in_psum[("k", half)][:].rearrange("p i s -> p (i s)"),
-                in1=stand_in_rows_of[h][:, keys],
-                op=ALU.add,
-            )
+            copy = nc.vector.tensor_copy if half == 0 else nc.scalar.copy
+            copy(out=k_t[:, h, keys], in_=in_psum[("k", half)][:].rearrange("p i s -> p (i s)"))
 
         v_grouped_of = {}
 
@@ -344,53 +347,41 @@ def tile_scaleddotproductattention_pa_kernel(
         a_mx_of = {}
         o_t_of = {}
         c_grouped_of = {}
+        pair_sums_of = {}
 
-        def masked_by_tensor(place):
-            h, queries = head_and_queries(place)
-            return h in UNPREPARED or place in ALSO_BY_TENSOR
+        def masked_in_psum(place):
+            return head_of(place) not in WITH_STAND_IN
 
-        def keep_warm(bank):
-            moving = slice(0, 2)
-            nc.tensor.matmul_mx(
-                out=bank[:, 0:WARM_N],
-                lhsT=v_codes[:, 0, 0:P].bitcast(FP8X4),
-                lhsT_scale=v_scales[:, 0, 0:P],
-                rhs=v_codes[:, moving, :].rearrange("p h w -> p (h w)")[:, 0:WARM_N].bitcast(FP8X4),
-                rhs_scale=v_scales[:, moving, :].rearrange("p h w -> p (h w)")[:, 0:WARM_N],
-                start=True,
-                stop=True,
-            )
+        def emptied_by_scalar(place):
+            return masked_in_psum(place) and place % GROUP not in EMPTY_ON_VECTOR
 
         def scores(place):
-            h, queries = head_and_queries(place)
+            h = head_of(place)
             group, i = divmod(place, GROUP)
             halves = []
             for half in range(KEY_HALVES):
-                score = score_psum.tile([P, BANK], F32, tag="score")
-                if half in WARM_HALVES and place >= WARM_FROM:
-                    keep_warm(score)
+                score = psum.tile([P, BANK], F32, tag="bank")
                 nc.tensor.matmul(
                     score[:],
                     lhsT=q_t_of[group][:, i, :],
                     rhs=k_t[:, h, half * BANK : (half + 1) * BANK],
                     start=True,
-                    stop=not masked_by_tensor(place),
+                    stop=not masked_in_psum(place),
                 )
-                if masked_by_tensor(place):
-                    nc.tensor.matmul(
-                        score[:],
-                        lhsT=neg_ident[:],
-                        rhs=masked_rows[:, half * BANK : (half + 1) * BANK],
-                        start=False,
-                        stop=True,
-                    )
                 halves.append(score)
+                if masked_in_psum(place):
+                    for b in range(GROUP):
+                        nc.tensor.matmul(
+                            score[:, b * P : (b + 1) * P],
+                            lhsT=neg_columns[:, half * GROUP + b, :],
+                            rhs=ident_f32[:],
+                            start=False,
+                            stop=(b == GROUP - 1),
+                            is_transpose=True,
+                        )
             scores_of[place] = halves
 
         def row_maximum(place):
-            if folded(place):
-                fold(place)
-                return
             maxima = stats.tile([P, KEY_HALVES], F32)
             for half in range(KEY_HALVES):
                 nc.vector.tensor_reduce(
@@ -402,42 +393,7 @@ def tile_scaleddotproductattention_pa_kernel(
                 )
             maxima_of[place] = maxima
 
-        hi_bf16_of = {}
-        folded_of = {}
-
-        def folded(place):
-            return place % GROUP in FOLDED and FOLD_FROM <= place < END - 1 and not masked_by_tensor(place)
-
-        def copy_hi(place):
-            hi_bf16 = work.tile([P, BANK], BF16)
-            nc.scalar.copy(out=hi_bf16[:], in_=scores_of[place][1][:])
-            hi_bf16_of[place] = hi_bf16
-
-        def fold(place):
-            fold_bf16 = work.tile([P, BANK], BF16)
-            nc.vector.tensor_tensor(
-                out=fold_bf16[:], in0=scores_of[place][0][:], in1=hi_bf16_of[place][:], op=ALU.max
-            )
-            folded_of[place] = fold_bf16
-
-        def fold_maximum(place):
-            neg_max = stats.tile([P, 1], F32)
-            scrap = work.tile([P, BANK], BF16)
-            nc.vector.tensor_scalar(
-                out=scrap[:],
-                in0=folded_of[place][:],
-                scalar1=-SCALE,
-                scalar2=None,
-                op0=ALU.mult,
-                op1=ALU.min,
-                accum_out=neg_max[:],
-            )
-            neg_max_of[place] = neg_max
-
         def join_maxima(place):
-            if folded(place):
-                fold_maximum(place)
-                return
             maxima = maxima_of[place]
             neg_max = stats.tile([P, 1], F32)
             nc.vector.tensor_scalar(
@@ -453,13 +409,14 @@ def tile_scaleddotproductattention_pa_kernel(
                 pair_sums_of[place // PAIR] = pair_sums
             pair_sums = pair_sums_of[place // PAIR]
             first = pair_sums[:, j, 0:1]
-            if not masked_by_tensor(place):
+            if not masked_in_psum(place):
                 first_raw = stats.tile([P, 1], F32)
                 first = first_raw[:]
                 stand_in_exp = stats.tile([P, 1], F32)
+                n = with_stand_in(group).index(i)
                 nc.scalar.activation(
                     out=stand_in_exp[:],
-                    in_=stand_in_scores_of[group][:, i : i + 1],
+                    in_=stand_in_scores_of[group][:, n : n + 1],
                     func=ACT.Exp,
                     bias=neg_max_of[place][:],
                     scale=SCALE,
@@ -475,26 +432,9 @@ def tile_scaleddotproductattention_pa_kernel(
                     accum_out=first if half == 0 else pair_sums[:, j, 1:2],
                 )
             weights_of[place] = weights
-            if not masked_by_tensor(place):
-                if T_ON_SCALAR:
-                    nc.scalar.activation(
-                        out=pair_sums[:, j, 0:1], in_=stand_in_exp[:], func=ACT.Identity, scale=neg_masked[:], bias=first
-                    )
-                stand_in_of[place] = (stand_in_exp, first)
-
-        pair_sums_of = {}
-        stand_in_of = {}
-
-        def take_off_masked(place):
-            if not masked_by_tensor(place) and not T_ON_SCALAR:
-                stand_in_exp, first = stand_in_of[place]
-                nc.vector.tensor_scalar(
-                    out=pair_sums_of[place // PAIR][:, place % PAIR, 0:1],
-                    in0=stand_in_exp[:],
-                    scalar1=neg_masked[:],
-                    scalar2=first,
-                    op0=ALU.mult,
-                    op1=ALU.add,
+            if not masked_in_psum(place):
+                nc.scalar.activation(
+                    out=pair_sums[:, j, 0:1], in_=stand_in_exp[:], func=ACT.Identity, scale=neg_masked[:], bias=first
                 )
 
         def join_sums(pair):
@@ -510,9 +450,10 @@ def tile_scaleddotproductattention_pa_kernel(
             inv_sum_of[pair] = inv_sums
 
         def normaliser(place):
-            if place in AT_THE_END:
-                return AT_THE_END[place]
-            return "scalar" if place % GROUP in ON_SCALAR and place // GROUP in range(SCALAR_FROM, SCALAR_TO) else "gpsimd"
+            if place >= END - LAST_ON_VECTOR:
+                return "vector"
+            on_scalar = place % GROUP in NORM_ON_SCALAR and place // GROUP < NORM_ON_SCALAR_GROUPS
+            return "scalar" if on_scalar else "gpsimd"
 
         def normalise(place):
             a_bf16 = work.tile([P, SEQ], BF16, bufs=4)
@@ -521,7 +462,7 @@ def tile_scaleddotproductattention_pa_kernel(
             inv_sum = inv_sum_of[place // PAIR][:, j : j + 1]
             if normaliser(place) == "gpsimd":
                 nc.gpsimd.tensor_scalar(
-                    out=a_bf16[:], in0=weights[:], scalar1=inv_sum, scalar2=any_valid[:], op0=ALU.mult, op1=ALU.mult
+                    out=a_bf16[:], in0=weights[:], scalar1=inv_sum, scalar2=1.0, op0=ALU.mult, op1=ALU.mult
                 )
             elif normaliser(place) == "scalar":
                 nc.scalar.activation(out=a_bf16[:], in_=weights[:], func=ACT.Copy, scale=inv_sum)
@@ -531,7 +472,7 @@ def tile_scaleddotproductattention_pa_kernel(
 
         def keys_to_partitions(place):
             a_words = a_bf16_of[place][:].bitcast(F32)
-            flipped = score_psum.tile([P, 2, KEY_PASSES * P], F32, tag="score")
+            flipped = psum.tile([P, 2, KEY_PASSES * P], F32, tag="bank")
             for g in range(KEY_PASSES):
                 for u in range(2):
                     c = 2 * g + u
@@ -540,13 +481,14 @@ def tile_scaleddotproductattention_pa_kernel(
                     )
             flipped_of[place] = flipped
 
-        def mask_weights(place):
+        def empty(place):
             group, i = divmod(place, GROUP)
             if i == 0:
-                a_grouped = work.tile([P, GROUP, KEY_PASSES * P * PACK], BF16, align_bytes=64)
+                a_grouped = work.tile([P, GROUP, KEY_PASSES * P * PACK], BF16, align_bytes=64, bufs=3)
                 a_grouped_of[group] = a_grouped
-            if masked_by_tensor(place):
-                nc.scalar.copy(
+            if masked_in_psum(place):
+                copy = nc.scalar.copy if emptied_by_scalar(place) else nc.vector.tensor_copy
+                copy(
                     out=a_grouped_of[group][:, i, :].bitcast(F32).rearrange("p (x u) -> p x u", u=2),
                     in_=flipped_of[place][:].rearrange("p u x -> p x u"),
                 )
@@ -572,11 +514,11 @@ def tile_scaleddotproductattention_pa_kernel(
 
         def weighted_values(group, first, last):
             if first == 0:
-                o_t = score_psum.tile([P, GROUP, P], F32, tag="score", name="o_t")
+                o_t = psum.tile([P, GROUP, P], F32, tag="bank", name="o_t")
                 o_t_of[group] = o_t
             a_codes, a_scales = a_mx_of[group]
             for i in range(first, last):
-                h, queries = head_and_queries(group * GROUP + i)
+                h = head_of(group * GROUP + i)
                 for g in range(KEY_PASSES):
                     block = slice(g * P, (g + 1) * P)
                     nc.tensor.matmul_mx(
@@ -591,15 +533,16 @@ def tile_scaleddotproductattention_pa_kernel(
 
         def take_values(group):
             c_grouped = work.tile([P, P * PACK], BF16, align_bytes=64)
-            parts = 1 if group != LAST or not SPLIT_TAIL else 2
+            parts = 1 if group != LAST else 2
             width = P // parts
             for part in range(parts):
-                copy = nc.scalar.copy if part == 0 else nc.vector.tensor_copy
                 some = slice(part * width, (part + 1) * width)
-                copy(
-                    out=c_grouped[:].rearrange("p (q i) -> p q i", i=PACK)[:, some, :],
-                    in_=o_t_of[group][:].rearrange("p i q -> p q i")[:, some, :],
-                )
+                there = c_grouped[:].rearrange("p (q i) -> p q i", i=PACK)[:, some, :]
+                here = o_t_of[group][:].rearrange("p i q -> p q i")[:, some, :]
+                if part == 0:
+                    nc.scalar.activation(out=there, in_=here, func=ACT.Copy, scale=any_valid[:])
+                else:
+                    nc.vector.tensor_scalar(out=there, in0=here, scalar1=any_valid[:], scalar2=None, op0=ALU.mult)
             c_grouped_of[group] = c_grouped
 
         def quantise_heads(group):
@@ -609,10 +552,10 @@ def tile_scaleddotproductattention_pa_kernel(
                 out=c_codes[:, g, queries].bitcast(FP8X4), scales=c_scales[:, g, queries], in_=c_grouped_of[group][:]
             )
 
-        def project(t, half, pool, tag):
+        def project(t, half):
             queries = slice(t * P, (t + 1) * P)
             cols = slice(half * BANK, (half + 1) * BANK)
-            acc = pool.tile([P, BANK], F32, tag=tag, name="acc")
+            acc = psum.tile([P, BANK], F32, tag="bank")
             for g in range(FEATURE_PASSES):
                 nc.tensor.matmul_mx(
                     out=acc[:],
@@ -627,9 +570,8 @@ def tile_scaleddotproductattention_pa_kernel(
 
         def take_result(t, half, on_vector):
             queries = slice(t * P, (t + 1) * P)
-            cols = slice(half * BANK, (half + 1) * BANK)
             result = work.tile([P, BANK], F32, bufs=8)
-            parts = 2 if QUARTERS and groups[LAST][1] == t else 1
+            parts = 2 if groups[LAST][1] == t else 1
             width = BANK // parts
             for part in range(parts):
                 some = slice(part * width, (part + 1) * width)
@@ -653,18 +595,14 @@ def tile_scaleddotproductattention_pa_kernel(
             return place // GROUP if place is not None and place % GROUP == GROUP - 1 else None
 
         def prepare_k(h):
-            if h not in UNPREPARED:
-                make_rows(h)
             for half in range(KEY_HALVES):
-                transpose_k(h, half, score_psum, "score")
+                transpose_k(h, half)
             for half in range(KEY_HALVES):
                 take_k(h, half)
 
         small_products(0, [], None)
         take_small_products(0, [], None)
         prepare_k(0)
-        small_products(None, [1], None)
-        take_small_products(None, [1], None)
         prepare_k(1)
         for h in range(V_ON_GPSIMD):
             mask_and_group_v(h, (0, 1))
@@ -679,38 +617,34 @@ def tile_scaleddotproductattention_pa_kernel(
 
             def tensor_side_jobs():
                 if i == 0 and 0 < step < END:
-                    heads = [GROUP + group - 1] if GROUP + group - 1 < HEADS else []
+                    heads = [h for h in [GROUP + group - 1] if h in WITH_STAND_IN]
                     small_products(following, heads, group)
                     taken_next.append((take_small_products, (following, heads, group)))
-                if step == 1:
-                    small_products(None, [], 0)
-                    taken_next.append((take_small_products, (None, [], 0)))
                 h = GROUP + group - 1
                 if i in (2, 3) and GROUP <= h < HEADS:
-                    if i == 2:
+                    if i == 2 and h in WITH_STAND_IN:
                         make_rows(h)
-                    transpose_k(h, i - 2, score_psum, "score")
+                    transpose_k(h, i - 2)
                     taken_next.append((take_k, (h, i - 2)))
-                if closed_group(step, QUANT_LAG + 2) is not None and closed_group(step, QUANT_LAG + 2) < LAST - 1:
-                    weighted_values(closed_group(step, QUANT_LAG + 2), 0, GROUP)
-                    taken_next.append((take_values, (closed_group(step, QUANT_LAG + 2),)))
+                done = closed_group(step, QUANT_LAG + 2)
+                if done is not None and done < LAST - 1:
+                    weighted_values(done, 0, GROUP)
+                    taken_next.append((take_values, (done,)))
                 for half in range(2):
                     done = closed_group(step, QUANT_LAG + 7 + half if step < END else P13_AT[half])
                     if done is not None and done < LAST - 1 and groups[done][0] == FEATURE_PASSES - 1:
                         t = groups[done][1]
-                        project(t, half, score_psum, "score")
+                        project(t, half)
                         taken_next.append((take_result, (t, half, False)))
 
             if entered(step, 0) is not None:
                 scores(step)
             if step == 0:
-                small_products(1, [2, 3], None)
-                take_small_products(1, [2, 3], None)
-            if SIDE_FIRST and entered(step, FLIP_LAG) is not None:
-                keys_to_partitions(step - FLIP_LAG)
+                small_products(1, [], None)
+                take_small_products(1, [], None)
             if step < END:
                 tensor_side_jobs()
-            if not SIDE_FIRST and entered(step, FLIP_LAG) is not None:
+            if entered(step, FLIP_LAG) is not None:
                 keys_to_partitions(step - FLIP_LAG)
 
             def do_R():
@@ -724,6 +658,8 @@ def tile_scaleddotproductattention_pa_kernel(
                 if 1 <= step < GROUP - 1:
                     prepare_k(step + 1)
                 if step == GROUP - 1:
+                    count_valid_keys()
+                if step == GROUP:
                     build_key_mask()
                 h = step - V_STEP + V_ON_GPSIMD
                 if V_ON_GPSIMD <= h < GROUP:
@@ -732,18 +668,15 @@ def tile_scaleddotproductattention_pa_kernel(
             closes_pair = entered(step, NORM_LAG) is not None and step % PAIR == (NORM_LAG + PAIR - 1) % PAIR
 
             def do_T():
-                if closes_pair and EARLY_T:
-                    join_sums((step - NORM_LAG) // PAIR)
-                if entered(step, T_LAG) is not None:
-                    take_off_masked(step - T_LAG)
-                if closes_pair and not EARLY_T:
+                if closes_pair:
                     join_sums((step - NORM_LAG) // PAIR)
 
-            late_copy = COPY_LATE and entered(step, MASK_LAG) is not None and masked_by_tensor(step - MASK_LAG)
+            place_to_empty = entered(step, EMPTY_LAG)
+            late_copy = place_to_empty is not None and emptied_by_scalar(place_to_empty)
 
             def do_E():
-                if entered(step, MASK_LAG) is not None and not late_copy:
-                    mask_weights(step - MASK_LAG)
+                if place_to_empty is not None and not late_copy:
+                    empty(place_to_empty)
 
             def do_J():
                 if entered(step, 1) is not None:
@@ -760,46 +693,34 @@ def tile_scaleddotproductattention_pa_kernel(
                             normalise(place)
 
             def do_Q():
-                if closed_group(step, QUANT_LAG + 4) is not None and closed_group(step, QUANT_LAG + 4) < LAST - 1:
-                    quantise_heads(closed_group(step, QUANT_LAG + 4))
+                done = closed_group(step, QUANT_LAG + 4)
+                if done is not None and done < LAST - 1:
+                    quantise_heads(done)
                 if step == V_QUANT_STEP:
                     for h in range(GROUP):
                         quantise_v(h)
-                if closed_group(step, 0) is not None and group - 1 in prepared_in:
-                    lay_out, quantise, what = prepared_in[group - 1]
+                now = closed_group(step, QUANT_LAG - 8)
+                if now is not None and now - 1 in prepared_in:
+                    lay_out, quantise, what = prepared_in[now - 1]
                     quantise(what)
-                place = entered(step, QUANT_LAG)
-                if place is not None and place // GROUP != LAST and (place + 1) % AT_ONCE == 0:
-                    quantise_weights(place // GROUP, place % GROUP + 1 - AT_ONCE, place % GROUP + 1)
+                done = closed_group(step, QUANT_LAG)
+                if done is not None and done != LAST:
+                    quantise_weights(done, 0, GROUP)
 
             jobs = {"R": do_R, "K": do_K, "E": do_E, "J": do_J, "N": do_N, "T": do_T, "Q": do_Q}
-            order = V_ORDER_CLOSING if i == GROUP - 1 and step < END else V_ORDER
-            if entered(step, 1) is not None and folded(step - 1):
-                order = order.replace("E", "").replace("R", "ER") if E_FIRST else order
-            if step < START_STEPS:
-                order = V_ORDER_START
-            for letter in order:
+            for letter in V_ORDER_CLOSING if closed_group(step, QUANT_LAG) is not None and step < END else V_ORDER:
                 jobs[letter]()
 
-            if SC == 2 or step >= NORMS_FIRST:
-                for place in for_scalar:
-                    normalise(place)
-                for_scalar = [place for place in inverted if normaliser(place) == "scalar"]
-            if SC == 1 and entered(step, 2) is not None:
-                exponentials(step - 2)
             for take, args in take_now:
                 if take is not take_k:
                     take(*args)
-            if SC in (0, 2) and entered(step, 2) is not None:
+            if entered(step, 2) is not None:
                 exponentials(step - 2)
-            if entered(step, 0) is not None and folded(step):
-                copy_hi(step)
             if late_copy:
-                mask_weights(step - MASK_LAG)
-            if SC != 2 and step < NORMS_FIRST:
-                for place in for_scalar:
-                    normalise(place)
-                for_scalar = [place for place in inverted if normaliser(place) == "scalar"]
+                empty(place_to_empty)
+            for place in for_scalar:
+                normalise(place)
+            for_scalar = [place for place in inverted if normaliser(place) == "scalar"]
 
             if entered(step, QUANT_LAG) is not None and (step - QUANT_LAG) // GROUP == LAST:
                 j = (step - QUANT_LAG) % GROUP
@@ -810,9 +731,6 @@ def tile_scaleddotproductattention_pa_kernel(
                 weighted_values(LAST, j, j + 1)
                 if j == C14_AT:
                     quantise_heads(LAST - 1)
-                if j == P14_AT:
-                    for half in range(2):
-                        project(groups[LAST - 1][1], half, score_psum, "score")
                 if j == GROUP - 1:
                     take_values(LAST)
                     quantise_heads(LAST)
@@ -820,13 +738,12 @@ def tile_scaleddotproductattention_pa_kernel(
                 tensor_side_jobs()
             if step == END - 1 + QUANT_LAG:
                 for half in range(2):
-                    if P14_AT is None:
-                        project(groups[LAST - 1][1], half, score_psum, "score")
+                    project(groups[LAST - 1][1], half)
                     taken_next.append((take_result, (groups[LAST - 1][1], half, half == 0)))
                 for take, args in taken_next:
                     take(*args)
                 for half in range(2):
-                    project(groups[LAST][1], half, score_psum, "score")
+                    project(groups[LAST][1], half)
                 for half in range(2):
                     take_result(groups[LAST][1], half, half == 0)
 

@@ -47,6 +47,8 @@ V_ON_GPSIMD = 4
 V_STEP = 3
 V_QUANT_STEP = 7
 NORM_ON_SCALAR = (1,)
+WARM_HALVES = (1,)
+WARM_FROM = 8
 NORM_ON_SCALAR_GROUPS = 8
 EMPTY_ON_VECTOR = (3,)
 LAST_ON_VECTOR = 3
@@ -355,12 +357,26 @@ def tile_scaleddotproductattention_pa_kernel(
         def emptied_by_scalar(place):
             return masked_in_psum(place) and place % GROUP not in EMPTY_ON_VECTOR
 
+        def keep_warm(bank):
+            moving = slice(0, 2)
+            nc.tensor.matmul_mx(
+                out=bank[:],
+                lhsT=v_codes[:, 0, 0:P].bitcast(FP8X4),
+                lhsT_scale=v_scales[:, 0, 0:P],
+                rhs=v_codes[:, moving, :].rearrange("p h w -> p (h w)").bitcast(FP8X4),
+                rhs_scale=v_scales[:, moving, :].rearrange("p h w -> p (h w)"),
+                start=True,
+                stop=True,
+            )
+
         def scores(place):
             h = head_of(place)
             group, i = divmod(place, GROUP)
             halves = []
             for half in range(KEY_HALVES):
                 score = psum.tile([P, BANK], F32, tag="bank")
+                if half in WARM_HALVES and place >= WARM_FROM:
+                    keep_warm(score)
                 nc.tensor.matmul(
                     score[:],
                     lhsT=q_t_of[group][:, i, :],
@@ -369,10 +385,11 @@ def tile_scaleddotproductattention_pa_kernel(
                     stop=not masked_in_psum(place),
                 )
                 halves.append(score)
-                if masked_in_psum(place):
+            if masked_in_psum(place):
+                for half in range(KEY_HALVES):
                     for b in range(GROUP):
                         nc.tensor.matmul(
-                            score[:, b * P : (b + 1) * P],
+                            halves[half][:, b * P : (b + 1) * P],
                             lhsT=neg_columns[:, half * GROUP + b, :],
                             rhs=ident_f32[:],
                             start=False,
@@ -642,10 +659,10 @@ def tile_scaleddotproductattention_pa_kernel(
             if step == 0:
                 small_products(1, [], None)
                 take_small_products(1, [], None)
-            if step < END:
-                tensor_side_jobs()
             if entered(step, FLIP_LAG) is not None:
                 keys_to_partitions(step - FLIP_LAG)
+            if step < END:
+                tensor_side_jobs()
 
             def do_R():
                 if entered(step, 1) is not None:
@@ -655,11 +672,11 @@ def tile_scaleddotproductattention_pa_kernel(
                 for take, args in take_now:
                     if take is take_k:
                         take(*args)
-                if 1 <= step < GROUP - 1:
-                    prepare_k(step + 1)
-                if step == GROUP - 1:
+                if step + 2 < GROUP:
+                    prepare_k(step + 2)
+                if step == GROUP + 1:
                     count_valid_keys()
-                if step == GROUP:
+                if step == 2 * GROUP:
                     build_key_mask()
                 h = step - V_STEP + V_ON_GPSIMD
                 if V_ON_GPSIMD <= h < GROUP:

@@ -41,16 +41,19 @@ EMPTY_LAG = 8
 QUANT_LAG = 8
 NORM_LAG = 4
 SIDE_AT = {1: (0,), 3: (1,)}
-V_ORDER = "RKTEJNQ"
-V_ORDER_CLOSING = "RKTEJQN"
+V_ORDER = "ERTKJNQ"
+V_ORDER_CLOSING = "RKTEJNQ"
 V_ON_GPSIMD = 4
-V_STEP = 3
+V_STEP = 2
 V_QUANT_STEP = 7
-NORM_ON_SCALAR = (1,)
-WARM_HALVES = (1,)
-WARM_FROM = 8
-NORM_ON_SCALAR_GROUPS = 8
-EMPTY_ON_VECTOR = (3,)
+NORM_ON_SCALAR = ((1, 3), ())
+EMPTY_ON_SCALAR = ((0, 1), (0, 2))
+V_HEAD_G = 3
+PROJECT_LAG = 7
+FLIPS_FIRST = False
+V_LOAD_EARLY = False
+V_JOB_AT = (((1, 1), (1, 3)), ((2, 1), (2, 3)), ((3, 1), (3, 3)), ((4, 1), (4, 3)))
+WO_JOB_AT = (((4, 1), (4, 3)), ((5, 1), (5, 3)), ((6, 1), (6, 3)), ((7, 1), (7, 3)))
 LAST_ON_VECTOR = 3
 P13_AT = (15, 16)
 C14_AT = 3
@@ -115,17 +118,20 @@ def tile_scaleddotproductattention_pa_kernel(
 
         ind_k_blocks = const.tile([P, P], BF16)
         nc.vector.memset(ind_k_blocks[:], 0.0)
-        nc.scalar.dma_start(out=ind_k_blocks[0:KEY_BLOCKS, :], in_=ind_k[0].rearrange("(b p) -> b p", p=P))
+        nc.sync.dma_start(out=ind_k_blocks[0:KEY_BLOCKS, :], in_=ind_k[0].rearrange("(b p) -> b p", p=P))
         load_k(0)
         load_q(0)
-        for h in range(1, GROUP):
-            load_k(h)
+        load_k(1)
+        load_v(0)
+        load_k(2)
+        load_v(1)
+        load_k(3)
         ind_v_words = const.tile([P, 2 * KEY_PASSES, 2], BF16)
         nc.scalar.dma_start(out=ind_v_words[:], in_=ind_v[0].rearrange("(c p e) -> p c e", p=P, e=2))
         ind_k_words = const.tile([P, 2 * KEY_PASSES, 2], BF16)
         nc.scalar.dma_start(out=ind_k_words[:], in_=ind_k[0].rearrange("(c p e) -> p c e", p=P, e=2))
         load_q(1)
-        for h in range(GROUP):
+        for h in range(2, GROUP):
             load_v(h)
         ind_k_rows = const.tile([P, SEQ], BF16)
         nc.scalar.dma_start(out=ind_k_rows[:], in_=ind_k[0].partition_broadcast(P))
@@ -185,6 +191,11 @@ def tile_scaleddotproductattention_pa_kernel(
         key_mask = const.tile([P, KEY_PASSES, P, PACK], BF16)
         masked_rows = const.tile([P, SEQ], BF16)
 
+        def build_masked_rows():
+            nc.vector.tensor_scalar(
+                out=masked_rows[:], in0=ind_k_rows[:], scalar1=-1.0, scalar2=1.0, op0=ALU.mult, op1=ALU.add
+            )
+
         def build_key_mask():
             nc.vector.tensor_copy(
                 out=key_mask[:],
@@ -192,9 +203,6 @@ def tile_scaleddotproductattention_pa_kernel(
                 .rearrange("p (g u) e -> p g (u e)", u=2)
                 .unsqueeze(2)
                 .to_broadcast([P, KEY_PASSES, P, PACK]),
-            )
-            nc.vector.tensor_scalar(
-                out=masked_rows[:], in0=ind_k_rows[:], scalar1=-1.0, scalar2=1.0, op0=ALU.mult, op1=ALU.add
             )
 
         in_psum = {}
@@ -271,20 +279,20 @@ def tile_scaleddotproductattention_pa_kernel(
             flipped_k = psum.tile([P, GROUP, P], BF16, tag="bank")
             for i in range(GROUP):
                 nc.tensor.transpose(flipped_k[:, i, :], k_raw_of[h][:, half * GROUP + i, :], ident_bf16[:])
-            in_psum[("k", half)] = flipped_k
+            in_psum[("k", h, half)] = flipped_k
 
         def take_k(h, half):
             keys = slice(half * BANK, (half + 1) * BANK)
             if h in WITH_STAND_IN:
                 nc.vector.tensor_tensor(
                     out=k_t[:, h, keys],
-                    in0=in_psum[("k", half)][:].rearrange("p i s -> p (i s)"),
+                    in0=in_psum[("k", h, half)][:].rearrange("p i s -> p (i s)"),
                     in1=stand_in_rows_of[h][:, keys],
                     op=ALU.add,
                 )
                 return
             copy = nc.vector.tensor_copy if half == 0 else nc.scalar.copy
-            copy(out=k_t[:, h, keys], in_=in_psum[("k", half)][:].rearrange("p i s -> p (i s)"))
+            copy(out=k_t[:, h, keys], in_=in_psum[("k", h, half)][:].rearrange("p i s -> p (i s)"))
 
         v_grouped_of = {}
 
@@ -355,19 +363,7 @@ def tile_scaleddotproductattention_pa_kernel(
             return head_of(place) not in WITH_STAND_IN
 
         def emptied_by_scalar(place):
-            return masked_in_psum(place) and place % GROUP not in EMPTY_ON_VECTOR
-
-        def keep_warm(bank):
-            moving = slice(0, 2)
-            nc.tensor.matmul_mx(
-                out=bank[:],
-                lhsT=v_codes[:, 0, 0:P].bitcast(FP8X4),
-                lhsT_scale=v_scales[:, 0, 0:P],
-                rhs=v_codes[:, moving, :].rearrange("p h w -> p (h w)").bitcast(FP8X4),
-                rhs_scale=v_scales[:, moving, :].rearrange("p h w -> p (h w)"),
-                start=True,
-                stop=True,
-            )
+            return masked_in_psum(place) and place % GROUP in EMPTY_ON_SCALAR[groups[place // GROUP][0]]
 
         def scores(place):
             h = head_of(place)
@@ -375,8 +371,6 @@ def tile_scaleddotproductattention_pa_kernel(
             halves = []
             for half in range(KEY_HALVES):
                 score = psum.tile([P, BANK], F32, tag="bank")
-                if half in WARM_HALVES and place >= WARM_FROM:
-                    keep_warm(score)
                 nc.tensor.matmul(
                     score[:],
                     lhsT=q_t_of[group][:, i, :],
@@ -469,8 +463,7 @@ def tile_scaleddotproductattention_pa_kernel(
         def normaliser(place):
             if place >= END - LAST_ON_VECTOR:
                 return "vector"
-            on_scalar = place % GROUP in NORM_ON_SCALAR and place // GROUP < NORM_ON_SCALAR_GROUPS
-            return "scalar" if on_scalar else "gpsimd"
+            return "scalar" if place % GROUP in NORM_ON_SCALAR[groups[place // GROUP][0]] else "gpsimd"
 
         def normalise(place):
             a_bf16 = work.tile([P, SEQ], BF16, bufs=4)
@@ -598,11 +591,28 @@ def tile_scaleddotproductattention_pa_kernel(
                 nc.sync.dma_start(out=out[0, queries, there], in_=result[:, some])
 
 
-        prepared_in = {}
-        for h in range(GROUP, HEADS):
-            prepared_in[h - GROUP] = (mask_and_group_v, quantise_v, h)
+        side_jobs = {}
+        for n, h in enumerate(range(GROUP, HEADS)):
+            for part in range(2):
+                side_jobs.setdefault(V_JOB_AT[n][part][0], []).append(
+                    (V_JOB_AT[n][part][1], mask_and_group_v, quantise_v, h, part)
+                )
         for piece in range(WO_PIECES):
-            prepared_in[GROUP + piece] = (group_wo, quantise_wo, piece)
+            for part in range(2):
+                side_jobs.setdefault(WO_JOB_AT[piece][part][0], []).append(
+                    (WO_JOB_AT[piece][part][1], group_wo, quantise_wo, piece, part)
+                )
+        to_quantise = []
+
+        done = {"flip": 0, "empty": 0, "quant": 0, "values": 0, "heads": 0, "project": 0}
+
+        def flip_to(place):
+            while done["flip"] <= min(place, END - 1):
+                keys_to_partitions(done["flip"])
+                done["flip"] += 1
+
+        taken_next = []
+        for_scalar = []
 
         def entered(step, lag):
             return step - lag if 0 <= step - lag < END else None
@@ -611,58 +621,82 @@ def tile_scaleddotproductattention_pa_kernel(
             place = entered(step, lag)
             return place // GROUP if place is not None and place % GROUP == GROUP - 1 else None
 
+        def prepare_stand_in(h):
+            if h in WITH_STAND_IN:
+                small_products(None, [h], None)
+                take_small_products(None, [h], None)
+                make_rows(h)
+
         def prepare_k(h):
+            prepare_stand_in(h)
             for half in range(KEY_HALVES):
                 transpose_k(h, half)
             for half in range(KEY_HALVES):
                 take_k(h, half)
 
+        EARLY = [h for h in WITH_STAND_IN if h < GROUP]
+        for half in range(KEY_HALVES):
+            transpose_k(0, half)
         small_products(0, [], None)
+        for half in range(KEY_HALVES):
+            take_k(0, half)
         take_small_products(0, [], None)
-        prepare_k(0)
+        if EARLY:
+            count_valid_keys()
+            build_masked_rows()
         prepare_k(1)
-        for h in range(V_ON_GPSIMD):
+        for h in range(V_HEAD_G):
             mask_and_group_v(h, (0, 1))
 
-        taken_next = []
-        for_scalar = []
-
-        for step in range(END + QUANT_LAG):
-            take_now, taken_next = taken_next, []
+        def step_of(step):
+            take_now = list(taken_next)
+            taken_next.clear()
             group, i = divmod(step, GROUP)
             following = group + 1 if group < LAST else None
 
             def tensor_side_jobs():
-                if i == 0 and 0 < step < END:
+                if i == 0 and step > 0:
                     heads = [h for h in [GROUP + group - 1] if h in WITH_STAND_IN]
                     small_products(following, heads, group)
                     taken_next.append((take_small_products, (following, heads, group)))
+                if step == 0 and EARLY:
+                    small_products(None, [], 0)
+                    taken_next.append((take_small_products, (None, [], 0)))
+                h = step + 2
+                if h < GROUP:
+                    prepare_stand_in(h)
+                    for half in range(KEY_HALVES):
+                        transpose_k(h, half)
+                        taken_next.append((take_k, (h, half)))
                 h = GROUP + group - 1
                 if i in (2, 3) and GROUP <= h < HEADS:
                     if i == 2 and h in WITH_STAND_IN:
                         make_rows(h)
                     transpose_k(h, i - 2)
                     taken_next.append((take_k, (h, i - 2)))
-                done = closed_group(step, QUANT_LAG + 2)
-                if done is not None and done < LAST - 1:
-                    weighted_values(done, 0, GROUP)
-                    taken_next.append((take_values, (done,)))
+                ready = closed_group(step, QUANT_LAG + 2)
+                if ready is not None:
+                    weighted_values(ready, 0, GROUP)
+                    done["values"] = ready + 1
+                    taken_next.append((take_values, (ready,)))
                 for half in range(2):
-                    done = closed_group(step, QUANT_LAG + 7 + half if step < END else P13_AT[half])
-                    if done is not None and done < LAST - 1 and groups[done][0] == FEATURE_PASSES - 1:
-                        t = groups[done][1]
+                    ready = closed_group(step, QUANT_LAG + PROJECT_LAG + half)
+                    if ready is not None and groups[ready][0] == FEATURE_PASSES - 1:
+                        t = groups[ready][1]
                         project(t, half)
+                        if half == 1:
+                            done["project"] = t + 1
                         taken_next.append((take_result, (t, half, False)))
 
-            if entered(step, 0) is not None:
-                scores(step)
-            if step == 0:
+            if FLIPS_FIRST:
+                flip_to(step - FLIP_LAG)
+            scores(step)
+            if step == 1:
                 small_products(1, [], None)
-                take_small_products(1, [], None)
-            if entered(step, FLIP_LAG) is not None:
-                keys_to_partitions(step - FLIP_LAG)
-            if step < END:
-                tensor_side_jobs()
+                taken_next.append((take_small_products, (1, [], None)))
+            if not FLIPS_FIRST:
+                flip_to(step - FLIP_LAG)
+            tensor_side_jobs()
 
             def do_R():
                 if entered(step, 1) is not None:
@@ -672,14 +706,13 @@ def tile_scaleddotproductattention_pa_kernel(
                 for take, args in take_now:
                     if take is take_k:
                         take(*args)
-                if step + 2 < GROUP:
-                    prepare_k(step + 2)
-                if step == GROUP + 1:
+                if step == GROUP + 1 and not EARLY:
                     count_valid_keys()
-                if step == 2 * GROUP:
+                    build_masked_rows()
+                if step == (GROUP if EARLY else 2 * GROUP):
                     build_key_mask()
-                h = step - V_STEP + V_ON_GPSIMD
-                if V_ON_GPSIMD <= h < GROUP:
+                h = V_HEAD_G + step - V_STEP
+                if V_HEAD_G <= h < GROUP and step >= V_STEP:
                     mask_and_group_v(h, (0, 1), nc.vector)
 
             closes_pair = entered(step, NORM_LAG) is not None and step % PAIR == (NORM_LAG + PAIR - 1) % PAIR
@@ -692,8 +725,10 @@ def tile_scaleddotproductattention_pa_kernel(
             late_copy = place_to_empty is not None and emptied_by_scalar(place_to_empty)
 
             def do_E():
-                if place_to_empty is not None and not late_copy:
-                    empty(place_to_empty)
+                if place_to_empty is not None:
+                    done["empty"] = place_to_empty + 1
+                    if not late_copy:
+                        empty(place_to_empty)
 
             def do_J():
                 if entered(step, 1) is not None:
@@ -705,27 +740,34 @@ def tile_scaleddotproductattention_pa_kernel(
                 if closes_pair:
                     invert_sums((step - NORM_LAG) // PAIR)
                     inverted.extend([step - NORM_LAG - PAIR + 1 + j for j in range(PAIR)])
-                    for place in inverted:
-                        if normaliser(place) != "scalar":
-                            normalise(place)
+                    for engine in ("vector", "gpsimd"):
+                        for place in inverted:
+                            if normaliser(place) == engine:
+                                normalise(place)
 
             def do_Q():
-                done = closed_group(step, QUANT_LAG + 4)
-                if done is not None and done < LAST - 1:
-                    quantise_heads(done)
+                ready = closed_group(step, QUANT_LAG)
+                if ready is None:
+                    if step == V_QUANT_STEP:
+                        for h in range(GROUP):
+                            quantise_v(h)
+                    return
                 if step == V_QUANT_STEP:
                     for h in range(GROUP):
                         quantise_v(h)
-                now = closed_group(step, QUANT_LAG - 8)
-                if now is not None and now - 1 in prepared_in:
-                    lay_out, quantise, what = prepared_in[now - 1]
-                    quantise(what)
-                done = closed_group(step, QUANT_LAG)
-                if done is not None and done != LAST:
-                    quantise_weights(done, 0, GROUP)
+                earlier = closed_group(step, QUANT_LAG + 4)
+                if earlier is not None:
+                    quantise_heads(earlier)
+                    done["heads"] = earlier + 1
+                for issued, quantise, what in list(to_quantise):
+                    if issued < step:
+                        quantise(what)
+                        to_quantise.remove((issued, quantise, what))
+                quantise_weights(ready, 0, GROUP)
+                done["quant"] = ready + 1
 
             jobs = {"R": do_R, "K": do_K, "E": do_E, "J": do_J, "N": do_N, "T": do_T, "Q": do_Q}
-            for letter in V_ORDER_CLOSING if closed_group(step, QUANT_LAG) is not None and step < END else V_ORDER:
+            for letter in V_ORDER_CLOSING if closed_group(step, QUANT_LAG) is not None else V_ORDER:
                 jobs[letter]()
 
             for take, args in take_now:
@@ -737,41 +779,112 @@ def tile_scaleddotproductattention_pa_kernel(
                 empty(place_to_empty)
             for place in for_scalar:
                 normalise(place)
-            for_scalar = [place for place in inverted if normaliser(place) == "scalar"]
-
-            if entered(step, QUANT_LAG) is not None and (step - QUANT_LAG) // GROUP == LAST:
-                j = (step - QUANT_LAG) % GROUP
-                quantise_weights(LAST, j, j + 1)
-                if j == 0:
-                    weighted_values(LAST - 1, 0, GROUP)
-                    take_values(LAST - 1)
-                weighted_values(LAST, j, j + 1)
-                if j == C14_AT:
-                    quantise_heads(LAST - 1)
-                if j == GROUP - 1:
-                    take_values(LAST)
-                    quantise_heads(LAST)
-            if step >= END:
-                tensor_side_jobs()
-            if step == END - 1 + QUANT_LAG:
-                for half in range(2):
-                    project(groups[LAST - 1][1], half)
-                    taken_next.append((take_result, (groups[LAST - 1][1], half, half == 0)))
-                for take, args in taken_next:
-                    take(*args)
-                for half in range(2):
-                    project(groups[LAST][1], half)
-                for half in range(2):
-                    take_result(groups[LAST][1], half, half == 0)
+            for_scalar.clear()
+            for_scalar.extend([place for place in inverted if normaliser(place) == "scalar"])
 
             if i == 0 and group + 2 < len(groups):
                 load_q(group + 2)
             if i == 0 and GROUP <= GROUP + group < HEADS:
                 load_k(GROUP + group)
-            if i == 1 and GROUP <= GROUP + group < HEADS:
-                load_v(GROUP + group)
-            if i == 0 and group - 3 in range(FEATURE_PASSES):
-                load_wo(group - 3)
-            if group in prepared_in and step < END and i in SIDE_AT:
-                lay_out, quantise, what = prepared_in[group]
-                lay_out(what, SIDE_AT[i])
+            for n, h in enumerate(range(GROUP, HEADS)):
+                if i == 1 and group == max(0, V_JOB_AT[n][0][0] - 1 if V_LOAD_EARLY else V_JOB_AT[n][0][0]):
+                    load_v(h)
+            for g in range(FEATURE_PASSES):
+                if i == 0 and group == WO_JOB_AT[2 * g][0][0] - 1:
+                    load_wo(g)
+            for at, lay_out, quantise, what, part in side_jobs.get(group, []):
+                if at == i:
+                    lay_out(what, (part,))
+                    if part == 1:
+                        to_quantise.append((step, quantise, what))
+
+        for step in range(END):
+            step_of(step)
+
+        def empty_to(place):
+            while done["empty"] <= place:
+                empty(done["empty"])
+                done["empty"] += 1
+
+        def quantise_to(group):
+            while done["quant"] <= group:
+                quantise_weights(done["quant"], 0, GROUP)
+                done["quant"] += 1
+
+        def values_to(group):
+            started = list(range(done["values"], group + 1))
+            for g in started:
+                weighted_values(g, 0, GROUP)
+            done["values"] = max(done["values"], group + 1)
+            return started
+
+        def heads_to(group):
+            while done["heads"] <= group:
+                quantise_heads(done["heads"])
+                done["heads"] += 1
+
+        def out_of_psum(t, on_vector):
+            for half in range(2):
+                take_result(t, half, on_vector[half])
+
+        def project_both(t):
+            for half in range(2):
+                project(t, half)
+
+        a, b, c, d = range(END - GROUP, END)
+        pair = (END - GROUP) // PAIR
+        order_of_t = [t for g, t in groups if g == FEATURE_PASSES - 1]
+        T4, T5, T6, T7 = order_of_t[-4:]
+
+        for take, args in taken_next:
+            take(*args)
+        for place in for_scalar:
+            normalise(place)
+        flip_to(a - 2)
+        row_maximum(d)
+        exponentials(c)
+        empty_to(a - 4)
+        join_maxima(d)
+        exponentials(d)
+        quantise_to(LAST - 2)
+        started = values_to(LAST - 2)
+        join_sums(pair)
+        empty_to(a - 3)
+        invert_sums(pair)
+        normalise(a)
+        normalise(b)
+        for g in started:
+            take_values(g)
+        flip_to(a - 1)
+        if done["project"] <= T4:
+            heads_to(LAST - 3)
+            project_both(T4)
+        empty_to(a - 1)
+        flip_to(b)
+        join_sums(pair + 1)
+        invert_sums(pair + 1)
+        normalise(c)
+        normalise(d)
+        heads_to(LAST - 2)
+        quantise_to(LAST - 1)
+        flip_to(d)
+        started = values_to(LAST - 1)
+        empty_to(b)
+        if done["project"] <= T4:
+            out_of_psum(T4, (False, False))
+        quantise_weights(LAST, 0, 2)
+        project_both(T5)
+        for g in started:
+            take_values(g)
+        empty_to(d)
+        heads_to(LAST - 1)
+        weighted_values(LAST, 0, 2)
+        quantise_weights(LAST, 2, 4)
+        out_of_psum(T5, (False, False))
+        weighted_values(LAST, 2, 4)
+        project_both(T6)
+        take_values(LAST)
+        quantise_heads(LAST)
+        out_of_psum(T6, (False, True))
+        project_both(T7)
+        out_of_psum(T7, (False, True))

@@ -42,7 +42,7 @@ QUANT_LAG = 8
 NORM_LAG = 4
 SIDE_AT = {1: (0,), 3: (1,)}
 V_ORDER = "ERTKJNQ"
-V_ORDER_CLOSING = "RKTEJNQ"
+V_ORDER_CLOSING = "RKTEJQN"
 V_ON_GPSIMD = 4
 V_STEP = 2
 V_QUANT_STEP = 7

@@ -35,24 +35,31 @@ MASKED_SCORE = -(2.0**100)
 
 FLOPS = 3 * 2 * SEQ * SEQ * HEADS * HEAD_DIM
 
-WITH_STAND_IN = (5, 7)
-FLIP_LAG = 7
+WITH_STAND_IN = (6, 7)
+FLIP_LAG = 8
 EMPTY_LAG = 8
 QUANT_LAG = 8
 NORM_LAG = 4
 SIDE_AT = {1: (0,), 3: (1,)}
-V_ORDER = "ERTKJNQ"
-V_ORDER_CLOSING = "RKTEJQN"
+V_ORDER = "RTKEJNQ"
+V_ORDER_CLOSING = "RTKEJQN"
 V_ON_GPSIMD = 4
-V_STEP = 2
+V_STEP = 3
 V_QUANT_STEP = 7
-NORM_ON_SCALAR = ((1, 3), ())
-EMPTY_ON_SCALAR = ((0, 1), (0, 2))
-V_HEAD_G = 3
+NORM_ON_SCALAR = ((0, 2), (0, 2), (), ())
+EMPTY_ON_SCALAR = ((0,), (0,), (0, 1), (0, 1))
+V_HEAD_G = 4
+K_ON_SCALAR = (1,)
+Q_ON_VECTOR = False
+C_ON_VECTOR = ((), (), (), ())
+NORM_ON_VECTOR = ((), (), (), ())
+MASK_BY_MATMUL = (5,)
+MERGED = False
+HEAD_MERGED = True
 PROJECT_LAG = 7
-FLIPS_FIRST = False
+FLIPS_FIRST = True
 V_LOAD_EARLY = False
-V_JOB_AT = (((1, 1), (1, 3)), ((2, 1), (2, 3)), ((3, 1), (3, 3)), ((4, 1), (4, 3)))
+V_JOB_AT = (((0, 1), (0, 3)), ((1, 1), (1, 3)), ((2, 1), (2, 3)), ((3, 1), (3, 3)))
 WO_JOB_AT = (((4, 1), (4, 3)), ((5, 1), (5, 3)), ((6, 1), (6, 3)), ((7, 1), (7, 3)))
 LAST_ON_VECTOR = 3
 P13_AT = (15, 16)
@@ -142,6 +149,7 @@ def tile_scaleddotproductattention_pa_kernel(
         nc.scalar.activation(out=table_loader[:], in_=ones[:, 0:1], func=ACT.Exp)
         ident_bf16 = const.tile([P, P], BF16)
         make_identity(nc, ident_bf16[:])
+        neg_ident = const.tile([P, P], BF16)
         ident_f32 = const.tile([P, P], F32)
         make_identity(nc, ident_f32[:])
 
@@ -291,7 +299,7 @@ def tile_scaleddotproductattention_pa_kernel(
                     op=ALU.add,
                 )
                 return
-            copy = nc.vector.tensor_copy if half == 0 else nc.scalar.copy
+            copy = nc.scalar.copy if half in K_ON_SCALAR else nc.vector.tensor_copy
             copy(out=k_t[:, h, keys], in_=in_psum[("k", h, half)][:].rearrange("p i s -> p (i s)"))
 
         v_grouped_of = {}
@@ -300,6 +308,17 @@ def tile_scaleddotproductattention_pa_kernel(
             if part[0] == 0:
                 v_grouped = work.tile([P, KEY_PASSES * HEAD_DIM * PACK], BF16, align_bytes=64, bufs=5)
                 v_grouped_of[h] = v_grouped
+            if len(part) == 2 and (MERGED if h >= GROUP else HEAD_MERGED):
+                engine.tensor_tensor(
+                    out=v_grouped_of[h][:].rearrange("p (g d w) -> p g d w", g=KEY_PASSES, w=PACK),
+                    in0=v_raw_of[h][:].rearrange("p (g u) (e d) -> p g d (u e)", u=2, e=2),
+                    in1=ind_v_words[:]
+                    .rearrange("p (g u) e -> p g (u e)", u=2)
+                    .unsqueeze(2)
+                    .to_broadcast([P, KEY_PASSES, HEAD_DIM, PACK]),
+                    op=ALU.mult,
+                )
+                return
             for g in part:
                 engine.tensor_tensor(
                     out=v_grouped_of[h][:].rearrange("p (g d w) -> p g d w", g=KEY_PASSES, w=PACK)[:, g, :, :],
@@ -363,7 +382,7 @@ def tile_scaleddotproductattention_pa_kernel(
             return head_of(place) not in WITH_STAND_IN
 
         def emptied_by_scalar(place):
-            return masked_in_psum(place) and place % GROUP in EMPTY_ON_SCALAR[groups[place // GROUP][0]]
+            return masked_in_psum(place) and place % GROUP in EMPTY_ON_SCALAR[place // 16]
 
         def scores(place):
             h = head_of(place)
@@ -379,7 +398,15 @@ def tile_scaleddotproductattention_pa_kernel(
                     stop=not masked_in_psum(place),
                 )
                 halves.append(score)
-            if masked_in_psum(place):
+                if masked_in_psum(place) and h in MASK_BY_MATMUL:
+                    nc.tensor.matmul(
+                        score[:],
+                        lhsT=neg_ident[:],
+                        rhs=masked_rows[:, half * BANK : (half + 1) * BANK],
+                        start=False,
+                        stop=True,
+                    )
+            if masked_in_psum(place) and h not in MASK_BY_MATMUL:
                 for half in range(KEY_HALVES):
                     for b in range(GROUP):
                         nc.tensor.matmul(
@@ -463,7 +490,9 @@ def tile_scaleddotproductattention_pa_kernel(
         def normaliser(place):
             if place >= END - LAST_ON_VECTOR:
                 return "vector"
-            return "scalar" if place % GROUP in NORM_ON_SCALAR[groups[place // GROUP][0]] else "gpsimd"
+            if place % GROUP in NORM_ON_VECTOR[place // 16]:
+                return "vector"
+            return "scalar" if place % GROUP in NORM_ON_SCALAR[place // 16] else "gpsimd"
 
         def normalise(place):
             a_bf16 = work.tile([P, SEQ], BF16, bufs=4)
@@ -635,15 +664,21 @@ def tile_scaleddotproductattention_pa_kernel(
                 take_k(h, half)
 
         EARLY = [h for h in WITH_STAND_IN if h < GROUP]
+        ROWS_EARLY = EARLY or [h for h in MASK_BY_MATMUL if h < GROUP]
+        if MASK_BY_MATMUL:
+            nc.gpsimd.tensor_scalar(
+                out=neg_ident[:], in0=ident_bf16[:], scalar1=MASKED_SCORE, scalar2=1.0, op0=ALU.mult, op1=ALU.mult
+            )
         for half in range(KEY_HALVES):
             transpose_k(0, half)
         small_products(0, [], None)
         for half in range(KEY_HALVES):
             take_k(0, half)
         take_small_products(0, [], None)
+        if ROWS_EARLY:
+            build_masked_rows()
         if EARLY:
             count_valid_keys()
-            build_masked_rows()
         prepare_k(1)
         for h in range(V_HEAD_G):
             mask_and_group_v(h, (0, 1))
@@ -659,7 +694,7 @@ def tile_scaleddotproductattention_pa_kernel(
                     heads = [h for h in [GROUP + group - 1] if h in WITH_STAND_IN]
                     small_products(following, heads, group)
                     taken_next.append((take_small_products, (following, heads, group)))
-                if step == 0 and EARLY:
+                if step == 2 and EARLY:
                     small_products(None, [], 0)
                     taken_next.append((take_small_products, (None, [], 0)))
                 h = step + 2
@@ -708,6 +743,7 @@ def tile_scaleddotproductattention_pa_kernel(
                         take(*args)
                 if step == GROUP + 1 and not EARLY:
                     count_valid_keys()
+                if step == GROUP + 1 and not ROWS_EARLY:
                     build_masked_rows()
                 if step == (GROUP if EARLY else 2 * GROUP):
                     build_key_mask()

@@ -46,13 +46,24 @@ V_ORDER_CLOSING = "RTKEJQN"
 V_ON_GPSIMD = 4
 V_STEP = 3
 V_QUANT_STEP = 7
-NORM_ON_SCALAR = ((0, 2), (0, 2), (), ())
-EMPTY_ON_SCALAR = ((0,), (0,), (0, 1), (0, 1))
+NORM_ON_SCALAR = ((0, 2), ())
+EMPTY_ON_SCALAR = ((0,), (0, 1))
 V_HEAD_G = 4
+V_FIRST = 1
+START_STEPS = 0
+EXPS_FIRST = False
+EXP_LAG = 2
+LAST_BY_TENSOR = 0
+LAST_EMPTY_ON_SCALAR = (-4, -3, -2, -1)
+MASK_STEP = 11
+BATCH = 2
+S_AT_ONCE = False
+COUNT_STEP = 6
+PRODUCTS_FIRST = True
 K_ON_SCALAR = (1,)
 Q_ON_VECTOR = False
 C_ON_VECTOR = ((), (), (), ())
-NORM_ON_VECTOR = ((), (), (), ())
+NORM_ON_VECTOR = ((), ())
 MASK_BY_MATMUL = (5,)
 MERGED = False
 HEAD_MERGED = True
@@ -155,7 +166,9 @@ def tile_scaleddotproductattention_pa_kernel(
 
         neg_columns = const.tile([P, KEY_BLOCKS, P], F32)
         ind_k_columns = const.tile([P, KEY_BLOCKS], BF16)
+        valid_keys = const.tile([P, 1], F32)
         any_valid = const.tile([P, 1], F32)
+        value_mask = const.tile([P, 2 * KEY_PASSES, 2], BF16)
         inv_valid = const.tile([P, 1], F32)
         neg_masked = const.tile([P, 1], F32)
 
@@ -182,9 +195,16 @@ def tile_scaleddotproductattention_pa_kernel(
         def count_valid_keys():
             counts = psum.tile([P, KEY_BLOCKS], F32, tag="bank")
             nc.tensor.matmul(counts[:], lhsT=ones[:], rhs=ind_k_columns[:], start=True, stop=True)
-            valid_keys = stats.tile([P, 1], F32)
-            nc.vector.reduce_sum(out=valid_keys[:], in_=counts[:], axis=mybir.AxisListType.X)
-            nc.vector.tensor_scalar(out=any_valid[:], in0=valid_keys[:], scalar1=1.0, scalar2=None, op0=ALU.min)
+            scrap = stats.tile([P, KEY_BLOCKS], F32)
+            nc.scalar.activation(out=scrap[:], in_=counts[:], func=ACT.Copy, accum_out=valid_keys[:])
+            nc.gpsimd.tensor_scalar(
+                out=any_valid[:], in0=valid_keys[:], scalar1=1.0, scalar2=0.0, op0=ALU.min, op1=ALU.max
+            )
+            nc.gpsimd.tensor_scalar(
+                out=value_mask[:], in0=ind_v_words[:], scalar1=any_valid[:], scalar2=1.0, op0=ALU.mult, op1=ALU.mult
+            )
+
+        def take_count():
             nc.vector.tensor_scalar(out=inv_valid[:], in0=valid_keys[:], scalar1=1.0, scalar2=None, op0=ALU.max)
             nc.vector.tensor_scalar(
                 out=neg_masked[:],
@@ -312,7 +332,7 @@ def tile_scaleddotproductattention_pa_kernel(
                 engine.tensor_tensor(
                     out=v_grouped_of[h][:].rearrange("p (g d w) -> p g d w", g=KEY_PASSES, w=PACK),
                     in0=v_raw_of[h][:].rearrange("p (g u) (e d) -> p g d (u e)", u=2, e=2),
-                    in1=ind_v_words[:]
+                    in1=value_mask[:]
                     .rearrange("p (g u) e -> p g (u e)", u=2)
                     .unsqueeze(2)
                     .to_broadcast([P, KEY_PASSES, HEAD_DIM, PACK]),
@@ -323,7 +343,7 @@ def tile_scaleddotproductattention_pa_kernel(
                 engine.tensor_tensor(
                     out=v_grouped_of[h][:].rearrange("p (g d w) -> p g d w", g=KEY_PASSES, w=PACK)[:, g, :, :],
                     in0=v_raw_of[h][:].rearrange("p (g u) (e d) -> p g d (u e)", u=2, e=2)[:, g, :, :],
-                    in1=ind_v_words[:]
+                    in1=value_mask[:]
                     .rearrange("p (g u) e -> p g (u e)", u=2)[:, g, :]
                     .unsqueeze(1)
                     .to_broadcast([P, HEAD_DIM, PACK]),
@@ -379,10 +399,12 @@ def tile_scaleddotproductattention_pa_kernel(
         pair_sums_of = {}
 
         def masked_in_psum(place):
-            return head_of(place) not in WITH_STAND_IN
+            return head_of(place) not in WITH_STAND_IN or place >= END - LAST_BY_TENSOR
 
         def emptied_by_scalar(place):
-            return masked_in_psum(place) and place % GROUP in EMPTY_ON_SCALAR[place // 16]
+            if place >= END - LAST_BY_TENSOR:
+                return place - END in LAST_EMPTY_ON_SCALAR
+            return masked_in_psum(place) and place % GROUP in EMPTY_ON_SCALAR[groups[place // GROUP][0]]
 
         def scores(place):
             h = head_of(place)
@@ -406,18 +428,20 @@ def tile_scaleddotproductattention_pa_kernel(
                         start=False,
                         stop=True,
                     )
-            if masked_in_psum(place) and h not in MASK_BY_MATMUL:
+            scores_of[place] = halves
+
+        def add_masks(place):
+            if masked_in_psum(place) and head_of(place) not in MASK_BY_MATMUL:
                 for half in range(KEY_HALVES):
                     for b in range(GROUP):
                         nc.tensor.matmul(
-                            halves[half][:, b * P : (b + 1) * P],
+                            scores_of[place][half][:, b * P : (b + 1) * P],
                             lhsT=neg_columns[:, half * GROUP + b, :],
                             rhs=ident_f32[:],
                             start=False,
                             stop=(b == GROUP - 1),
                             is_transpose=True,
                         )
-            scores_of[place] = halves
 
         def row_maximum(place):
             maxima = stats.tile([P, KEY_HALVES], F32)
@@ -441,11 +465,11 @@ def tile_scaleddotproductattention_pa_kernel(
 
         def exponentials(place):
             group, i = divmod(place, GROUP)
-            j = place % PAIR
+            j = place % GROUP
             if j == 0:
-                pair_sums = stats.tile([P, PAIR, KEY_HALVES], F32)
-                pair_sums_of[place // PAIR] = pair_sums
-            pair_sums = pair_sums_of[place // PAIR]
+                pair_sums = stats.tile([P, GROUP, KEY_HALVES], F32)
+                pair_sums_of[group] = pair_sums
+            pair_sums = pair_sums_of[group]
             first = pair_sums[:, j, 0:1]
             if not masked_in_psum(place):
                 first_raw = stats.tile([P, 1], F32)
@@ -459,7 +483,7 @@ def tile_scaleddotproductattention_pa_kernel(
                     bias=neg_max_of[place][:],
                     scale=SCALE,
                 )
-            weights = work.tile([P, SEQ], F32, bufs=5)
+            weights = work.tile([P, SEQ], F32, bufs=10)
             for half in range(KEY_HALVES):
                 nc.scalar.activation(
                     out=weights[:, half * BANK : (half + 1) * BANK],
@@ -475,30 +499,30 @@ def tile_scaleddotproductattention_pa_kernel(
                     out=pair_sums[:, j, 0:1], in_=stand_in_exp[:], func=ACT.Identity, scale=neg_masked[:], bias=first
                 )
 
-        def join_sums(pair):
-            row_sums = stats.tile([P, PAIR], F32)
+        def join_sums(group, first, last):
+            row_sums = stats.tile([P, last - first], F32)
             nc.vector.tensor_reduce(
-                out=row_sums[:], in_=pair_sums_of[pair][:], axis=mybir.AxisListType.X, op=ALU.add
+                out=row_sums[:], in_=pair_sums_of[group][:, first:last, :], axis=mybir.AxisListType.X, op=ALU.add
             )
-            row_sum_of[pair] = row_sums
+            row_sum_of[group, first] = row_sums
 
-        def invert_sums(pair):
-            inv_sums = stats.tile([P, PAIR], F32)
-            nc.vector.reciprocal(out=inv_sums[:], in_=row_sum_of[pair][:])
-            inv_sum_of[pair] = inv_sums
+        def invert_sums(group, first, last):
+            inv_sums = stats.tile([P, last - first], F32)
+            nc.vector.reciprocal(out=inv_sums[:], in_=row_sum_of[group, first][:])
+            for j in range(first, last):
+                inv_sum_of[group * GROUP + j] = inv_sums[:, j - first : j - first + 1]
 
         def normaliser(place):
             if place >= END - LAST_ON_VECTOR:
                 return "vector"
-            if place % GROUP in NORM_ON_VECTOR[place // 16]:
+            if place % GROUP in NORM_ON_VECTOR[groups[place // GROUP][0]]:
                 return "vector"
-            return "scalar" if place % GROUP in NORM_ON_SCALAR[place // 16] else "gpsimd"
+            return "scalar" if place % GROUP in NORM_ON_SCALAR[groups[place // GROUP][0]] else "gpsimd"
 
         def normalise(place):
-            a_bf16 = work.tile([P, SEQ], BF16, bufs=4)
+            a_bf16 = work.tile([P, SEQ], BF16, bufs=6)
             weights = weights_of[place]
-            j = place % PAIR
-            inv_sum = inv_sum_of[place // PAIR][:, j : j + 1]
+            inv_sum = inv_sum_of[place]
             if normaliser(place) == "gpsimd":
                 nc.gpsimd.tensor_scalar(
                     out=a_bf16[:], in0=weights[:], scalar1=inv_sum, scalar2=1.0, op0=ALU.mult, op1=ALU.mult
@@ -579,9 +603,9 @@ def tile_scaleddotproductattention_pa_kernel(
                 there = c_grouped[:].rearrange("p (q i) -> p q i", i=PACK)[:, some, :]
                 here = o_t_of[group][:].rearrange("p i q -> p q i")[:, some, :]
                 if part == 0:
-                    nc.scalar.activation(out=there, in_=here, func=ACT.Copy, scale=any_valid[:])
+                    nc.scalar.copy(out=there, in_=here)
                 else:
-                    nc.vector.tensor_scalar(out=there, in0=here, scalar1=any_valid[:], scalar2=None, op0=ALU.mult)
+                    nc.vector.tensor_copy(out=there, in_=here)
             c_grouped_of[group] = c_grouped
 
         def quantise_heads(group):
@@ -677,10 +701,13 @@ def tile_scaleddotproductattention_pa_kernel(
         take_small_products(0, [], None)
         if ROWS_EARLY:
             build_masked_rows()
+        count_valid_keys()
         if EARLY:
-            count_valid_keys()
+            take_count()
         prepare_k(1)
-        for h in range(V_HEAD_G):
+        for h in range(V_FIRST):
+            mask_and_group_v(h, (0, 1), nc.vector)
+        for h in range(V_FIRST, V_HEAD_G):
             mask_and_group_v(h, (0, 1))
 
         def step_of(step):
@@ -689,11 +716,28 @@ def tile_scaleddotproductattention_pa_kernel(
             group, i = divmod(step, GROUP)
             following = group + 1 if group < LAST else None
 
+            def tensor_products():
+                ready = closed_group(step, QUANT_LAG + 2)
+                if ready is not None:
+                    weighted_values(ready, 0, GROUP)
+                    done["values"] = ready + 1
+                    taken_next.append((take_values, (ready,)))
+                for half in range(2):
+                    ready = closed_group(step, QUANT_LAG + PROJECT_LAG + half)
+                    if ready is not None and groups[ready][0] == FEATURE_PASSES - 1:
+                        t = groups[ready][1]
+                        project(t, half)
+                        if half == 1:
+                            done["project"] = t + 1
+                        taken_next.append((take_result, (t, half, False)))
+
             def tensor_side_jobs():
                 if i == 0 and step > 0:
                     heads = [h for h in [GROUP + group - 1] if h in WITH_STAND_IN]
                     small_products(following, heads, group)
                     taken_next.append((take_small_products, (following, heads, group)))
+                if step == COUNT_STEP and not EARLY:
+                    taken_next.append((take_count, ()))
                 if step == 2 and EARLY:
                     small_products(None, [], 0)
                     taken_next.append((take_small_products, (None, [], 0)))
@@ -709,28 +753,20 @@ def tile_scaleddotproductattention_pa_kernel(
                         make_rows(h)
                     transpose_k(h, i - 2)
                     taken_next.append((take_k, (h, i - 2)))
-                ready = closed_group(step, QUANT_LAG + 2)
-                if ready is not None:
-                    weighted_values(ready, 0, GROUP)
-                    done["values"] = ready + 1
-                    taken_next.append((take_values, (ready,)))
-                for half in range(2):
-                    ready = closed_group(step, QUANT_LAG + PROJECT_LAG + half)
-                    if ready is not None and groups[ready][0] == FEATURE_PASSES - 1:
-                        t = groups[ready][1]
-                        project(t, half)
-                        if half == 1:
-                            done["project"] = t + 1
-                        taken_next.append((take_result, (t, half, False)))
 
             if FLIPS_FIRST:
                 flip_to(step - FLIP_LAG)
             scores(step)
+            if PRODUCTS_FIRST:
+                tensor_products()
+            add_masks(step)
             if step == 1:
                 small_products(1, [], None)
                 taken_next.append((take_small_products, (1, [], None)))
             if not FLIPS_FIRST:
                 flip_to(step - FLIP_LAG)
+            if not PRODUCTS_FIRST:
+                tensor_products()
             tensor_side_jobs()
 
             def do_R():
@@ -739,23 +775,21 @@ def tile_scaleddotproductattention_pa_kernel(
 
             def do_K():
                 for take, args in take_now:
-                    if take is take_k:
+                    if take in (take_k, take_count):
                         take(*args)
-                if step == GROUP + 1 and not EARLY:
-                    count_valid_keys()
-                if step == GROUP + 1 and not ROWS_EARLY:
-                    build_masked_rows()
-                if step == (GROUP if EARLY else 2 * GROUP):
-                    build_key_mask()
                 h = V_HEAD_G + step - V_STEP
                 if V_HEAD_G <= h < GROUP and step >= V_STEP:
                     mask_and_group_v(h, (0, 1), nc.vector)
 
-            closes_pair = entered(step, NORM_LAG) is not None and step % PAIR == (NORM_LAG + PAIR - 1) % PAIR
+            summed = entered(step, NORM_LAG)
+            batch = PAIR if summed is None or summed >= END - GROUP else BATCH
+            closes = summed is not None and summed % batch == batch - 1
+            if closes:
+                of_group, last = summed // GROUP, summed % GROUP + 1
 
             def do_T():
-                if closes_pair:
-                    join_sums((step - NORM_LAG) // PAIR)
+                if closes:
+                    join_sums(of_group, last - batch, last)
 
             place_to_empty = entered(step, EMPTY_LAG)
             late_copy = place_to_empty is not None and emptied_by_scalar(place_to_empty)
@@ -773,24 +807,25 @@ def tile_scaleddotproductattention_pa_kernel(
             inverted = []
 
             def do_N():
-                if closes_pair:
-                    invert_sums((step - NORM_LAG) // PAIR)
-                    inverted.extend([step - NORM_LAG - PAIR + 1 + j for j in range(PAIR)])
+                if closes:
+                    invert_sums(of_group, last - batch, last)
+                    inverted.extend([of_group * GROUP + j for j in range(last - batch, last)])
                     for engine in ("vector", "gpsimd"):
                         for place in inverted:
                             if normaliser(place) == engine:
                                 normalise(place)
 
             def do_Q():
-                ready = closed_group(step, QUANT_LAG)
-                if ready is None:
-                    if step == V_QUANT_STEP:
-                        for h in range(GROUP):
-                            quantise_v(h)
-                    return
                 if step == V_QUANT_STEP:
                     for h in range(GROUP):
                         quantise_v(h)
+                ready = closed_group(step, QUANT_LAG)
+                if step == MASK_STEP and not ROWS_EARLY:
+                    build_masked_rows()
+                if step == MASK_STEP:
+                    build_key_mask()
+                if ready is None:
+                    return
                 earlier = closed_group(step, QUANT_LAG + 4)
                 if earlier is not None:
                     quantise_heads(earlier)
@@ -803,20 +838,22 @@ def tile_scaleddotproductattention_pa_kernel(
                 done["quant"] = ready + 1
 
             jobs = {"R": do_R, "K": do_K, "E": do_E, "J": do_J, "N": do_N, "T": do_T, "Q": do_Q}
-            for letter in V_ORDER_CLOSING if closed_group(step, QUANT_LAG) is not None else V_ORDER:
+            for letter in V_ORDER_CLOSING if closed_group(step, QUANT_LAG) is not None or step == V_QUANT_STEP else V_ORDER:
                 jobs[letter]()
 
+            exps_first = EXPS_FIRST or step < START_STEPS
+            if exps_first and entered(step, EXP_LAG) is not None:
+                exponentials(step - EXP_LAG)
             for take, args in take_now:
-                if take is not take_k:
+                if take not in (take_k, take_count):
                     take(*args)
-            if entered(step, 2) is not None:
-                exponentials(step - 2)
+            if not exps_first and entered(step, EXP_LAG) is not None:
+                exponentials(step - EXP_LAG)
             if late_copy:
                 empty(place_to_empty)
-            for place in for_scalar:
-                normalise(place)
-            for_scalar.clear()
             for_scalar.extend([place for place in inverted if normaliser(place) == "scalar"])
+            if for_scalar and (S_AT_ONCE or for_scalar[0] not in inverted):
+                normalise(for_scalar.pop(0))
 
             if i == 0 and group + 2 < len(groups):
                 load_q(group + 2)
@@ -868,9 +905,9 @@ def tile_scaleddotproductattention_pa_kernel(
                 project(t, half)
 
         a, b, c, d = range(END - GROUP, END)
-        pair = (END - GROUP) // PAIR
         order_of_t = [t for g, t in groups if g == FEATURE_PASSES - 1]
-        T4, T5, T6, T7 = order_of_t[-4:]
+        early = order_of_t[done["project"] : -3]
+        T5, T6, T7 = order_of_t[-3:]
 
         for take, args in taken_next:
             take(*args)
@@ -878,27 +915,29 @@ def tile_scaleddotproductattention_pa_kernel(
             normalise(place)
         flip_to(a - 2)
         row_maximum(d)
-        exponentials(c)
+        if EXP_LAG == 2:
+            exponentials(c)
         empty_to(a - 4)
         join_maxima(d)
         exponentials(d)
         quantise_to(LAST - 2)
         started = values_to(LAST - 2)
-        join_sums(pair)
+        join_sums(LAST, 0, PAIR)
         empty_to(a - 3)
-        invert_sums(pair)
+        invert_sums(LAST, 0, PAIR)
         normalise(a)
         normalise(b)
         for g in started:
             take_values(g)
         flip_to(a - 1)
-        if done["project"] <= T4:
+        if early:
             heads_to(LAST - 3)
-            project_both(T4)
+        for t in early:
+            project_both(t)
         empty_to(a - 1)
         flip_to(b)
-        join_sums(pair + 1)
-        invert_sums(pair + 1)
+        join_sums(LAST, PAIR, GROUP)
+        invert_sums(LAST, PAIR, GROUP)
         normalise(c)
         normalise(d)
         heads_to(LAST - 2)
@@ -906,8 +945,8 @@ def tile_scaleddotproductattention_pa_kernel(
         flip_to(d)
         started = values_to(LAST - 1)
         empty_to(b)
-        if done["project"] <= T4:
-            out_of_psum(T4, (False, False))
+        for t in early:
+            out_of_psum(t, (False, False))
         quantise_weights(LAST, 0, 2)
         project_both(T5)
         for g in started:

@@ -42,11 +42,11 @@ QUANT_LAG = 8
 NORM_LAG = 4
 SIDE_AT = {1: (0,), 3: (1,)}
 V_ORDER = "RTKEJNQ"
-V_ORDER_CLOSING = "RTKEJQN"
+V_ORDER_CLOSING = "RTKEJNQ"
 V_ON_GPSIMD = 4
-V_STEP = 3
+V_STEP = 2
 V_QUANT_STEP = 7
-NORM_ON_SCALAR = ((0, 2), ())
+NORM_ON_SCALAR = ((0, 3), ())
 EMPTY_ON_SCALAR = ((0,), (0, 1))
 V_HEAD_G = 4
 V_FIRST = 1
@@ -55,16 +55,16 @@ EXPS_FIRST = False
 EXP_LAG = 2
 LAST_BY_TENSOR = 0
 LAST_EMPTY_ON_SCALAR = (-4, -3, -2, -1)
-MASK_STEP = 11
+MASK_STEP = 7
 BATCH = 2
 S_AT_ONCE = False
 COUNT_STEP = 6
-PRODUCTS_FIRST = True
+PRODUCTS_FIRST = False
 K_ON_SCALAR = (1,)
 Q_ON_VECTOR = False
 C_ON_VECTOR = ((), (), (), ())
 NORM_ON_VECTOR = ((), ())
-MASK_BY_MATMUL = (5,)
+MASK_BY_MATMUL = (1,)
 MERGED = False
 HEAD_MERGED = True
 PROJECT_LAG = 7

@@ -46,9 +46,11 @@ V_ORDER_CLOSING = "RTKEJNQ"
 V_ON_GPSIMD = 4
 V_STEP = 2
 V_QUANT_STEP = 7
-NORM_ON_SCALAR = ((0, 3), ())
-EMPTY_ON_SCALAR = ((0,), (0, 1))
+NORM_ON_SCALAR = ((0, 3, 4, 7), ())
+EMPTY_ON_SCALAR = ((0, 4), (0, 1, 4, 5))
 V_HEAD_G = 4
+LAST_ON_SCALAR = (-3,)
+K_LATE = False
 V_FIRST = 1
 START_STEPS = 0
 EXPS_FIRST = False
@@ -62,6 +64,8 @@ COUNT_STEP = 6
 PRODUCTS_FIRST = False
 K_ON_SCALAR = (1,)
 Q_ON_VECTOR = False
+RESULT_ON_VECTOR = ()
+GROUP0_ON_SCALAR = 0
 C_ON_VECTOR = ((), (), (), ())
 NORM_ON_VECTOR = ((), ())
 MASK_BY_MATMUL = (1,)
@@ -270,10 +274,19 @@ def tile_scaleddotproductattention_pa_kernel(
                         start=True,
                         stop=True,
                     )
-            in_psum["small"] = bank
+            in_psum["small", next_group, tuple(heads), group] = bank
+
+        def take_queries(next_group, bank):
+            q_t = work.tile([P, GROUP, P], BF16, bufs=3)
+            copy = nc.vector.tensor_copy if Q_ON_VECTOR and next_group > 1 else nc.scalar.copy
+            copy(
+                out=q_t[:],
+                in_=bank[:, 0:Q_WORDS].bitcast(BF16).rearrange("p (i q) -> p i q", i=GROUP),
+            )
+            q_t_of[next_group] = q_t
 
         def take_small_products(next_group, heads, group):
-            bank = in_psum["small"]
+            bank = in_psum["small", next_group, tuple(heads), group]
             if group is not None and with_stand_in(group):
                 count = len(with_stand_in(group))
                 stand_in_scores = stats.tile([P, count], F32)
@@ -286,13 +299,8 @@ def tile_scaleddotproductattention_pa_kernel(
                 )
                 for j, h in enumerate(heads):
                     mean_of[h] = mean[:, j : j + 1]
-            if next_group is not None:
-                q_t = work.tile([P, GROUP, P], BF16, bufs=3)
-                nc.scalar.copy(
-                    out=q_t[:],
-                    in_=bank[:, 0:Q_WORDS].bitcast(BF16).rearrange("p (i q) -> p i q", i=GROUP),
-                )
-                q_t_of[next_group] = q_t
+            if next_group is not None and not (Q_ON_VECTOR and next_group > 1):
+                take_queries(next_group, bank)
             for j, h in enumerate(heads):
                 nc.scalar.copy(out=stand_in[:, h : h + 1], in_=mean[:, j : j + 1])
 
@@ -308,6 +316,9 @@ def tile_scaleddotproductattention_pa_kernel(
             for i in range(GROUP):
                 nc.tensor.transpose(flipped_k[:, i, :], k_raw_of[h][:, half * GROUP + i, :], ident_bf16[:])
             in_psum[("k", h, half)] = flipped_k
+
+        def k_on_scalar(h, half):
+            return h not in WITH_STAND_IN and half in K_ON_SCALAR
 
         def take_k(h, half):
             keys = slice(half * BANK, (half + 1) * BANK)
@@ -363,8 +374,8 @@ def tile_scaleddotproductattention_pa_kernel(
             if part[0] == 0:
                 wo_grouped = work.tile([P, BANK * PACK], BF16, align_bytes=64)
                 wo_grouped_of[piece] = wo_grouped
-            WIDTH = BANK // 2
-            for b in part:
+            WIDTH = BANK // (2 if len(part) == 1 else 1)
+            for b in part if len(part) == 1 else (0,):
                 cols = slice(half * BANK + b * WIDTH, half * BANK + (b + 1) * WIDTH)
                 nc.gpsimd.tensor_scalar(
                     out=wo_grouped_of[piece][:, b * WIDTH * PACK : (b + 1) * WIDTH * PACK].rearrange(
@@ -404,7 +415,7 @@ def tile_scaleddotproductattention_pa_kernel(
         def emptied_by_scalar(place):
             if place >= END - LAST_BY_TENSOR:
                 return place - END in LAST_EMPTY_ON_SCALAR
-            return masked_in_psum(place) and place % GROUP in EMPTY_ON_SCALAR[groups[place // GROUP][0]]
+            return masked_in_psum(place) and place % (2 * GROUP) in EMPTY_ON_SCALAR[groups[place // GROUP][0]]
 
         def scores(place):
             h = head_of(place)
@@ -513,11 +524,15 @@ def tile_scaleddotproductattention_pa_kernel(
                 inv_sum_of[group * GROUP + j] = inv_sums[:, j - first : j - first + 1]
 
         def normaliser(place):
+            if place - END in LAST_ON_SCALAR:
+                return "scalar"
+            if place < GROUP0_ON_SCALAR:
+                return "scalar"
             if place >= END - LAST_ON_VECTOR:
                 return "vector"
             if place % GROUP in NORM_ON_VECTOR[groups[place // GROUP][0]]:
                 return "vector"
-            return "scalar" if place % GROUP in NORM_ON_SCALAR[groups[place // GROUP][0]] else "gpsimd"
+            return "scalar" if place % (2 * GROUP) in NORM_ON_SCALAR[groups[place // GROUP][0]] else "gpsimd"
 
         def normalise(place):
             a_bf16 = work.tile([P, SEQ], BF16, bufs=6)
@@ -702,8 +717,6 @@ def tile_scaleddotproductattention_pa_kernel(
         if ROWS_EARLY:
             build_masked_rows()
         count_valid_keys()
-        if EARLY:
-            take_count()
         prepare_k(1)
         for h in range(V_FIRST):
             mask_and_group_v(h, (0, 1), nc.vector)
@@ -729,7 +742,7 @@ def tile_scaleddotproductattention_pa_kernel(
                         project(t, half)
                         if half == 1:
                             done["project"] = t + 1
-                        taken_next.append((take_result, (t, half, False)))
+                        taken_next.append((take_result, (t, half, half in RESULT_ON_VECTOR)))
 
             def tensor_side_jobs():
                 if i == 0 and step > 0:
@@ -738,12 +751,15 @@ def tile_scaleddotproductattention_pa_kernel(
                     taken_next.append((take_small_products, (following, heads, group)))
                 if step == COUNT_STEP and not EARLY:
                     taken_next.append((take_count, ()))
-                if step == 2 and EARLY:
+                if step == 3 and EARLY:
                     small_products(None, [], 0)
                     taken_next.append((take_small_products, (None, [], 0)))
                 h = step + 2
                 if h < GROUP:
-                    prepare_stand_in(h)
+                    if h in WITH_STAND_IN:
+                        small_products(None, [h], None)
+                        taken_next.append((take_small_products, (None, [h], None)))
+                        taken_next.append((make_rows, (h,)))
                     for half in range(KEY_HALVES):
                         transpose_k(h, half)
                         taken_next.append((take_k, (h, half)))
@@ -774,8 +790,14 @@ def tile_scaleddotproductattention_pa_kernel(
                     row_maximum(step - 1)
 
             def do_K():
+                if EARLY and step == 0:
+                    take_count()
                 for take, args in take_now:
-                    if take in (take_k, take_count):
+                    if take in (take_count, make_rows) or take is take_k and not k_on_scalar(*args):
+                        if take is make_rows:
+                            for other, its in take_now:
+                                if other is take_small_products and its[1] == [args[0]]:
+                                    other(*its)
                         take(*args)
                 h = V_HEAD_G + step - V_STEP
                 if V_HEAD_G <= h < GROUP and step >= V_STEP:
@@ -795,6 +817,11 @@ def tile_scaleddotproductattention_pa_kernel(
             late_copy = place_to_empty is not None and emptied_by_scalar(place_to_empty)
 
             def do_E():
+                for take, args in take_now:
+                    if take is take_small_products and args[0] is not None and Q_ON_VECTOR and args[0] > 1:
+                        take_queries(args[0], in_psum["small", args[0], tuple(args[1]), args[2]])
+                    if take is take_result and args[2]:
+                        take(*args)
                 if place_to_empty is not None:
                     done["empty"] = place_to_empty + 1
                     if not late_copy:
@@ -845,10 +872,20 @@ def tile_scaleddotproductattention_pa_kernel(
             if exps_first and entered(step, EXP_LAG) is not None:
                 exponentials(step - EXP_LAG)
             for take, args in take_now:
-                if take not in (take_k, take_count):
+                if take not in (take_k, take_count, make_rows) and not (take is take_result and args[2]):
+                    if take is take_small_products and args[0] is None and args[1] and args[2] is None:
+                        continue
                     take(*args)
+            if not K_LATE:
+                for take, args in take_now:
+                    if take is take_k and k_on_scalar(*args):
+                        take(*args)
             if not exps_first and entered(step, EXP_LAG) is not None:
                 exponentials(step - EXP_LAG)
+            if K_LATE:
+                for take, args in take_now:
+                    if take is take_k and k_on_scalar(*args):
+                        take(*args)
             if late_copy:
                 empty(place_to_empty)
             for_scalar.extend([place for place in inverted if normaliser(place) == "scalar"])
@@ -867,7 +904,10 @@ def tile_scaleddotproductattention_pa_kernel(
                     load_wo(g)
             for at, lay_out, quantise, what, part in side_jobs.get(group, []):
                 if at == i:
-                    lay_out(what, (part,))
+                    if not MERGED:
+                        lay_out(what, (part,))
+                    elif part == 0:
+                        lay_out(what, (0, 1))
                     if part == 1:
                         to_quantise.append((step, quantise, what))
 
@@ -913,40 +953,39 @@ def tile_scaleddotproductattention_pa_kernel(
             take(*args)
         for place in for_scalar:
             normalise(place)
-        flip_to(a - 2)
-        row_maximum(d)
-        if EXP_LAG == 2:
-            exponentials(c)
-        empty_to(a - 4)
-        join_maxima(d)
-        exponentials(d)
-        quantise_to(LAST - 2)
+        flip_to(a - 3)
         started = values_to(LAST - 2)
-        join_sums(LAST, 0, PAIR)
-        empty_to(a - 3)
-        invert_sums(LAST, 0, PAIR)
-        normalise(a)
-        normalise(b)
-        for g in started:
-            take_values(g)
-        flip_to(a - 1)
         if early:
             heads_to(LAST - 3)
         for t in early:
             project_both(t)
+        flip_to(a - 1)
+        row_maximum(d)
+        exponentials(c)
+        join_maxima(d)
+        exponentials(d)
+        join_sums(LAST, 0, PAIR)
+        invert_sums(LAST, 0, PAIR)
+        normalise(a)
+        normalise(b)
+        for t in early:
+            take_result(t, 0, True)
+        empty_to(a - 2)
+        for t in early:
+            take_result(t, 1, True)
         empty_to(a - 1)
         flip_to(b)
         join_sums(LAST, PAIR, GROUP)
         invert_sums(LAST, PAIR, GROUP)
         normalise(c)
         normalise(d)
+        for g in started:
+            take_values(g)
+        flip_to(d)
         heads_to(LAST - 2)
         quantise_to(LAST - 1)
-        flip_to(d)
         started = values_to(LAST - 1)
         empty_to(b)
-        for t in early:
-            out_of_psum(t, (False, False))
         quantise_weights(LAST, 0, 2)
         project_both(T5)
         for g in started:
@@ -956,10 +995,12 @@ def tile_scaleddotproductattention_pa_kernel(
         weighted_values(LAST, 0, 2)
         quantise_weights(LAST, 2, 4)
         out_of_psum(T5, (False, False))
+        project(T6, 0)
         weighted_values(LAST, 2, 4)
-        project_both(T6)
+        project(T6, 1)
+        take_result(T6, 0, False)
         take_values(LAST)
         quantise_heads(LAST)
-        out_of_psum(T6, (False, True))
+        take_result(T6, 1, True)
         project_both(T7)
         out_of_psum(T7, (False, True))

@@ -49,6 +49,7 @@ V_QUANT_STEP = 7
 NORM_ON_SCALAR = ((0, 3, 4, 7), ())
 EMPTY_ON_SCALAR = ((0, 4), (0, 1, 4, 5))
 V_HEAD_G = 4
+LATE_LOAD_STEP = 2
 LAST_ON_SCALAR = (-3,)
 K_LATE = False
 V_FIRST = 1
@@ -57,7 +58,7 @@ EXPS_FIRST = False
 EXP_LAG = 2
 LAST_BY_TENSOR = 0
 LAST_EMPTY_ON_SCALAR = (-4, -3, -2, -1)
-MASK_STEP = 7
+MASK_STEP = 11
 BATCH = 2
 S_AT_ONCE = False
 COUNT_STEP = 6
@@ -68,7 +69,7 @@ RESULT_ON_VECTOR = ()
 GROUP0_ON_SCALAR = 0
 C_ON_VECTOR = ((), (), (), ())
 NORM_ON_VECTOR = ((), ())
-MASK_BY_MATMUL = (1,)
+MASK_BY_MATMUL = (5,)
 MERGED = False
 HEAD_MERGED = True
 PROJECT_LAG = 7
@@ -151,12 +152,10 @@ def tile_scaleddotproductattention_pa_kernel(
         ind_v_words = const.tile([P, 2 * KEY_PASSES, 2], BF16)
         nc.scalar.dma_start(out=ind_v_words[:], in_=ind_v[0].rearrange("(c p e) -> p c e", p=P, e=2))
         ind_k_words = const.tile([P, 2 * KEY_PASSES, 2], BF16)
-        nc.scalar.dma_start(out=ind_k_words[:], in_=ind_k[0].rearrange("(c p e) -> p c e", p=P, e=2))
         load_q(1)
         for h in range(2, GROUP):
             load_v(h)
         ind_k_rows = const.tile([P, SEQ], BF16)
-        nc.scalar.dma_start(out=ind_k_rows[:], in_=ind_k[0].partition_broadcast(P))
 
         ones = const.tile([P, P], BF16)
         nc.vector.memset(ones[:], 1.0)
@@ -892,6 +891,9 @@ def tile_scaleddotproductattention_pa_kernel(
             if for_scalar and (S_AT_ONCE or for_scalar[0] not in inverted):
                 normalise(for_scalar.pop(0))
 
+            if step == LATE_LOAD_STEP:
+                nc.sync.dma_start(out=ind_k_rows[:], in_=ind_k[0].partition_broadcast(P))
+                nc.sync.dma_start(out=ind_k_words[:], in_=ind_k[0].rearrange("(c p e) -> p c e", p=P, e=2))
             if i == 0 and group + 2 < len(groups):
                 load_q(group + 2)
             if i == 0 and GROUP <= GROUP + group < HEADS:

import math
from contextlib import ExitStack

import concourse.mybir as mybir
from concourse.masks import make_identity

BF16 = mybir.dt.bfloat16
F32 = mybir.dt.float32
U32 = mybir.dt.uint32
U8 = mybir.dt.uint8
FP8X4 = mybir.dt.float8_e4m3fn_x4
ALU = mybir.AluOpType
ACT = mybir.ActivationFunctionType

P = 128
PACK = 4
K_PASS = P * PACK
BANK = 512

HEADS = 8
SEQ = 1024
HEAD_DIM = 128
D_OUT = 1024
KEY_PASSES = SEQ // K_PASS
FEATURE_PASSES = HEADS * HEAD_DIM // K_PASS
GROUP = K_PASS // HEAD_DIM
Q_TILES = SEQ // P
KEY_HALVES = SEQ // BANK
KEY_BLOCKS = SEQ // P
PAIR = 2

SCALE = 1.0 / math.sqrt(HEAD_DIM)
BANKS = 8
MASKED_SCORE = -(2.0**100)

FLOPS = 3 * 2 * SEQ * SEQ * HEADS * HEAD_DIM

WITH_STAND_IN = (6, 7)
FLIP_LAG = 8
EMPTY_LAG = 8
QUANT_LAG = 8
NORM_LAG = 4
SIDE_AT = {1: (0,), 3: (1,)}
V_ORDER = "RTKEJNQ"
V_ORDER_CLOSING = "RTKEJNQ"
V_ON_GPSIMD = 4
V_STEP = 2
V_QUANT_STEP = 7
NORM_ON_SCALAR = ((0, 3, 4, 7), ())
EMPTY_ON_SCALAR = ((0, 4), (0, 1, 4, 5))
V_HEAD_G = 4
LATE_LOAD_STEP = 2
LAST_ON_SCALAR = (-3,)
K_LATE = False
V_FIRST = 1
START_STEPS = 0
EXPS_FIRST = False
EXP_LAG = 2
LAST_BY_TENSOR = 0
LAST_EMPTY_ON_SCALAR = (-4, -3, -2, -1)
MASK_STEP = 11
BATCH = 2
S_AT_ONCE = False
COUNT_STEP = 6
PRODUCTS_FIRST = False
K_ON_SCALAR = (1,)
Q_ON_VECTOR = False
RESULT_ON_VECTOR = ()
GROUP0_ON_SCALAR = 0
C_ON_VECTOR = ((), (), (), ())
NORM_ON_VECTOR = ((), ())
MASK_BY_MATMUL = (5,)
MERGED = False
HEAD_MERGED = True
PROJECT_LAG = 7
FLIPS_FIRST = True
V_LOAD_EARLY = False
V_JOB_AT = (((0, 1), (0, 3)), ((1, 1), (1, 3)), ((2, 1), (2, 3)), ((3, 1), (3, 3)))
WO_JOB_AT = (((4, 1), (4, 3)), ((5, 1), (5, 3)), ((6, 1), (6, 3)), ((7, 1), (7, 3)))
LAST_ON_VECTOR = 3
P13_AT = (15, 16)
C14_AT = 3


def tile_scaleddotproductattention_pa_kernel(
    tc, q_masked, k_masked, v_proj, ind_k, ind_v, Wo, out
):
    nc = tc.nc
    with ExitStack() as stack:
        const = stack.enter_context(tc.tile_pool(name="const", bufs=1))
        keep = stack.enter_context(tc.tile_pool(name="keep", bufs=1))
        raw = stack.enter_context(tc.tile_pool(name="raw", bufs=4))
        work = stack.enter_context(tc.tile_pool(name="work", bufs=2))
        stats = stack.enter_context(tc.tile_pool(name="stats", bufs=8))
        psum = stack.enter_context(tc.psum_pool(name="psum", bufs=BANKS))
        stack.enter_context(tc.manual_schedule())

        groups = [(g, t) for g in range(FEATURE_PASSES) for t in range(Q_TILES)]
        END = GROUP * len(groups)
        LAST = len(groups) - 1

        def head_of(place):
            return groups[place // GROUP][0] * GROUP + place % GROUP

        k_t = keep.tile([P, HEADS, SEQ], BF16)
        stand_in = keep.tile([P, HEADS], BF16)
        v_codes = keep.tile([P, HEADS, KEY_PASSES * HEAD_DIM], U32, align_bytes=64)
        v_scales = keep.tile([P, HEADS, KEY_PASSES * HEAD_DIM], U8, align_bytes=64)
        wo_codes = keep.tile([P, FEATURE_PASSES, D_OUT], U32, align_bytes=64)
        wo_scales = keep.tile([P, FEATURE_PASSES, D_OUT], U8, align_bytes=64)
        c_codes = keep.tile([P, FEATURE_PASSES, SEQ], U32, align_bytes=64)
        c_scales = keep.tile([P, FEATURE_PASSES, SEQ], U8, align_bytes=64)

        q_raw_of = {}
        k_raw_of = {}
        v_raw_of = {}
        wo_raw_of = {}

        def load_q(group):
            g, t = groups[group]
            q_raw = raw.tile([P, GROUP, HEAD_DIM], BF16)
            rows = q_masked[0, g * GROUP : (g + 1) * GROUP, t * P : (t + 1) * P, :]
            nc.sync.dma_start(out=q_raw[:], in_=rows.rearrange("i p d -> p i d"))
            q_raw_of[group] = q_raw

        def load_k(h):
            k_raw = raw.tile([P, KEY_BLOCKS, HEAD_DIM], BF16)
            nc.sync.dma_start(out=k_raw[:], in_=k_masked[0, h].rearrange("(i p) d -> p i d", p=P))
            k_raw_of[h] = k_raw

        def load_v(h):
            v_raw = raw.tile([P, 2 * KEY_PASSES, 2 * HEAD_DIM], BF16)
            nc.sync.dma_start(out=v_raw[:], in_=v_proj[0, h].rearrange("(c p e) d -> p c (e d)", p=P, e=2))
            v_raw_of[h] = v_raw

        def load_wo(g):
            wo_raw = raw.tile([P, PACK, D_OUT], BF16, bufs=2)
            rows = Wo[g * K_PASS : (g + 1) * K_PASS, :]
            nc.sync.dma_start(out=wo_raw[:], in_=rows.rearrange("(i p) n -> p i n", p=P))
            wo_raw_of[g] = wo_raw

        ind_k_blocks = const.tile([P, P], BF16)
        nc.vector.memset(ind_k_blocks[:], 0.0)
        nc.sync.dma_start(out=ind_k_blocks[0:KEY_BLOCKS, :], in_=ind_k[0].rearrange("(b p) -> b p", p=P))
        load_k(0)
        load_q(0)
        load_k(1)
        load_v(0)
        load_k(2)
        load_v(1)
        load_k(3)
        ind_v_words = const.tile([P, 2 * KEY_PASSES, 2], BF16)
        nc.scalar.dma_start(out=ind_v_words[:], in_=ind_v[0].rearrange("(c p e) -> p c e", p=P, e=2))
        ind_k_words = const.tile([P, 2 * KEY_PASSES, 2], BF16)
        load_q(1)
        for h in range(2, GROUP):
            load_v(h)
        ind_k_rows = const.tile([P, SEQ], BF16)

        ones = const.tile([P, P], BF16)
        nc.vector.memset(ones[:], 1.0)
        table_loader = const.tile([P, 1], F32)
        nc.scalar.activation(out=table_loader[:], in_=ones[:, 0:1], func=ACT.Exp)
        ident_bf16 = const.tile([P, P], BF16)
        make_identity(nc, ident_bf16[:])
        neg_ident = const.tile([P, P], BF16)
        ident_f32 = const.tile([P, P], F32)
        make_identity(nc, ident_f32[:])

        neg_columns = const.tile([P, KEY_BLOCKS, P], F32)
        ind_k_columns = const.tile([P, KEY_BLOCKS], BF16)
        valid_keys = const.tile([P, 1], F32)
        any_valid = const.tile([P, 1], F32)
        value_mask = const.tile([P, 2 * KEY_PASSES, 2], BF16)
        inv_valid = const.tile([P, 1], F32)
        neg_masked = const.tile([P, 1], F32)

        flipped_ind = psum.tile([P, P], BF16, tag="bank")
        nc.tensor.transpose(flipped_ind[:], ind_k_blocks[:], ident_bf16[:])
        neg_column = const.tile([P, KEY_BLOCKS], F32)
        nc.vector.tensor_scalar(
            out=neg_column[:],
            in0=flipped_ind[:, 0:KEY_BLOCKS],
            scalar1=-1.0,
            scalar2=-MASKED_SCORE,
            op0=ALU.add,
            op1=ALU.mult,
        )
        half_blocks = KEY_BLOCKS // 2
        for half, copy in ((0, nc.vector.tensor_copy), (1, nc.scalar.copy)):
            blocks = slice(half * half_blocks, (half + 1) * half_blocks)
            copy(
                out=neg_columns[:, blocks, :],
                in_=neg_column[:, blocks].unsqueeze(2).to_broadcast([P, half_blocks, P]),
            )
        nc.scalar.copy(out=ind_k_columns[:], in_=flipped_ind[:, 0:KEY_BLOCKS])

        def count_valid_keys():
            counts = psum.tile([P, KEY_BLOCKS], F32, tag="bank")
            nc.tensor.matmul(counts[:], lhsT=ones[:], rhs=ind_k_columns[:], start=True, stop=True)
            scrap = stats.tile([P, KEY_BLOCKS], F32)
            nc.scalar.activation(out=scrap[:], in_=counts[:], func=ACT.Copy, accum_out=valid_keys[:])
            nc.gpsimd.tensor_scalar(
                out=any_valid[:], in0=valid_keys[:], scalar1=1.0, scalar2=0.0, op0=ALU.min, op1=ALU.max
            )
            nc.gpsimd.tensor_scalar(
                out=value_mask[:], in0=ind_v_words[:], scalar1=any_valid[:], scalar2=1.0, op0=ALU.mult, op1=ALU.mult
            )

        def take_count():
            nc.vector.tensor_scalar(out=inv_valid[:], in0=valid_keys[:], scalar1=1.0, scalar2=None, op0=ALU.max)
            nc.vector.tensor_scalar(
                out=neg_masked[:],
                in0=valid_keys[:],
                scalar1=-float(SEQ),
                scalar2=any_valid[:],
                op0=ALU.add,
                op1=ALU.mult,
            )
            nc.vector.reciprocal(out=inv_valid[:], in_=inv_valid[:])

        key_mask = const.tile([P, KEY_PASSES, P, PACK], BF16)
        masked_rows = const.tile([P, SEQ], BF16)

        def build_masked_rows():
            nc.vector.tensor_scalar(
                out=masked_rows[:], in0=ind_k_rows[:], scalar1=-1.0, scalar2=1.0, op0=ALU.mult, op1=ALU.add
            )

        def build_key_mask():
            nc.vector.tensor_copy(
                out=key_mask[:],
                in_=ind_k_words[:]
                .rearrange("p (g u) e -> p g (u e)", u=2)
                .unsqueeze(2)
                .to_broadcast([P, KEY_PASSES, P, PACK]),
            )

        in_psum = {}

        q_t_of = {}
        mean_of = {}
        stand_in_rows_of = {}
        stand_in_scores_of = {}

        Q_WORDS = GROUP * P // 2

        def with_stand_in(group):
            return [i for i in range(GROUP) if head_of(group * GROUP + i) in WITH_STAND_IN]

        def small_products(next_group, heads, group):
            bank = psum.tile([P, BANK], F32, tag="bank")
            if next_group is not None:
                q_view = bank[:, 0:Q_WORDS].bitcast(BF16).rearrange("p (i q) -> p i q", i=GROUP)
                for i in range(GROUP):
                    nc.tensor.transpose(q_view[:, i, :], q_raw_of[next_group][:, i, :], ident_bf16[:])
            for j, h in enumerate(heads):
                for i in range(KEY_BLOCKS):
                    nc.tensor.matmul(
                        bank[:, Q_WORDS + j : Q_WORDS + j + 1],
                        lhsT=k_raw_of[h][:, i, :],
                        rhs=ones[:, 0:1],
                        start=(i == 0),
                        stop=(i == KEY_BLOCKS - 1),
                    )
            if group is not None:
                for j, i in enumerate(with_stand_in(group)):
                    h = head_of(group * GROUP + i)
                    nc.tensor.matmul(
                        bank[:, Q_WORDS + GROUP + j : Q_WORDS + GROUP + j + 1],
                        lhsT=q_t_of[group][:, i, :],
                        rhs=stand_in[:, h : h + 1],
                        start=True,
                        stop=True,
                    )
            in_psum["small", next_group, tuple(heads), group] = bank

        def take_queries(next_group, bank):
            q_t = work.tile([P, GROUP, P], BF16, bufs=3)
            copy = nc.vector.tensor_copy if Q_ON_VECTOR and next_group > 1 else nc.scalar.copy
            copy(
                out=q_t[:],
                in_=bank[:, 0:Q_WORDS].bitcast(BF16).rearrange("p (i q) -> p i q", i=GROUP),
            )
            q_t_of[next_group] = q_t

        def take_small_products(next_group, heads, group):
            bank = in_psum["small", next_group, tuple(heads), group]
            if group is not None and with_stand_in(group):
                count = len(with_stand_in(group))
                stand_in_scores = stats.tile([P, count], F32)
                nc.scalar.copy(out=stand_in_scores[:], in_=bank[:, Q_WORDS + GROUP : Q_WORDS + GROUP + count])
                stand_in_scores_of[group] = stand_in_scores
            if heads:
                mean = stats.tile([P, len(heads)], F32)
                nc.scalar.activation(
                    out=mean[:], in_=bank[:, Q_WORDS : Q_WORDS + len(heads)], func=ACT.Copy, scale=inv_valid[:]
                )
                for j, h in enumerate(heads):
                    mean_of[h] = mean[:, j : j + 1]
            if next_group is not None and not (Q_ON_VECTOR and next_group > 1):
                take_queries(next_group, bank)
            for j, h in enumerate(heads):
                nc.scalar.copy(out=stand_in[:, h : h + 1], in_=mean[:, j : j + 1])

        def make_rows(h):
            stand_in_rows = work.tile([P, SEQ], BF16)
            nc.vector.tensor_scalar(
                out=stand_in_rows[:], in0=masked_rows[:], scalar1=mean_of[h], scalar2=None, op0=ALU.mult
            )
            stand_in_rows_of[h] = stand_in_rows

        def transpose_k(h, half):
            flipped_k = psum.tile([P, GROUP, P], BF16, tag="bank")
            for i in range(GROUP):
                nc.tensor.transpose(flipped_k[:, i, :], k_raw_of[h][:, half * GROUP + i, :], ident_bf16[:])
            in_psum[("k", h, half)] = flipped_k

        def k_on_scalar(h, half):
            return h not in WITH_STAND_IN and half in K_ON_SCALAR

        def take_k(h, half):
            keys = slice(half * BANK, (half + 1) * BANK)
            if h in WITH_STAND_IN:
                nc.vector.tensor_tensor(
                    out=k_t[:, h, keys],
                    in0=in_psum[("k", h, half)][:].rearrange("p i s -> p (i s)"),
                    in1=stand_in_rows_of[h][:, keys],
                    op=ALU.add,
                )
                return
            copy = nc.scalar.copy if half in K_ON_SCALAR else nc.vector.tensor_copy
            copy(out=k_t[:, h, keys], in_=in_psum[("k", h, half)][:].rearrange("p i s -> p (i s)"))

        v_grouped_of = {}

        def mask_and_group_v(h, part, engine=nc.gpsimd):
            if part[0] == 0:
                v_grouped = work.tile([P, KEY_PASSES * HEAD_DIM * PACK], BF16, align_bytes=64, bufs=5)
                v_grouped_of[h] = v_grouped
            if len(part) == 2 and (MERGED if h >= GROUP else HEAD_MERGED):
                engine.tensor_tensor(
                    out=v_grouped_of[h][:].rearrange("p (g d w) -> p g d w", g=KEY_PASSES, w=PACK),
                    in0=v_raw_of[h][:].rearrange("p (g u) (e d) -> p g d (u e)", u=2, e=2),
                    in1=value_mask[:]
                    .rearrange("p (g u) e -> p g (u e)", u=2)
                    .unsqueeze(2)
                    .to_broadcast([P, KEY_PASSES, HEAD_DIM, PACK]),
                    op=ALU.mult,
                )
                return
            for g in part:
                engine.tensor_tensor(
                    out=v_grouped_of[h][:].rearrange("p (g d w) -> p g d w", g=KEY_PASSES, w=PACK)[:, g, :, :],
                    in0=v_raw_of[h][:].rearrange("p (g u) (e d) -> p g d (u e)", u=2, e=2)[:, g, :, :],
                    in1=value_mask[:]
                    .rearrange("p (g u) e -> p g (u e)", u=2)[:, g, :]
                    .unsqueeze(1)
                    .to_broadcast([P, HEAD_DIM, PACK]),
                    op=ALU.mult,
                )

        def quantise_v(h):
            nc.vector.quantize_mx(
                out=v_codes[:, h, :].bitcast(FP8X4), scales=v_scales[:, h, :], in_=v_grouped_of[h][:]
            )

        WO_PIECES = 2 * FEATURE_PASSES
        wo_grouped_of = {}

        def group_wo(piece, part):
            g, half = divmod(piece, 2)
            if part[0] == 0:
                wo_grouped = work.tile([P, BANK * PACK], BF16, align_bytes=64)
                wo_grouped_of[piece] = wo_grouped
            WIDTH = BANK // (2 if len(part) == 1 else 1)
            for b in part if len(part) == 1 else (0,):
                cols = slice(half * BANK + b * WIDTH, half * BANK + (b + 1) * WIDTH)
                nc.gpsimd.tensor_scalar(
                    out=wo_grouped_of[piece][:, b * WIDTH * PACK : (b + 1) * WIDTH * PACK].rearrange(
                        "p (n i) -> p n i", i=PACK
                    ),
                    in0=wo_raw_of[g][:, :, cols].rearrange("p i n -> p n i"),
                    scalar1=1.0,
                    scalar2=0.0,
                    op0=ALU.mult,
                    op1=ALU.add,
                )

        def quantise_wo(piece):
            g, half = divmod(piece, 2)
            cols = slice(half * BANK, (half + 1) * BANK)
            nc.vector.quantize_mx(
                out=wo_codes[:, g, cols].bitcast(FP8X4), scales=wo_scales[:, g, cols], in_=wo_grouped_of[piece][:]
            )

        scores_of = {}
        maxima_of = {}
        neg_max_of = {}
        weights_of = {}
        row_sum_of = {}
        inv_sum_of = {}
        a_bf16_of = {}
        flipped_of = {}
        a_grouped_of = {}
        a_mx_of = {}
        o_t_of = {}
        c_grouped_of = {}
        pair_sums_of = {}

        def masked_in_psum(place):
            return head_of(place) not in WITH_STAND_IN or place >= END - LAST_BY_TENSOR

        def emptied_by_scalar(place):
            if place >= END - LAST_BY_TENSOR:
                return place - END in LAST_EMPTY_ON_SCALAR
            return masked_in_psum(place) and place % (2 * GROUP) in EMPTY_ON_SCALAR[groups[place // GROUP][0]]

        def scores(place):
            h = head_of(place)
            group, i = divmod(place, GROUP)
            halves = []
            for half in range(KEY_HALVES):
                score = psum.tile([P, BANK], F32, tag="bank")
                nc.tensor.matmul(
                    score[:],
                    lhsT=q_t_of[group][:, i, :],
                    rhs=k_t[:, h, half * BANK : (half + 1) * BANK],
                    start=True,
                    stop=not masked_in_psum(place),
                )
                halves.append(score)
                if masked_in_psum(place) and h in MASK_BY_MATMUL:
                    nc.tensor.matmul(
                        score[:],
                        lhsT=neg_ident[:],
                        rhs=masked_rows[:, half * BANK : (half + 1) * BANK],
                        start=False,
                        stop=True,
                    )
            scores_of[place] = halves

        def add_masks(place):
            if masked_in_psum(place) and head_of(place) not in MASK_BY_MATMUL:
                for half in range(KEY_HALVES):
                    for b in range(GROUP):
                        nc.tensor.matmul(
                            scores_of[place][half][:, b * P : (b + 1) * P],
                            lhsT=neg_columns[:, half * GROUP + b, :],
                            rhs=ident_f32[:],
                            start=False,
                            stop=(b == GROUP - 1),
                            is_transpose=True,
                        )

        def row_maximum(place):
            maxima = stats.tile([P, KEY_HALVES], F32)
            for half in range(KEY_HALVES):
                nc.vector.tensor_reduce(
                    out=maxima[:, half : half + 1],
                    in_=scores_of[place][half][:],
                    axis=mybir.AxisListType.X,
                    op=ALU.max,
                    negate=True,
                )
            maxima_of[place] = maxima

        def join_maxima(place):
            maxima = maxima_of[place]
            neg_max = stats.tile([P, 1], F32)
            nc.vector.tensor_scalar(
                out=neg_max[:], in0=maxima[:, 0:1], scalar1=maxima[:, 1:2], scalar2=SCALE, op0=ALU.min, op1=ALU.mult
            )
            neg_max_of[place] = neg_max

        def exponentials(place):
            group, i = divmod(place, GROUP)
            j = place % GROUP
            if j == 0:
                pair_sums = stats.tile([P, GROUP, KEY_HALVES], F32)
                pair_sums_of[group] = pair_sums
            pair_sums = pair_sums_of[group]
            first = pair_sums[:, j, 0:1]
            if not masked_in_psum(place):
                first_raw = stats.tile([P, 1], F32)
                first = first_raw[:]
                stand_in_exp = stats.tile([P, 1], F32)
                n = with_stand_in(group).index(i)
                nc.scalar.activation(
                    out=stand_in_exp[:],
                    in_=stand_in_scores_of[group][:, n : n + 1],
                    func=ACT.Exp,
                    bias=neg_max_of[place][:],
                    scale=SCALE,
                )
            weights = work.tile([P, SEQ], F32, bufs=10)
            for half in range(KEY_HALVES):
                nc.scalar.activation(
                    out=weights[:, half * BANK : (half + 1) * BANK],
                    in_=scores_of[place][half][:],
                    func=ACT.Exp,
                    bias=neg_max_of[place][:],
                    scale=SCALE,
                    accum_out=first if half == 0 else pair_sums[:, j, 1:2],
                )
            weights_of[place] = weights
            if not masked_in_psum(place):
                nc.scalar.activation(
                    out=pair_sums[:, j, 0:1], in_=stand_in_exp[:], func=ACT.Identity, scale=neg_masked[:], bias=first
                )

        def join_sums(group, first, last):
            row_sums = stats.tile([P, last - first], F32)
            nc.vector.tensor_reduce(
                out=row_sums[:], in_=pair_sums_of[group][:, first:last, :], axis=mybir.AxisListType.X, op=ALU.add
            )
            row_sum_of[group, first] = row_sums

        def invert_sums(group, first, last):
            inv_sums = stats.tile([P, last - first], F32)
            nc.vector.reciprocal(out=inv_sums[:], in_=row_sum_of[group, first][:])
            for j in range(first, last):
                inv_sum_of[group * GROUP + j] = inv_sums[:, j - first : j - first + 1]

        def normaliser(place):
            if place - END in LAST_ON_SCALAR:
                return "scalar"
            if place < GROUP0_ON_SCALAR:
                return "scalar"
            if place >= END - LAST_ON_VECTOR:
                return "vector"
            if place % GROUP in NORM_ON_VECTOR[groups[place // GROUP][0]]:
                return "vector"
            return "scalar" if place % (2 * GROUP) in NORM_ON_SCALAR[groups[place // GROUP][0]] else "gpsimd"

        def normalise(place):
            a_bf16 = work.tile([P, SEQ], BF16, bufs=6)
            weights = weights_of[place]
            inv_sum = inv_sum_of[place]
            if normaliser(place) == "gpsimd":
                nc.gpsimd.tensor_scalar(
                    out=a_bf16[:], in0=weights[:], scalar1=inv_sum, scalar2=1.0, op0=ALU.mult, op1=ALU.mult
                )
            elif normaliser(place) == "scalar":
                nc.scalar.activation(out=a_bf16[:], in_=weights[:], func=ACT.Copy, scale=inv_sum)
            else:
                nc.vector.tensor_scalar(out=a_bf16[:], in0=weights[:], scalar1=inv_sum, scalar2=None, op0=ALU.mult)
            a_bf16_of[place] = a_bf16

        def keys_to_partitions(place):
            a_words = a_bf16_of[place][:].bitcast(F32)
            flipped = psum.tile([P, 2, KEY_PASSES * P], F32, tag="bank")
            for g in range(KEY_PASSES):
                for u in range(2):
                    c = 2 * g + u
                    nc.tensor.transpose(
                        flipped[:, u, g * P : (g + 1) * P], a_words[:, c * P : (c + 1) * P], ident_f32[:]
                    )
            flipped_of[place] = flipped

        def empty(place):
            group, i = divmod(place, GROUP)
            if i == 0:
                a_grouped = work.tile([P, GROUP, KEY_PASSES * P * PACK], BF16, align_bytes=64, bufs=3)
                a_grouped_of[group] = a_grouped
            if masked_in_psum(place):
                copy = nc.scalar.copy if emptied_by_scalar(place) else nc.vector.tensor_copy
                copy(
                    out=a_grouped_of[group][:, i, :].bitcast(F32).rearrange("p (x u) -> p x u", u=2),
                    in_=flipped_of[place][:].rearrange("p u x -> p x u"),
                )
                return
            nc.vector.tensor_tensor(
                out=a_grouped_of[group][:, i, :].rearrange("p (x u e) -> p x u e", u=2, e=2),
                in0=flipped_of[place][:].bitcast(BF16).rearrange("p u (x e) -> p x u e", e=2),
                in1=key_mask[:].rearrange("p g q (u e) -> p (g q) u e", u=2),
                op=ALU.mult,
            )

        def quantise_weights(group, first, last):
            if first == 0:
                a_codes = work.tile([P, GROUP, KEY_PASSES * P], U32, align_bytes=64)
                a_scales = work.tile([P, GROUP, KEY_PASSES * P], U8, align_bytes=64)
                a_mx_of[group] = (a_codes, a_scales)
            a_codes, a_scales = a_mx_of[group]
            nc.vector.quantize_mx(
                out=a_codes[:, first:last, :].rearrange("p i w -> p (i w)").bitcast(FP8X4),
                scales=a_scales[:, first:last, :].rearrange("p i w -> p (i w)"),
                in_=a_grouped_of[group][:, first:last, :].rearrange("p i w -> p (i w)"),
            )

        def weighted_values(group, first, last):
            if first == 0:
                o_t = psum.tile([P, GROUP, P], F32, tag="bank", name="o_t")
                o_t_of[group] = o_t
            a_codes, a_scales = a_mx_of[group]
            for i in range(first, last):
                h = head_of(group * GROUP + i)
                for g in range(KEY_PASSES):
                    block = slice(g * P, (g + 1) * P)
                    nc.tensor.matmul_mx(
                        out=o_t_of[group][:, i, :],
                        lhsT=v_codes[:, h, block].bitcast(FP8X4),
                        lhsT_scale=v_scales[:, h, block],
                        rhs=a_codes[:, i, block].bitcast(FP8X4),
                        rhs_scale=a_scales[:, i, block],
                        start=(g == 0),
                        stop=(g == KEY_PASSES - 1),
                    )

        def take_values(group):
            c_grouped = work.tile([P, P * PACK], BF16, align_bytes=64)
            parts = 1 if group != LAST else 2
            width = P // parts
            for part in range(parts):
                some = slice(part * width, (part + 1) * width)
                there = c_grouped[:].rearrange("p (q i) -> p q i", i=PACK)[:, some, :]
                here = o_t_of[group][:].rearrange("p i q -> p q i")[:, some, :]
                if part == 0:
                    nc.scalar.copy(out=there, in_=here)
                else:
                    nc.vector.tensor_copy(out=there, in_=here)
            c_grouped_of[group] = c_grouped

        def quantise_heads(group):
            g, t = groups[group]
            queries = slice(t * P, (t + 1) * P)
            nc.vector.quantize_mx(
                out=c_codes[:, g, queries].bitcast(FP8X4), scales=c_scales[:, g, queries], in_=c_grouped_of[group][:]
            )

        def project(t, half):
            queries = slice(t * P, (t + 1) * P)
            cols = slice(half * BANK, (half + 1) * BANK)
            acc = psum.tile([P, BANK], F32, tag="bank")
            for g in range(FEATURE_PASSES):
                nc.tensor.matmul_mx(
                    out=acc[:],
                    lhsT=c_codes[:, g, queries].bitcast(FP8X4),
                    lhsT_scale=c_scales[:, g, queries],
                    rhs=wo_codes[:, g, cols].bitcast(FP8X4),
                    rhs_scale=wo_scales[:, g, cols],
                    start=(g == 0),
                    stop=(g == FEATURE_PASSES - 1),
                )
            in_psum[("out", t, half)] = acc

        def take_result(t, half, on_vector):
            queries = slice(t * P, (t + 1) * P)
            result = work.tile([P, BANK], F32, bufs=8)
            parts = 2 if groups[LAST][1] == t else 1
            width = BANK // parts
            for part in range(parts):
                some = slice(part * width, (part + 1) * width)
                there = slice(half * BANK + part * width, half * BANK + (part + 1) * width)
                copy = nc.vector.tensor_copy if on_vector else nc.scalar.copy
                copy(out=result[:, some], in_=in_psum[("out", t, half)][:, some])
                nc.sync.dma_start(out=out[0, queries, there], in_=result[:, some])


        side_jobs = {}
        for n, h in enumerate(range(GROUP, HEADS)):
            for part in range(2):
                side_jobs.setdefault(V_JOB_AT[n][part][0], []).append(
                    (V_JOB_AT[n][part][1], mask_and_group_v, quantise_v, h, part)
                )
        for piece in range(WO_PIECES):
            for part in range(2):
                side_jobs.setdefault(WO_JOB_AT[piece][part][0], []).append(
                    (WO_JOB_AT[piece][part][1], group_wo, quantise_wo, piece, part)
                )
        to_quantise = []

        done = {"flip": 0, "empty": 0, "quant": 0, "values": 0, "heads": 0, "project": 0}

        def flip_to(place):
            while done["flip"] <= min(place, END - 1):
                keys_to_partitions(done["flip"])
                done["flip"] += 1

        taken_next = []
        for_scalar = []

        def entered(step, lag):
            return step - lag if 0 <= step - lag < END else None

        def closed_group(step, lag):
            place = entered(step, lag)
            return place // GROUP if place is not None and place % GROUP == GROUP - 1 else None

        def prepare_stand_in(h):
            if h in WITH_STAND_IN:
                small_products(None, [h], None)
                take_small_products(None, [h], None)
                make_rows(h)

        def prepare_k(h):
            prepare_stand_in(h)
            for half in range(KEY_HALVES):
                transpose_k(h, half)
            for half in range(KEY_HALVES):
                take_k(h, half)

        EARLY = [h for h in WITH_STAND_IN if h < GROUP]
        ROWS_EARLY = EARLY or [h for h in MASK_BY_MATMUL if h < GROUP]
        if MASK_BY_MATMUL:
            nc.gpsimd.tensor_scalar(
                out=neg_ident[:], in0=ident_bf16[:], scalar1=MASKED_SCORE, scalar2=1.0, op0=ALU.mult, op1=ALU.mult
            )
        for half in range(KEY_HALVES):
            transpose_k(0, half)
        small_products(0, [], None)
        for half in range(KEY_HALVES):
            take_k(0, half)
        take_small_products(0, [], None)
        if ROWS_EARLY:
            build_masked_rows()
        count_valid_keys()
        prepare_k(1)
        for h in range(V_FIRST):
            mask_and_group_v(h, (0, 1), nc.vector)
        for h in range(V_FIRST, V_HEAD_G):
            mask_and_group_v(h, (0, 1))

        def step_of(step):
            take_now = list(taken_next)
            taken_next.clear()
            group, i = divmod(step, GROUP)
            following = group + 1 if group < LAST else None

            def tensor_products():
                ready = closed_group(step, QUANT_LAG + 2)
                if ready is not None:
                    weighted_values(ready, 0, GROUP)
                    done["values"] = ready + 1
                    taken_next.append((take_values, (ready,)))
                for half in range(2):
                    ready = closed_group(step, QUANT_LAG + PROJECT_LAG + half)
                    if ready is not None and groups[ready][0] == FEATURE_PASSES - 1:
                        t = groups[ready][1]
                        project(t, half)
                        if half == 1:
                            done["project"] = t + 1
                        taken_next.append((take_result, (t, half, half in RESULT_ON_VECTOR)))

            def tensor_side_jobs():
                if i == 0 and step > 0:
                    heads = [h for h in [GROUP + group - 1] if h in WITH_STAND_IN]
                    small_products(following, heads, group)
                    taken_next.append((take_small_products, (following, heads, group)))
                if step == COUNT_STEP and not EARLY:
                    taken_next.append((take_count, ()))
                if step == 3 and EARLY:
                    small_products(None, [], 0)
                    taken_next.append((take_small_products, (None, [], 0)))
                h = step + 2
                if h < GROUP:
                    if h in WITH_STAND_IN:
                        small_products(None, [h], None)
                        taken_next.append((take_small_products, (None, [h], None)))
                        taken_next.append((make_rows, (h,)))
                    for half in range(KEY_HALVES):
                        transpose_k(h, half)
                        taken_next.append((take_k, (h, half)))
                h = GROUP + group - 1
                if i in (2, 3) and GROUP <= h < HEADS:
                    if i == 2 and h in WITH_STAND_IN:
                        make_rows(h)
                    transpose_k(h, i - 2)
                    taken_next.append((take_k, (h, i - 2)))

            if FLIPS_FIRST:
                flip_to(step - FLIP_LAG)
            scores(step)
            if PRODUCTS_FIRST:
                tensor_products()
            add_masks(step)
            if step == 1:
                small_products(1, [], None)
                taken_next.append((take_small_products, (1, [], None)))
            if not FLIPS_FIRST:
                flip_to(step - FLIP_LAG)
            if not PRODUCTS_FIRST:
                tensor_products()
            tensor_side_jobs()

            def do_R():
                if entered(step, 1) is not None:
                    row_maximum(step - 1)

            def do_K():
                if EARLY and step == 0:
                    take_count()
                for take, args in take_now:
                    if take in (take_count, make_rows) or take is take_k and not k_on_scalar(*args):
                        if take is make_rows:
                            for other, its in take_now:
                                if other is take_small_products and its[1] == [args[0]]:
                                    other(*its)
                        take(*args)
                h = V_HEAD_G + step - V_STEP
                if V_HEAD_G <= h < GROUP and step >= V_STEP:
                    mask_and_group_v(h, (0, 1), nc.vector)

            summed = entered(step, NORM_LAG)
            batch = PAIR if summed is None or summed >= END - GROUP else BATCH
            closes = summed is not None and summed % batch == batch - 1
            if closes:
                of_group, last = summed // GROUP, summed % GROUP + 1

            def do_T():
                if closes:
                    join_sums(of_group, last - batch, last)

            place_to_empty = entered(step, EMPTY_LAG)
            late_copy = place_to_empty is not None and emptied_by_scalar(place_to_empty)

            def do_E():
                for take, args in take_now:
                    if take is take_small_products and args[0] is not None and Q_ON_VECTOR and args[0] > 1:
                        take_queries(args[0], in_psum["small", args[0], tuple(args[1]), args[2]])
                    if take is take_result and args[2]:
                        take(*args)
                if place_to_empty is not None:
                    done["empty"] = place_to_empty + 1
                    if not late_copy:
                        empty(place_to_empty)

            def do_J():
                if entered(step, 1) is not None:
                    join_maxima(step - 1)

            inverted = []

            def do_N():
                if closes:
                    invert_sums(of_group, last - batch, last)
                    inverted.extend([of_group * GROUP + j for j in range(last - batch, last)])
                    for engine in ("vector", "gpsimd"):
                        for place in inverted:
                            if normaliser(place) == engine:
                                normalise(place)

            def do_Q():
                if step == V_QUANT_STEP:
                    for h in range(GROUP):
                        quantise_v(h)
                ready = closed_group(step, QUANT_LAG)
                if step == MASK_STEP and not ROWS_EARLY:
                    build_masked_rows()
                if step == MASK_STEP:
                    build_key_mask()
                if ready is None:
                    return
                earlier = closed_group(step, QUANT_LAG + 4)
                if earlier is not None:
                    quantise_heads(earlier)
                    done["heads"] = earlier + 1
                for issued, quantise, what in list(to_quantise):
                    if issued < step:
                        quantise(what)
                        to_quantise.remove((issued, quantise, what))
                quantise_weights(ready, 0, GROUP)
                done["quant"] = ready + 1

            jobs = {"R": do_R, "K": do_K, "E": do_E, "J": do_J, "N": do_N, "T": do_T, "Q": do_Q}
            for letter in V_ORDER_CLOSING if closed_group(step, QUANT_LAG) is not None or step == V_QUANT_STEP else V_ORDER:
                jobs[letter]()

            exps_first = EXPS_FIRST or step < START_STEPS
            if exps_first and entered(step, EXP_LAG) is not None:
                exponentials(step - EXP_LAG)
            for take, args in take_now:
                if take not in (take_k, take_count, make_rows) and not (take is take_result and args[2]):
                    if take is take_small_products and args[0] is None and args[1] and args[2] is None:
                        continue
                    take(*args)
            if not K_LATE:
                for take, args in take_now:
                    if take is take_k and k_on_scalar(*args):
                        take(*args)
            if not exps_first and entered(step, EXP_LAG) is not None:
                exponentials(step - EXP_LAG)
            if K_LATE:
                for take, args in take_now:
                    if take is take_k and k_on_scalar(*args):
                        take(*args)
            if late_copy:
                empty(place_to_empty)
            for_scalar.extend([place for place in inverted if normaliser(place) == "scalar"])
            if for_scalar and (S_AT_ONCE or for_scalar[0] not in inverted):
                normalise(for_scalar.pop(0))

            if step == LATE_LOAD_STEP:
                nc.sync.dma_start(out=ind_k_rows[:], in_=ind_k[0].partition_broadcast(P))
                nc.sync.dma_start(out=ind_k_words[:], in_=ind_k[0].rearrange("(c p e) -> p c e", p=P, e=2))
            if i == 0 and group + 2 < len(groups):
                load_q(group + 2)
            if i == 0 and GROUP <= GROUP + group < HEADS:
                load_k(GROUP + group)
            for n, h in enumerate(range(GROUP, HEADS)):
                if i == 1 and group == max(0, V_JOB_AT[n][0][0] - 1 if V_LOAD_EARLY else V_JOB_AT[n][0][0]):
                    load_v(h)
            for g in range(FEATURE_PASSES):
                if i == 0 and group == WO_JOB_AT[2 * g][0][0] - 1:
                    load_wo(g)
            for at, lay_out, quantise, what, part in side_jobs.get(group, []):
                if at == i:
                    if not MERGED:
                        lay_out(what, (part,))
                    elif part == 0:
                        lay_out(what, (0, 1))
                    if part == 1:
                        to_quantise.append((step, quantise, what))

        for step in range(END):
            step_of(step)

        def empty_to(place):
            while done["empty"] <= place:
                empty(done["empty"])
                done["empty"] += 1

        def quantise_to(group):
            while done["quant"] <= group:
                quantise_weights(done["quant"], 0, GROUP)
                done["quant"] += 1

        def values_to(group):
            started = list(range(done["values"], group + 1))
            for g in started:
                weighted_values(g, 0, GROUP)
            done["values"] = max(done["values"], group + 1)
            return started

        def heads_to(group):
            while done["heads"] <= group:
                quantise_heads(done["heads"])
                done["heads"] += 1

        def out_of_psum(t, on_vector):
            for half in range(2):
                take_result(t, half, on_vector[half])

        def project_both(t):
            for half in range(2):
                project(t, half)

        a, b, c, d = range(END - GROUP, END)
        order_of_t = [t for g, t in groups if g == FEATURE_PASSES - 1]
        early = order_of_t[done["project"] : -3]
        T5, T6, T7 = order_of_t[-3:]

        for take, args in taken_next:
            take(*args)
        for place in for_scalar:
            normalise(place)
        flip_to(a - 3)
        started = values_to(LAST - 2)
        if early:
            heads_to(LAST - 3)
        for t in early:
            project_both(t)
        flip_to(a - 1)
        row_maximum(d)
        exponentials(c)
        join_maxima(d)
        exponentials(d)
        join_sums(LAST, 0, PAIR)
        invert_sums(LAST, 0, PAIR)
        normalise(a)
        normalise(b)
        for t in early:
            take_result(t, 0, True)
        empty_to(a - 2)
        for t in early:
            take_result(t, 1, True)
        empty_to(a - 1)
        flip_to(b)
        join_sums(LAST, PAIR, GROUP)
        invert_sums(LAST, PAIR, GROUP)
        normalise(c)
        normalise(d)
        for g in started:
            take_values(g)
        flip_to(d)
        heads_to(LAST - 2)
        quantise_to(LAST - 1)
        started = values_to(LAST - 1)
        empty_to(b)
        quantise_weights(LAST, 0, 2)
        project_both(T5)
        for g in started:
            take_values(g)
        empty_to(d)
        heads_to(LAST - 1)
        weighted_values(LAST, 0, 2)
        quantise_weights(LAST, 2, 4)
        out_of_psum(T5, (False, False))
        project(T6, 0)
        weighted_values(LAST, 2, 4)
        project(T6, 1)
        take_result(T6, 0, False)
        take_values(LAST)
        quantise_heads(LAST)
        take_result(T6, 1, True)
        project_both(T7)
        out_of_psum(T7, (False, True))
